import numpy as np
import ml_dtypes


def mxq(x, axis, fmt="e4m3"):
    dtype, down = {"e4m3": (ml_dtypes.float8_e4m3fn, 7), "e5m2": (ml_dtypes.float8_e5m2, 14)}[fmt]
    v = np.moveaxis(np.asarray(x, np.float32).astype(ml_dtypes.bfloat16).astype(np.float64), axis, -1)
    blocks = v.reshape(v.shape[:-1] + (-1, 32))
    amax = np.abs(blocks).max(-1, keepdims=True)
    byte = np.maximum(np.where(amax > 0, np.frexp(amax)[1] - 1 + 127, 0) - down, 1)
    scale = np.exp2(byte - 127.0)
    codes = (blocks / scale).astype(np.float32).astype(dtype).astype(np.float64)
    return np.moveaxis((codes * scale).reshape(v.shape), -1, axis)


WIDE = False


def mx_kscale(k):
    if not WIDE:
        return np.ones(k)
    levels = np.array([10, -10, 5, -5, 0])
    if k % 512:
        return np.exp2(np.random.permutation(np.resize(levels, k // 32))).repeat(32)
    a = np.empty((k // 512, 16))
    for p in range(k // 512):
        a[p, :8] = np.random.permutation(np.resize(levels, 8))
        for g in range(8):
            far = levels[np.abs(levels - a[p, g]) >= 10]
            a[p, g + 8] = far[np.random.randint(len(far))]
    return np.exp2(a.ravel()).repeat(32)


BF16 = ml_dtypes.bfloat16


def bf(x):
    return np.asarray(x, np.float32).astype(BF16)


def f64(x):
    return np.asarray(x).astype(np.float64)


T, H, NQ, NKV, HD = 512, 2048, 32, 2, 128
RD = HD // 2
QS, KS = NQ * HD, NKV * HD
OUT = QS + 2 * KS


def extract_rope(x):
    r = x[..., :RD]
    r = r.reshape(*r.shape[:-1], RD // 2, 2)
    return np.swapaxes(r, -2, -1).reshape(*x.shape[:-1], RD)


def fill_rope(x, rope):
    r = rope.reshape(*rope.shape[:-1], 2, RD // 2)
    r = np.swapaxes(r, -2, -1).reshape(*rope.shape)
    return np.concatenate([r, x[..., RD:]], axis=-1)


def rotate_half(x):
    half = x.shape[-1] // 2
    return np.concatenate([-x[..., half:], x[..., :half]], axis=-1)


def draw0():
    s = mx_kscale(H)
    ang = np.random.uniform(0.0, 2.0 * np.pi, (T, RD))
    return {'hidden_states': bf(np.random.standard_normal((T, H)) * s),
            'cos': bf(np.cos(ang)), 'sin': bf(np.sin(ang)),
            'W_qkv': bf(np.random.standard_normal((H, OUT)) / np.sqrt(H) / s[:, None]),
            'b_qkv': bf(np.random.standard_normal(OUT) * 0.3)}


def core(hidden_states, cos, sin, W_qkv, b_qkv):
    qkv = (mxq(f64(hidden_states), 1, 'e4m3') @ mxq(f64(W_qkv), 0, 'e4m3')) + f64(b_qkv)
    q = qkv[:, :QS].reshape(T, NQ, HD)
    k = qkv[:, QS:QS + KS].reshape(T, NKV, HD)
    v = qkv[:, QS + KS:].reshape(T, NKV, HD)
    cos_b = f64(cos)[:, None, :]
    sin_b = f64(sin)[:, None, :]
    q_r = extract_rope(q)
    k_r = extract_rope(k)
    q_r = q_r * cos_b + rotate_half(q_r) * sin_b
    k_r = k_r * cos_b + rotate_half(k_r) * sin_b
    q = fill_rope(q, q_r)
    k = fill_rope(k, k_r)
    return q, k, v


def e4m3fn_bytes(y):
    return np.clip(np.asarray(y, np.float64), -448.0, 448.0).astype(np.float32).astype(ml_dtypes.float8_e4m3fn).view(np.uint8)


def e4m3fn_values(b):
    return np.asarray(b, np.uint8).view(ml_dtypes.float8_e4m3fn).astype(np.float64)


def setup_inputs():
    d = draw0()
    x0 = np.asarray(d['W_qkv']).astype(np.float64)
    s = (np.max(np.abs(x0), axis=(1,), keepdims=True) / 448.0).astype(np.float32)
    out = {}
    for k, v in d.items():
        if k == 'W_qkv':
            out['W_qkv_bytes'] = e4m3fn_bytes(x0 / s.astype(np.float64))
            out['W_qkv_scale'] = s
        else:
            out[k] = v
    return out


def reference(hidden_states, cos, sin, W_qkv_bytes, W_qkv_scale, b_qkv):
    return core(hidden_states, cos, sin, e4m3fn_values(W_qkv_bytes) * W_qkv_scale.astype(np.float64), b_qkv)

@@ -1,0 +1,327 @@
+from contextlib import ExitStack
+
+import concourse.mybir as mybir
+from concourse.masks import make_identity
+
+T, H, OUT = 512, 2048, 4608
+FLOPS = 2 * T * H * OUT
+
+F32 = mybir.dt.float32
+BF16 = mybir.dt.bfloat16
+U32 = mybir.dt.uint32
+U8 = mybir.dt.uint8
+FP8 = mybir.dt.float8_e4m3fn
+FP8X4 = mybir.dt.float8_e4m3fn_x4
+ADD = mybir.AluOpType.add
+MULT = mybir.AluOpType.mult
+COPY = mybir.ActivationFunctionType.Copy
+
+P = 128
+PACK = 4
+KP = P * PACK
+G = H // KP
+TT = T // P
+NT = 512
+RD = 64
+HD = 128
+QCOLS = 4096
+KCOLS = 256
+
+TILES = [
+    (0, 512, 0, 0),
+    (512, 512, 128, 0),
+    (1024, 512, 128, 0),
+    (1536, 512, 256, 0),
+    (2048, 512, 256, 0),
+    (2560, 512, 256, 0),
+    (3072, 512, 256, 0),
+    (3584, 512, 256, 0),
+    (4096, 256, 128, 0),
+    (4352, 256, 128, 0),
+]
+LOAD_COLS = 512
+LOADS_AHEAD = 12
+SPLIT = 3
+
+
+def tile_selfattention_pa_kernel(
+    tc, hidden_states, cos, sin, W_qkv_bytes, W_qkv_scale, b_qkv, out_0, out_1, out_2
+):
+    nc = tc.nc
+    with ExitStack() as ctx:
+        const = ctx.enter_context(tc.tile_pool(name="const", bufs=1))
+        wbp = ctx.enter_context(tc.tile_pool(name="wbp", bufs=16))
+        plp = ctx.enter_context(tc.tile_pool(name="plp", bufs=3))
+        grp = ctx.enter_context(tc.tile_pool(name="grp", bufs=3))
+        cdp = ctx.enter_context(tc.tile_pool(name="cdp", bufs=3))
+        hid = ctx.enter_context(tc.tile_pool(name="hid", bufs=2))
+        obp = ctx.enter_context(tc.tile_pool(name="obp", bufs=4))
+        tmp = ctx.enter_context(tc.tile_pool(name="tmp", bufs=2))
+        accp = ctx.enter_context(tc.psum_pool(name="accp", bufs=6))
+        ilp = ctx.enter_context(tc.psum_pool(name="ilp", bufs=2))
+        ctx.enter_context(tc.manual_schedule())
+
+        units = [(n, gp) for n in range(len(TILES)) for gp in range(2)]
+        n_units = len(units)
+        w_tiles = {}
+        st = {}
+        codes = {}
+
+        loads = [(c0, g) for c0 in range(0, OUT, LOAD_COLS) for g in range(G)]
+
+        def load(j):
+            c0, g = loads[j]
+            wc = min(LOAD_COLS, OUT - c0)
+            w_bytes = wbp.tile([P, PACK, LOAD_COLS], U8, name="w_bytes")
+            nc.sync.dma_start(
+                out=w_bytes[:, :, 0:wc],
+                in_=W_qkv_bytes[g * KP : (g + 1) * KP, c0 : c0 + wc].rearrange("(p t) n -> p t n", t=PACK),
+            )
+            w_tiles[(c0, g)] = w_bytes
+
+        def widen(i, lo, hi):
+            n, gp = units[i]
+            c0, w = TILES[n][0], TILES[n][1]
+            if lo == 0:
+                planes = plp.tile([P, 2, PACK, w], BF16, name="planes")
+                grouped = grp.tile([P, 2, w * PACK], BF16, name="grouped", align_bytes=64)
+                st[i] = [planes, grouped, []]
+            planes = st[i][0]
+            base = (c0 // LOAD_COLS) * LOAD_COLS
+            for q in range(lo, hi):
+                gl, t = q // PACK, q % PACK
+                g = 2 * gp + gl
+                nc.scalar.activation(
+                    out=planes[:, gl, t, :],
+                    in_=w_tiles[(base, g)][:, t, c0 - base : c0 - base + w].bitcast(FP8),
+                    func=COPY,
+                    scale=wscale[:, g, t : t + 1],
+                )
+
+        def pe_interleave(i):
+            n, gp = units[i]
+            a = TILES[n][2]
+            planes = st[i][0]
+            for b in range(a // P):
+                bank = ilp.tile([P, 2, NT], BF16, name="bank")
+                for gl in range(2):
+                    nc.tensor.matmul(
+                        out=bank[:, gl, :].rearrange("p (c t) -> p c t", t=PACK),
+                        lhsT=ident_b[:],
+                        rhs=planes[:, gl, :, b * P : (b + 1) * P].rearrange("p t c -> p c t"),
+                        start=True,
+                        stop=True,
+                    )
+                st[i][2].append(bank)
+
+        def scalar_interleave(i):
+            n, gp = units[i]
+            a, sil = TILES[n][2], TILES[n][3]
+            planes, grouped, banks = st[i]
+            for b in range(len(banks)):
+                nc.scalar.copy(out=grouped[:, :, b * NT : (b + 1) * NT], in_=banks[b][:])
+            if sil > 0:
+                nc.scalar.copy(
+                    out=grouped[:, :, a * PACK : (a + sil) * PACK].rearrange("p g (c t) -> p g c t", t=PACK),
+                    in_=planes[:, :, :, a : a + sil].rearrange("p g t c -> p g c t"),
+                )
+
+        def vector_interleave(i):
+            n, gp = units[i]
+            w, a, sil = TILES[n][1], TILES[n][2], TILES[n][3]
+            planes, grouped = st[i][0], st[i][1]
+            a = a + sil
+            if a < w:
+                nc.vector.tensor_copy(
+                    out=grouped[:, :, a * PACK : w * PACK].rearrange("p g (c t) -> p g c t", t=PACK),
+                    in_=planes[:, :, :, a:w].rearrange("p g t c -> p g c t"),
+                )
+
+        def quantise(i):
+            n, gp = units[i]
+            w = TILES[n][1]
+            if gp == 0:
+                wcod = cdp.tile([P, G, w], U32, name="wcod", align_bytes=64)
+                wsc = cdp.tile([P, G, w], U8, name="wsc", align_bytes=64)
+                codes[n] = (wcod, wsc)
+            wcod, wsc = codes[n]
+            nc.vector.quantize_mx(
+                out=wcod[:, 2 * gp : 2 * gp + 2, :].rearrange("p g c -> p (g c)").bitcast(FP8X4),
+                scales=wsc[:, 2 * gp : 2 * gp + 2, :].rearrange("p g c -> p (g c)"),
+                in_=st[i][1][:].rearrange("p g c -> p (g c)"),
+            )
+
+        def mx_pass(acc, n, tt, g):
+            wcod, wsc = codes[n]
+            w = TILES[n][1]
+            nc.tensor.matmul_mx(
+                out=acc[:, 0:w],
+                lhsT=xc[:, tt, g * P : (g + 1) * P].bitcast(FP8X4),
+                lhsT_scale=xs[:, tt, g * P : (g + 1) * P],
+                rhs=wcod[:, g, :].bitcast(FP8X4),
+                rhs_scale=wsc[:, g, :],
+                start=(g == 0),
+                stop=(g == G - 1),
+            )
+
+        def out_half(n, half, accs):
+            col, w = TILES[n][0], TILES[n][1]
+            xb = obp.tile([P, 2, w], F32, name="xb")
+            for k in range(2):
+                nc.vector.tensor_tensor(out=xb[:, k, :], in0=accs[k][:, 0:w], in1=bias_sb[:, col : col + w], op=ADD)
+            t0 = 2 * half
+            if col < QCOLS + KCOLS:
+                nh = w // HD
+                m12 = tmp.tile([P, 2, nh, 2, RD], F32, name="m12")
+                xr = xb[:].rearrange("p t (h d) -> p t h d", d=HD)[:, :, :, 0:RD]
+                nc.vector.tensor_tensor(
+                    out=m12[:],
+                    in0=xr.unsqueeze(3).to_broadcast([P, 2, nh, 2, RD]),
+                    in1=cs_tab[:, t0 : t0 + 2, :, :].unsqueeze(2).to_broadcast([P, 2, nh, 2, RD]),
+                    op=MULT,
+                )
+                nc.vector.tensor_tensor(
+                    out=xr.rearrange("p t h (j e) -> p t h j e", e=2),
+                    in0=m12[:, :, :, 0, :].rearrange("p t h (j e) -> p t h j e", e=2),
+                    in1=m12[:, :, :, 1, :].rearrange("p t h (j e) -> p t h j e", e=2)[:, :, :, :, ::-1],
+                    op=ADD,
+                )
+            if col < QCOLS:
+                dst = out_0.rearrange("(t p) h d -> p t (h d)", p=P)[:, t0 : t0 + 2, col : col + w]
+            elif col < QCOLS + KCOLS:
+                dst = out_1.rearrange("(t p) h d -> p t (h d)", p=P)[:, t0 : t0 + 2, :]
+            else:
+                dst = out_2.rearrange("(t p) h d -> p t (h d)", p=P)[:, t0 : t0 + 2, :]
+            nc.sync.dma_start(out=dst, in_=xb[:])
+
+        wscale = const.tile([P, G, PACK], F32, name="wscale")
+        nc.sync.dma_start(out=wscale[:], in_=W_qkv_scale.rearrange("(g p t) o -> p g (t o)", p=P, t=PACK))
+        x_sb = const.tile([P, TT, H], BF16, name="x_sb")
+        cos_sb = const.tile([P, TT, RD], BF16, name="cos_sb")
+        sin_sb = const.tile([P, TT, RD], BF16, name="sin_sb")
+        bias_sb = const.tile([P, OUT], BF16, name="bias_sb")
+        for half in range(2):
+            load(2 * half)
+            load(2 * half + 1)
+            for tt in (2 * half, 2 * half + 1):
+                nc.sync.dma_start(out=x_sb[:, tt, :], in_=hidden_states[tt * P : (tt + 1) * P, :])
+        nc.sync.dma_start(out=cos_sb[:], in_=cos.rearrange("(t p) d -> p t d", p=P))
+        nc.sync.dma_start(out=sin_sb[:], in_=sin.rearrange("(t p) d -> p t d", p=P))
+        for j in range(4, 8):
+            load(j)
+        nc.sync.dma_start(out=bias_sb[:], in_=b_qkv.partition_broadcast(P))
+        for j in range(8, LOADS_AHEAD):
+            load(j)
+        next_load = LOADS_AHEAD
+
+        warm = const.tile([P, 2], F32, name="warm")
+        nc.vector.memset(warm[:, 0:1], 0.0)
+        nc.scalar.activation(out=warm[:, 1:2], in_=warm[:, 0:1], func=COPY)
+
+        ident_f = const.tile([P, P], F32, name="ident_f")
+        make_identity(nc, ident_f[:])
+        ident_b = const.tile([P, P], BF16, name="ident_b")
+        make_identity(nc, ident_b[:])
+
+        xc = const.tile([P, TT, G * P], U32, name="xc", align_bytes=64)
+        xs = const.tile([P, TT, G * P], U8, name="xs", align_bytes=64)
+        cs_tab = const.tile([P, TT, 2, RD], F32, name="cs_tab")
+        xgs = {}
+
+        def hidden_transpose(tt):
+            words = x_sb[:, tt, :].bitcast(F32)
+            pts = []
+            for gh in range(2):
+                pt = accp.tile([P, NT], F32, name="acc")
+                for gl in range(2):
+                    g = 2 * gh + gl
+                    for u in range(2):
+                        q = 2 * gl + u
+                        nc.tensor.transpose(
+                            pt[:, q * P : (q + 1) * P], words[:, 256 * g + u : 256 * (g + 1) : 2], ident_f[:]
+                        )
+                pts.append(pt)
+            return pts
+
+        def hidden_copy(tt, pts):
+            xg = hid.tile([P, G, P, PACK], BF16, name="xg", align_bytes=64)
+            for gh in range(2):
+                nc.vector.tensor_copy(
+                    out=xg[:, 2 * gh : 2 * gh + 2, :, :].bitcast(F32),
+                    in_=pts[gh][:].rearrange("p (g u r) -> p g r u", g=2, u=2),
+                )
+            xgs[tt] = xg
+
+        def hidden_quantise(tt):
+            nc.vector.quantize_mx(
+                out=xc[:, tt, :].bitcast(FP8X4),
+                scales=xs[:, tt, :],
+                in_=xgs[tt][:].rearrange("p g r j -> p (g r j)"),
+            )
+
+        def rope_tables():
+            nc.vector.tensor_copy(
+                out=cs_tab[:, :, 0, :].rearrange("p t (j e) -> p t j e", e=2),
+                in_=cos_sb[:].rearrange("p t (e j) -> p t j e", e=2),
+            )
+            sv = cs_tab[:, :, 1, :].rearrange("p t (j e) -> p t j e", e=2)
+            sn = sin_sb[:].rearrange("p t (e j) -> p t j e", e=2)
+            nc.vector.tensor_scalar(out=sv[:, :, :, 1:2], in0=sn[:, :, :, 0:1], scalar1=-1.0, scalar2=None, op0=MULT)
+            nc.vector.tensor_copy(out=sv[:, :, :, 0:1], in_=sn[:, :, :, 1:2])
+
+        mm_queue = []
+        pending = []
+        last_n = len(TILES) - 1
+        last_accs = []
+        s = 0
+        while s < n_units + 1 or pending or mm_queue:
+            if s >= 1:
+                for r in range(2):
+                    if next_load < len(loads):
+                        load(next_load)
+                        next_load += 1
+            if s < n_units:
+                widen(s, 0, SPLIT)
+            if 0 <= s - 1 < n_units:
+                scalar_interleave(s - 1)
+            if s < n_units:
+                widen(s, SPLIT, 2 * PACK)
+                pe_interleave(s)
+            if 0 <= s - 1 < n_units:
+                vector_interleave(s - 1)
+            if s < 2:
+                for tt in (2 * s, 2 * s + 1):
+                    hidden_copy(tt, hidden_transpose(tt))
+                for tt in (2 * s, 2 * s + 1):
+                    hidden_quantise(tt)
+            if s == 2:
+                rope_tables()
+            if pending:
+                out_half(*pending.pop(0))
+            if 0 <= s - 1 < n_units:
+                i = s - 1
+                quantise(i)
+                n, gp = units[i]
+                if n == last_n:
+                    for tt in range(TT):
+                        if gp == 0:
+                            acc = accp.tile([P, NT], F32, name="acc")
+                            last_accs.append(acc)
+                        mx_pass(last_accs[tt], n, tt, 2 * gp)
+                        mx_pass(last_accs[tt], n, tt, 2 * gp + 1)
+                    if gp == 1:
+                        pending.append((n, 0, last_accs[0:2]))
+                        pending.append((n, 1, last_accs[2:4]))
+                elif gp == 1:
+                    mm_queue.append((n, 0))
+                    mm_queue.append((n, 1))
+            if mm_queue:
+                n, half = mm_queue.pop(0)
+                accs = []
+                for k in range(2):
+                    acc = accp.tile([P, NT], F32, name="acc")
+                    for g in range(G):
+                        mx_pass(acc, n, 2 * half + k, g)
+                    accs.append(acc)
+                pending.append((n, half, accs))
+            s += 1

@@ -28,20 +28,20 @@ QCOLS = 4096
 KCOLS = 256
 
 TILES = [
-    (0, 512, 0, 0),
-    (512, 512, 128, 0),
-    (1024, 512, 128, 0),
-    (1536, 512, 256, 0),
-    (2048, 512, 256, 0),
-    (2560, 512, 256, 0),
-    (3072, 512, 256, 0),
-    (3584, 512, 256, 0),
-    (4096, 256, 128, 0),
-    (4352, 256, 128, 0),
+    (0, 512, 2, 0, 3),
+    (512, 512, 3, 0, 0),
+    (1024, 512, 3, 0, 0),
+    (1536, 512, 4, 0, 0),
+    (2048, 512, 4, 0, 0),
+    (2560, 512, 4, 0, 0),
+    (3072, 512, 4, 0, 0),
+    (3584, 512, 4, 2, 0),
+    (4096, 256, 0, 2, 0),
+    (4352, 256, 0, 2, 0),
 ]
+HIDDEN_ON_SCALAR = False
 LOAD_COLS = 512
 LOADS_AHEAD = 12
-SPLIT = 3
 
 
 def tile_selfattention_pa_kernel(
@@ -84,58 +84,76 @@ def tile_selfattention_pa_kernel(
             c0, w = TILES[n][0], TILES[n][1]
             if lo == 0:
                 planes = plp.tile([P, 2, PACK, w], BF16, name="planes")
-                grouped = grp.tile([P, 2, w * PACK], BF16, name="grouped", align_bytes=64)
+                grouped = grp.tile([P, 2 * w * PACK], BF16, name="grouped", align_bytes=64)
                 st[i] = [planes, grouped, []]
             planes = st[i][0]
             base = (c0 // LOAD_COLS) * LOAD_COLS
+            vw = TILES[n][4]
             for q in range(lo, hi):
                 gl, t = q // PACK, q % PACK
                 g = 2 * gp + gl
-                nc.scalar.activation(
-                    out=planes[:, gl, t, :],
-                    in_=w_tiles[(base, g)][:, t, c0 - base : c0 - base + w].bitcast(FP8),
-                    func=COPY,
-                    scale=wscale[:, g, t : t + 1],
-                )
+                if q >= 2 * PACK - vw:
+                    nc.vector.tensor_scalar(
+                        out=planes[:, gl, t, :],
+                        in0=w_tiles[(base, g)][:, t, c0 - base : c0 - base + w].bitcast(FP8),
+                        scalar1=wscale[:, g, t : t + 1],
+                        scalar2=None,
+                        op0=MULT,
+                    )
+                else:
+                    nc.scalar.activation(
+                        out=planes[:, gl, t, :],
+                        in_=w_tiles[(base, g)][:, t, c0 - base : c0 - base + w].bitcast(FP8),
+                        func=COPY,
+                        scale=wscale[:, g, t : t + 1],
+                    )
 
         def pe_interleave(i):
             n, gp = units[i]
-            a = TILES[n][2]
+            w, npe = TILES[n][1], TILES[n][2]
+            per_pass = w // P
             planes = st[i][0]
-            for b in range(a // P):
+            for b in range(0, npe, 2):
+                k = min(2, npe - b)
                 bank = ilp.tile([P, 2, NT], BF16, name="bank")
-                for gl in range(2):
+                for h in range(k):
+                    gl, sb = (b + h) // per_pass, (b + h) % per_pass
                     nc.tensor.matmul(
-                        out=bank[:, gl, :].rearrange("p (c t) -> p c t", t=PACK),
+                        out=bank[:, h, :].rearrange("p (c t) -> p c t", t=PACK),
                         lhsT=ident_b[:],
-                        rhs=planes[:, gl, :, b * P : (b + 1) * P].rearrange("p t c -> p c t"),
+                        rhs=planes[:, gl, :, sb * P : (sb + 1) * P].rearrange("p t c -> p c t"),
                         start=True,
                         stop=True,
                     )
-                st[i][2].append(bank)
+                st[i][2].append((bank, b, k))
+
+        def sbuf_interleave(copy, i, lo, hi):
+            n, gp = units[i]
+            per_pass = TILES[n][1] // P
+            planes, grouped = st[i][0], st[i][1]
+            for gl in range(2):
+                b0, b1 = max(lo, gl * per_pass), min(hi, (gl + 1) * per_pass)
+                if b0 < b1:
+                    c0, c1 = (b0 - gl * per_pass) * P, (b1 - gl * per_pass) * P
+                    copy(
+                        out=grouped[:, b0 * NT : b1 * NT].rearrange("p (c t) -> p c t", t=PACK),
+                        in_=planes[:, gl, :, c0:c1].rearrange("p t c -> p c t"),
+                    )
 
         def scalar_interleave(i):
             n, gp = units[i]
-            a, sil = TILES[n][2], TILES[n][3]
-            planes, grouped, banks = st[i]
-            for b in range(len(banks)):
-                nc.scalar.copy(out=grouped[:, :, b * NT : (b + 1) * NT], in_=banks[b][:])
-            if sil > 0:
+            npe, nsc = TILES[n][2], TILES[n][3]
+            grouped = st[i][1]
+            for (bank, b, k) in st[i][2]:
                 nc.scalar.copy(
-                    out=grouped[:, :, a * PACK : (a + sil) * PACK].rearrange("p g (c t) -> p g c t", t=PACK),
-                    in_=planes[:, :, :, a : a + sil].rearrange("p g t c -> p g c t"),
+                    out=grouped[:, b * NT : (b + k) * NT], in_=bank[:, 0:k, :].rearrange("p h c -> p (h c)")
                 )
+            sbuf_interleave(nc.scalar.copy, i, npe, npe + nsc)
 
         def vector_interleave(i):
             n, gp = units[i]
-            w, a, sil = TILES[n][1], TILES[n][2], TILES[n][3]
-            planes, grouped = st[i][0], st[i][1]
-            a = a + sil
-            if a < w:
-                nc.vector.tensor_copy(
-                    out=grouped[:, :, a * PACK : w * PACK].rearrange("p g (c t) -> p g c t", t=PACK),
-                    in_=planes[:, :, :, a:w].rearrange("p g t c -> p g c t"),
-                )
+            w, npe, nsc = TILES[n][1], TILES[n][2], TILES[n][3]
+            sbuf_interleave(nc.vector.tensor_copy, i, npe + nsc, 2 * w // P)
 
         def quantise(i):
             n, gp = units[i]
@@ -148,7 +166,7 @@ def tile_selfattention_pa_kernel(
             nc.vector.quantize_mx(
                 out=wcod[:, 2 * gp : 2 * gp + 2, :].rearrange("p g c -> p (g c)").bitcast(FP8X4),
                 scales=wsc[:, 2 * gp : 2 * gp + 2, :].rearrange("p g c -> p (g c)"),
-                in_=st[i][1][:].rearrange("p g c -> p (g c)"),
+                in_=st[i][1][:],
             )
 
         def mx_pass(acc, n, tt, g):
@@ -164,22 +182,33 @@ def tile_selfattention_pa_kernel(
                 stop=(g == G - 1),
             )
 
-        def out_half(n, half, accs):
+        def out_bias(n, half, accs):
             col, w = TILES[n][0], TILES[n][1]
             xb = obp.tile([P, 2, w], F32, name="xb")
             for k in range(2):
                 nc.vector.tensor_tensor(out=xb[:, k, :], in0=accs[k][:, 0:w], in1=bias_sb[:, col : col + w], op=ADD)
+            return xb
+
+        def out_products(n, half, xb):
+            col, w = TILES[n][0], TILES[n][1]
+            if col >= QCOLS + KCOLS:
+                return None
+            nh = w // HD
+            m12 = tmp.tile([P, 2, nh, 2, RD], F32, name="m12")
+            xr = xb[:].rearrange("p t (h d) -> p t h d", d=HD)[:, :, :, 0:RD]
+            nc.vector.tensor_tensor(
+                out=m12[:],
+                in0=xr.unsqueeze(3).to_broadcast([P, 2, nh, 2, RD]),
+                in1=cs_tab[:, 2 * half : 2 * half + 2, :, :].unsqueeze(2).to_broadcast([P, 2, nh, 2, RD]),
+                op=MULT,
+            )
+            return m12
+
+        def out_sum_store(n, half, xb, m12):
+            col, w = TILES[n][0], TILES[n][1]
             t0 = 2 * half
-            if col < QCOLS + KCOLS:
-                nh = w // HD
-                m12 = tmp.tile([P, 2, nh, 2, RD], F32, name="m12")
+            if m12 is not None:
                 xr = xb[:].rearrange("p t (h d) -> p t h d", d=HD)[:, :, :, 0:RD]
-                nc.vector.tensor_tensor(
-                    out=m12[:],
-                    in0=xr.unsqueeze(3).to_broadcast([P, 2, nh, 2, RD]),
-                    in1=cs_tab[:, t0 : t0 + 2, :, :].unsqueeze(2).to_broadcast([P, 2, nh, 2, RD]),
-                    op=MULT,
-                )
                 nc.vector.tensor_tensor(
                     out=xr.rearrange("p t h (j e) -> p t h j e", e=2),
                     in0=m12[:, :, :, 0, :].rearrange("p t h (j e) -> p t h j e", e=2),
@@ -246,10 +275,16 @@ def tile_selfattention_pa_kernel(
         def hidden_copy(tt, pts):
             xg = hid.tile([P, G, P, PACK], BF16, name="xg", align_bytes=64)
             for gh in range(2):
-                nc.vector.tensor_copy(
-                    out=xg[:, 2 * gh : 2 * gh + 2, :, :].bitcast(F32),
-                    in_=pts[gh][:].rearrange("p (g u r) -> p g r u", g=2, u=2),
-                )
+                if HIDDEN_ON_SCALAR:
+                    nc.scalar.copy(
+                        out=xg[:, 2 * gh : 2 * gh + 2, :, :].bitcast(F32),
+                        in_=pts[gh][:].rearrange("p (g u r) -> p g r u", g=2, u=2),
+                    )
+                else:
+                    nc.vector.tensor_copy(
+                        out=xg[:, 2 * gh : 2 * gh + 2, :, :].bitcast(F32),
+                        in_=pts[gh][:].rearrange("p (g u r) -> p g r u", g=2, u=2),
+                    )
             xgs[tt] = xg
 
         def hidden_quantise(tt):
@@ -271,23 +306,20 @@ def tile_selfattention_pa_kernel(
 
         mm_queue = []
         pending = []
+        summing = []
         last_n = len(TILES) - 1
         last_accs = []
         s = 0
-        while s < n_units + 1 or pending or mm_queue:
+        while s < n_units + 2 or pending or mm_queue or summing:
             if s >= 1:
                 for r in range(2):
                     if next_load < len(loads):
                         load(next_load)
                         next_load += 1
             if s < n_units:
-                widen(s, 0, SPLIT)
+                widen(s, 0, 2 * PACK)
             if 0 <= s - 1 < n_units:
                 scalar_interleave(s - 1)
-            if s < n_units:
-                widen(s, SPLIT, 2 * PACK)
-                pe_interleave(s)
-            if 0 <= s - 1 < n_units:
                 vector_interleave(s - 1)
             if s < 2:
                 for tt in (2 * s, 2 * s + 1):
@@ -296,10 +328,14 @@ def tile_selfattention_pa_kernel(
                     hidden_quantise(tt)
             if s == 2:
                 rope_tables()
+            if summing:
+                out_sum_store(*summing.pop(0))
+            job = None
             if pending:
-                out_half(*pending.pop(0))
-            if 0 <= s - 1 < n_units:
-                i = s - 1
+                job = pending.pop(0)
+                xb = out_bias(*job)
+            if 0 <= s - 2 < n_units:
+                i = s - 2
                 quantise(i)
                 n, gp = units[i]
                 if n == last_n:
@@ -315,6 +351,8 @@ def tile_selfattention_pa_kernel(
                 elif gp == 1:
                     mm_queue.append((n, 0))
                     mm_queue.append((n, 1))
+            if job is not None:
+                summing.append((job[0], job[1], xb, out_products(job[0], job[1], xb)))
             if mm_queue:
                 n, half = mm_queue.pop(0)
                 accs = []
@@ -324,4 +362,6 @@ def tile_selfattention_pa_kernel(
                         mx_pass(acc, n, 2 * half + k, g)
                     accs.append(acc)
                 pending.append((n, half, accs))
+            if s < n_units:
+                pe_interleave(s)
             s += 1

@@ -136,8 +136,8 @@ def tile_selfattention_pa_kernel(
                 if b0 < b1:
                     c0, c1 = (b0 - gl * per_pass) * P, (b1 - gl * per_pass) * P
                     copy(
-                        out=grouped[:, b0 * NT : b1 * NT].rearrange("p (c t) -> p c t", t=PACK),
-                        in_=planes[:, gl, :, c0:c1].rearrange("p t c -> p c t"),
+                        out=grouped[:, b0 * NT : b1 * NT].rearrange("p (c i t) -> p c t i", i=4, t=PACK),
+                        in_=planes[:, gl, :, c0:c1].rearrange("p t (c i) -> p c t i", i=4),
                     )
 
         def scalar_interleave(i):

@@ -28,20 +28,21 @@ QCOLS = 4096
 KCOLS = 256
 
 TILES = [
-    (0, 512, 2, 0, 3),
-    (512, 512, 3, 0, 0),
+    (0, 512, 2, 0, 8),
+    (512, 512, 3, 0, 2),
     (1024, 512, 3, 0, 0),
-    (1536, 512, 4, 0, 0),
-    (2048, 512, 4, 0, 0),
-    (2560, 512, 4, 0, 0),
-    (3072, 512, 4, 0, 0),
+    (1536, 512, 4, 0, 1),
+    (2048, 512, 4, 0, 1),
+    (2560, 512, 4, 0, 1),
+    (3072, 512, 4, 0, 1),
     (3584, 512, 4, 2, 0),
     (4096, 256, 0, 2, 0),
     (4352, 256, 0, 2, 0),
 ]
-HIDDEN_ON_SCALAR = False
+HIDDEN_ON_SCALAR = True
 LOAD_COLS = 512
 LOADS_AHEAD = 12
+HEAD = [("l", 0), ("l", 1), ("x", 0), ("x", 1), ("l", 2), ("l", 3), ("x", 2), ("x", 3), ("c", 0), ("l", 4), ("l", 5), ("l", 6), ("l", 7), ("b", 0), ("l", 8), ("l", 9), ("l", 10), ("l", 11)]
 
 
 def tile_selfattention_pa_kernel(
@@ -88,7 +89,7 @@ def tile_selfattention_pa_kernel(
                 st[i] = [planes, grouped, []]
             planes = st[i][0]
             base = (c0 // LOAD_COLS) * LOAD_COLS
-            vw = TILES[n][4]
+            vw = (TILES[n][4] + gp) // 2
             for q in range(lo, hi):
                 gl, t = q // PACK, q % PACK
                 g = 2 * gp + gl
@@ -229,18 +230,17 @@ def tile_selfattention_pa_kernel(
         cos_sb = const.tile([P, TT, RD], BF16, name="cos_sb")
         sin_sb = const.tile([P, TT, RD], BF16, name="sin_sb")
         bias_sb = const.tile([P, OUT], BF16, name="bias_sb")
-        for half in range(2):
-            load(2 * half)
-            load(2 * half + 1)
-            for tt in (2 * half, 2 * half + 1):
+        for item in HEAD:
+            if item[0] == "l":
+                load(item[1])
+            elif item[0] == "x":
+                tt = item[1]
                 nc.sync.dma_start(out=x_sb[:, tt, :], in_=hidden_states[tt * P : (tt + 1) * P, :])
-        nc.sync.dma_start(out=cos_sb[:], in_=cos.rearrange("(t p) d -> p t d", p=P))
-        nc.sync.dma_start(out=sin_sb[:], in_=sin.rearrange("(t p) d -> p t d", p=P))
-        for j in range(4, 8):
-            load(j)
-        nc.sync.dma_start(out=bias_sb[:], in_=b_qkv.partition_broadcast(P))
-        for j in range(8, LOADS_AHEAD):
-            load(j)
+            elif item[0] == "c":
+                nc.sync.dma_start(out=cos_sb[:], in_=cos.rearrange("(t p) d -> p t d", p=P))
+                nc.sync.dma_start(out=sin_sb[:], in_=sin.rearrange("(t p) d -> p t d", p=P))
+            else:
+                nc.sync.dma_start(out=bias_sb[:], in_=b_qkv.partition_broadcast(P))
         next_load = LOADS_AHEAD
 
         warm = const.tile([P, 2], F32, name="warm")

@@ -28,16 +28,16 @@ QCOLS = 4096
 KCOLS = 256
 
 TILES = [
-    (0, 512, 2, 0, 8),
+    (0, 512, 2, 0, 9),
     (512, 512, 3, 0, 2),
     (1024, 512, 3, 0, 0),
-    (1536, 512, 4, 0, 1),
+    (1536, 512, 4, 0, 2),
     (2048, 512, 4, 0, 1),
     (2560, 512, 4, 0, 1),
     (3072, 512, 4, 0, 1),
     (3584, 512, 4, 2, 0),
-    (4096, 256, 0, 2, 0),
-    (4352, 256, 0, 2, 0),
+    (4096, 256, 0, 3, 0),
+    (4352, 256, 0, 3, 0),
 ]
 HIDDEN_ON_SCALAR = True
 LOAD_COLS = 512
@@ -52,12 +52,12 @@ def tile_selfattention_pa_kernel(
     with ExitStack() as ctx:
         const = ctx.enter_context(tc.tile_pool(name="const", bufs=1))
         wbp = ctx.enter_context(tc.tile_pool(name="wbp", bufs=16))
-        plp = ctx.enter_context(tc.tile_pool(name="plp", bufs=3))
-        grp = ctx.enter_context(tc.tile_pool(name="grp", bufs=3))
+        plp = ctx.enter_context(tc.tile_pool(name="plp", bufs=4))
+        grp = ctx.enter_context(tc.tile_pool(name="grp", bufs=4))
         cdp = ctx.enter_context(tc.tile_pool(name="cdp", bufs=3))
         hid = ctx.enter_context(tc.tile_pool(name="hid", bufs=2))
-        obp = ctx.enter_context(tc.tile_pool(name="obp", bufs=4))
-        tmp = ctx.enter_context(tc.tile_pool(name="tmp", bufs=2))
+        obp = ctx.enter_context(tc.tile_pool(name="obp", bufs=6))
+        tmp = ctx.enter_context(tc.tile_pool(name="tmp", bufs=3))
         accp = ctx.enter_context(tc.psum_pool(name="accp", bufs=6))
         ilp = ctx.enter_context(tc.psum_pool(name="ilp", bufs=2))
         ctx.enter_context(tc.manual_schedule())

@@ -23,26 +23,26 @@ G = H // KP
 TT = T // P
 NT = 512
 RD = 64
+HJ = RD // 2
 HD = 128
 QCOLS = 4096
 KCOLS = 256
 
 TILES = [
-    (0, 512, 2, 0, 9),
-    (512, 512, 3, 0, 2),
-    (1024, 512, 3, 0, 0),
-    (1536, 512, 4, 0, 2),
-    (2048, 512, 4, 0, 1),
-    (2560, 512, 4, 0, 1),
-    (3072, 512, 4, 0, 1),
-    (3584, 512, 4, 2, 0),
-    (4096, 256, 0, 3, 0),
-    (4352, 256, 0, 3, 0),
+    (0, 512, "q", (2, 3), (0, 0), (4, 4)),
+    (512, 512, "q", (3, 3), (0, 0), (3, 3)),
+    (1024, 512, "q", (4, 3), (0, 0), (2, 2)),
+    (1536, 512, "q", (4, 3), (0, 0), (2, 2)),
+    (2048, 512, "q", (4, 3), (0, 0), (2, 2)),
+    (2560, 512, "q", (4, 3), (0, 0), (2, 2)),
+    (3072, 512, "q", (4, 3), (0, 0), (2, 2)),
+    (3584, 512, "q", (4, 3), (0, 0), (2, 2)),
+    (4096, 256, "k", (2, 2), (0, 0), (1, 1)),
+    (4352, 256, "v", (0, 0), (2, 2), (0, 0)),
 ]
-HIDDEN_ON_SCALAR = True
 LOAD_COLS = 512
 LOADS_AHEAD = 12
-HEAD = [("l", 0), ("l", 1), ("x", 0), ("x", 1), ("l", 2), ("l", 3), ("x", 2), ("x", 3), ("c", 0), ("l", 4), ("l", 5), ("l", 6), ("l", 7), ("b", 0), ("l", 8), ("l", 9), ("l", 10), ("l", 11)]
+HEAD = [("l", 0), ("l", 1), ("l", 2), ("l", 3), ("c", 0), ("x", 0), ("x", 1), ("l", 4), ("l", 5), ("x", 2), ("x", 3), ("l", 6), ("l", 7), ("b", 0), ("l", 8), ("l", 9), ("l", 10), ("l", 11)]
 
 
 def tile_selfattention_pa_kernel(
@@ -55,9 +55,9 @@ def tile_selfattention_pa_kernel(
         plp = ctx.enter_context(tc.tile_pool(name="plp", bufs=4))
         grp = ctx.enter_context(tc.tile_pool(name="grp", bufs=4))
         cdp = ctx.enter_context(tc.tile_pool(name="cdp", bufs=3))
-        hid = ctx.enter_context(tc.tile_pool(name="hid", bufs=2))
+        hid = ctx.enter_context(tc.tile_pool(name="hid", bufs=4))
         obp = ctx.enter_context(tc.tile_pool(name="obp", bufs=6))
-        tmp = ctx.enter_context(tc.tile_pool(name="tmp", bufs=3))
+        mp = ctx.enter_context(tc.tile_pool(name="mp", bufs=4))
         accp = ctx.enter_context(tc.psum_pool(name="accp", bufs=6))
         ilp = ctx.enter_context(tc.psum_pool(name="ilp", bufs=2))
         ctx.enter_context(tc.manual_schedule())
@@ -72,25 +72,22 @@ def tile_selfattention_pa_kernel(
 
         def load(j):
             c0, g = loads[j]
-            wc = min(LOAD_COLS, OUT - c0)
             w_bytes = wbp.tile([P, PACK, LOAD_COLS], U8, name="w_bytes")
             nc.sync.dma_start(
-                out=w_bytes[:, :, 0:wc],
-                in_=W_qkv_bytes[g * KP : (g + 1) * KP, c0 : c0 + wc].rearrange("(p t) n -> p t n", t=PACK),
+                out=w_bytes[:],
+                in_=W_qkv_bytes[g * KP : (g + 1) * KP, c0 : c0 + LOAD_COLS].rearrange("(p t) n -> p t n", t=PACK),
             )
             w_tiles[(c0, g)] = w_bytes
 
-        def widen(i, lo, hi):
+        def widen(i):
             n, gp = units[i]
             c0, w = TILES[n][0], TILES[n][1]
-            if lo == 0:
-                planes = plp.tile([P, 2, PACK, w], BF16, name="planes")
-                grouped = grp.tile([P, 2 * w * PACK], BF16, name="grouped", align_bytes=64)
-                st[i] = [planes, grouped, []]
-            planes = st[i][0]
+            planes = plp.tile([P, 2, PACK, w], BF16, name="planes")
+            grouped = grp.tile([P, 2 * w * PACK], BF16, name="grouped", align_bytes=64)
+            st[i] = [planes, grouped, []]
             base = (c0 // LOAD_COLS) * LOAD_COLS
-            vw = (TILES[n][4] + gp) // 2
-            for q in range(lo, hi):
+            vw = TILES[n][5][gp]
+            for q in range(2 * PACK):
                 gl, t = q // PACK, q % PACK
                 g = 2 * gp + gl
                 if q >= 2 * PACK - vw:
@@ -109,52 +106,94 @@ def tile_selfattention_pa_kernel(
                         scale=wscale[:, g, t : t + 1],
                     )
 
+        def rope_src(planes, gl, e):
+            v = planes[:, gl, :, :].rearrange("p t (h r j e) -> p t h r j e", r=2, j=HJ, e=2)
+            return v[:, :, :, 0, :, e].rearrange("p t h j -> p h j t")
+
+        def plain_src(planes, gl, kind, h0, h1):
+            if kind == "v":
+                v = planes[:, gl, :, :].rearrange("p t (h d) -> p t h d", d=RD)
+            else:
+                v = planes[:, gl, :, :].rearrange("p t (h r d) -> p t h r d", r=2, d=RD)[:, :, :, 1, :]
+            return v[:, :, h0:h1, :].rearrange("p t h d -> p h d t")
+
+        def rope_cols(n):
+            return 0 if TILES[n][2] == "v" else (TILES[n][1] // HD) * HJ
+
         def pe_interleave(i):
             n, gp = units[i]
-            w, npe = TILES[n][1], TILES[n][2]
-            per_pass = w // P
+            kind, npe = TILES[n][2], TILES[n][3][gp]
             planes = st[i][0]
-            for b in range(0, npe, 2):
-                k = min(2, npe - b)
+            if kind == "q":
+                for gl in range(2):
+                    k = min(2, npe - 2 * gl)
+                    if k > 0:
+                        bank = ilp.tile([P, 2, NT], BF16, name="bank")
+                        for e in range(k):
+                            nc.tensor.matmul(
+                                out=bank[:, e, :].rearrange("p (h j t) -> p h j t", j=HJ, t=PACK),
+                                lhsT=ident_b[:],
+                                rhs=rope_src(planes, gl, e),
+                                start=True,
+                                stop=True,
+                            )
+                        st[i][2].append((bank, gl, k))
+            elif kind == "k" and npe > 0:
                 bank = ilp.tile([P, 2, NT], BF16, name="bank")
-                for h in range(k):
-                    gl, sb = (b + h) // per_pass, (b + h) % per_pass
-                    nc.tensor.matmul(
-                        out=bank[:, h, :].rearrange("p (c t) -> p c t", t=PACK),
-                        lhsT=ident_b[:],
-                        rhs=planes[:, gl, :, sb * P : (sb + 1) * P].rearrange("p t c -> p c t"),
-                        start=True,
-                        stop=True,
-                    )
-                st[i][2].append((bank, b, k))
+                for gl in range(2):
+                    for e in range(2):
+                        nc.tensor.matmul(
+                            out=bank[:, gl, e * 256 : (e + 1) * 256].rearrange("p (h j t) -> p h j t", j=HJ, t=PACK),
+                            lhsT=ident_b[:],
+                            rhs=rope_src(planes, gl, e),
+                            start=True,
+                            stop=True,
+                        )
+                st[i][2].append((bank, 0, 0))
 
-        def sbuf_interleave(copy, i, lo, hi):
+        def plain_interleave(copy, i, gl, h0, h1):
             n, gp = units[i]
-            per_pass = TILES[n][1] // P
+            w, kind = TILES[n][1], TILES[n][2]
             planes, grouped = st[i][0], st[i][1]
-            for gl in range(2):
-                b0, b1 = max(lo, gl * per_pass), min(hi, (gl + 1) * per_pass)
-                if b0 < b1:
-                    c0, c1 = (b0 - gl * per_pass) * P, (b1 - gl * per_pass) * P
-                    copy(
-                        out=grouped[:, b0 * NT : b1 * NT].rearrange("p (c i t) -> p c t i", i=4, t=PACK),
-                        in_=planes[:, gl, :, c0:c1].rearrange("p t (c i) -> p c t i", i=4),
-                    )
+            a = gl * w * PACK + 2 * rope_cols(n) * PACK
+            copy(
+                out=grouped[:, a + h0 * RD * PACK : a + h1 * RD * PACK].rearrange("p (h d t) -> p h d t", d=RD, t=PACK),
+                in_=plain_src(planes, gl, kind, h0, h1),
+            )
+
+        def plain_blocks(n):
+            return (TILES[n][1] - 2 * rope_cols(n)) // RD
 
         def scalar_interleave(i):
             n, gp = units[i]
-            npe, nsc = TILES[n][2], TILES[n][3]
+            w, kind, nsc = TILES[n][1], TILES[n][2], TILES[n][4][gp]
             grouped = st[i][1]
-            for (bank, b, k) in st[i][2]:
-                nc.scalar.copy(
-                    out=grouped[:, b * NT : (b + k) * NT], in_=bank[:, 0:k, :].rearrange("p h c -> p (h c)")
-                )
-            sbuf_interleave(nc.scalar.copy, i, npe, npe + nsc)
+            for (bank, gl, k) in st[i][2]:
+                if kind == "q":
+                    a = gl * w * PACK
+                    nc.scalar.copy(out=grouped[:, a : a + k * NT], in_=bank[:, 0:k, :].rearrange("p h c -> p (h c)"))
+                else:
+                    nc.scalar.copy(out=grouped[:].rearrange("p (g c) -> p g c", g=2)[:, :, 0:NT], in_=bank[:])
+            if nsc > 0:
+                for gl in range(2):
+                    plain_interleave(nc.scalar.copy, i, gl, plain_blocks(n) - nsc, plain_blocks(n))
 
         def vector_interleave(i):
             n, gp = units[i]
-            w, npe, nsc = TILES[n][1], TILES[n][2], TILES[n][3]
-            sbuf_interleave(nc.vector.tensor_copy, i, npe + nsc, 2 * w // P)
+            w, kind, npe, nsc = TILES[n][1], TILES[n][2], TILES[n][3][gp], TILES[n][4][gp]
+            planes, grouped = st[i][0], st[i][1]
+            rc = rope_cols(n)
+            for gl in range(2):
+                for e in range(2):
+                    on_pe = (2 * gl + e < npe) if kind == "q" else (npe > 0)
+                    if rc > 0 and not on_pe:
+                        a = gl * w * PACK + e * rc * PACK
+                        nc.vector.tensor_copy(
+                            out=grouped[:, a : a + rc * PACK].rearrange("p (h j t) -> p h j t", j=HJ, t=PACK),
+                            in_=rope_src(planes, gl, e),
+                        )
+                if plain_blocks(n) - nsc > 0:
+                    plain_interleave(nc.vector.tensor_copy, i, gl, 0, plain_blocks(n) - nsc)
 
         def quantise(i):
             n, gp = units[i]
@@ -170,59 +209,124 @@ def tile_selfattention_pa_kernel(
                 in_=st[i][1][:],
             )
 
-        def mx_pass(acc, n, tt, g):
+        rope_acc = {}
+        plain_acc = {}
+        prods = {}
+        ybanks = {}
+        xbs = {}
+
+        def mx_rope(n):
             wcod, wsc = codes[n]
-            w = TILES[n][1]
-            nc.tensor.matmul_mx(
-                out=acc[:, 0:w],
-                lhsT=xc[:, tt, g * P : (g + 1) * P].bitcast(FP8X4),
-                lhsT_scale=xs[:, tt, g * P : (g + 1) * P],
-                rhs=wcod[:, g, :].bitcast(FP8X4),
-                rhs_scale=wsc[:, g, :],
-                start=(g == 0),
-                stop=(g == G - 1),
-            )
+            rc = rope_cols(n)
+            rope_acc[n] = []
+            for e in range(2):
+                acc = accp.tile([P, NT], F32, name="acc")
+                for g in range(G):
+                    nc.tensor.matmul_mx(
+                        out=acc[:],
+                        lhsT=wcod[:, g, e * rc : e * rc + P].bitcast(FP8X4),
+                        lhsT_scale=wsc[:, g, e * rc : e * rc + P],
+                        rhs=xc[:, g, :].bitcast(FP8X4),
+                        rhs_scale=xs[:, g, :],
+                        start=(g == 0),
+                        stop=(g == G - 1),
+                    )
+                rope_acc[n].append(acc)
 
-        def out_bias(n, half, accs):
-            col, w = TILES[n][0], TILES[n][1]
+        def mx_plain(n):
+            wcod, wsc = codes[n]
+            p0 = 2 * rope_cols(n)
+            pw = TILES[n][1] - p0
+            per_bank = NT // pw
+            views = []
+            for b in range(TT // per_bank):
+                acc = accp.tile([P, per_bank, pw], F32, name="acc")
+                for k in range(per_bank):
+                    tt = b * per_bank + k
+                    for g in range(G):
+                        nc.tensor.matmul_mx(
+                            out=acc[:, k, :],
+                            lhsT=xc[:, g, tt * P : (tt + 1) * P].bitcast(FP8X4),
+                            lhsT_scale=xs[:, g, tt * P : (tt + 1) * P],
+                            rhs=wcod[:, g, p0 : p0 + pw].bitcast(FP8X4),
+                            rhs_scale=wsc[:, g, p0 : p0 + pw],
+                            start=(g == 0),
+                            stop=(g == G - 1),
+                        )
+                for k in range(0, per_bank, 2):
+                    views.append(acc[:, k : k + 2, :])
+            plain_acc[n] = views
+
+        def products(n, e):
+            m = mp.tile([P, 2, T], F32, name="m")
+            nc.vector.scalar_tensor_tensor(
+                out=m[:],
+                in0=rope_acc[n][e][:].unsqueeze(1).to_broadcast([P, 2, T]),
+                scalar=bias_r[:, n, e : e + 1],
+                in1=tabs[e][:],
+                op0=ADD,
+                op1=MULT,
+            )
+            prods[(n, e)] = m
+
+        def rope_transposes(n):
+            ybanks[n] = []
+            for half in range(2):
+                y = accp.tile([P, 2, 2, P], F32, name="acc")
+                for f in range(2):
+                    for tl in range(2):
+                        tt = 2 * half + tl
+                        for e in range(2):
+                            nc.tensor.matmul(
+                                out=y[:, f, tl, :],
+                                lhsT=prods[(n, e)][:, f, tt * P : (tt + 1) * P],
+                                rhs=ident_f[:],
+                                is_transpose=True,
+                                start=(e == 0),
+                                stop=(e == 1),
+                            )
+                ybanks[n].append(y)
+
+        def bias_plain(n, half):
+            col, w, kind = TILES[n][0], TILES[n][1], TILES[n][2]
             xb = obp.tile([P, 2, w], F32, name="xb")
-            for k in range(2):
-                nc.vector.tensor_tensor(out=xb[:, k, :], in0=accs[k][:, 0:w], in1=bias_sb[:, col : col + w], op=ADD)
-            return xb
-
-        def out_products(n, half, xb):
-            col, w = TILES[n][0], TILES[n][1]
-            if col >= QCOLS + KCOLS:
-                return None
-            nh = w // HD
-            m12 = tmp.tile([P, 2, nh, 2, RD], F32, name="m12")
-            xr = xb[:].rearrange("p t (h d) -> p t h d", d=HD)[:, :, :, 0:RD]
-            nc.vector.tensor_tensor(
-                out=m12[:],
-                in0=xr.unsqueeze(3).to_broadcast([P, 2, nh, 2, RD]),
-                in1=cs_tab[:, 2 * half : 2 * half + 2, :, :].unsqueeze(2).to_broadcast([P, 2, nh, 2, RD]),
-                op=MULT,
-            )
-            return m12
-
-        def out_sum_store(n, half, xb, m12):
-            col, w = TILES[n][0], TILES[n][1]
-            t0 = 2 * half
-            if m12 is not None:
-                xr = xb[:].rearrange("p t (h d) -> p t h d", d=HD)[:, :, :, 0:RD]
+            acc = plain_acc[n][half]
+            if kind == "v":
                 nc.vector.tensor_tensor(
-                    out=xr.rearrange("p t h (j e) -> p t h j e", e=2),
-                    in0=m12[:, :, :, 0, :].rearrange("p t h (j e) -> p t h j e", e=2),
-                    in1=m12[:, :, :, 1, :].rearrange("p t h (j e) -> p t h j e", e=2)[:, :, :, :, ::-1],
+                    out=xb[:], in0=acc, in1=bias_sb[:, col : col + w].unsqueeze(1).to_broadcast([P, 2, w]), op=ADD
+                )
+            else:
+                nh = w // HD
+                nc.vector.tensor_tensor(
+                    out=xb[:].rearrange("p t (h d) -> p t h d", d=HD)[:, :, :, RD:HD],
+                    in0=acc.rearrange("p t (h d) -> p t h d", d=RD),
+                    in1=bias_sb[:, col : col + w]
+                    .rearrange("p (h d) -> p h d", d=HD)[:, :, RD:HD]
+                    .unsqueeze(1)
+                    .to_broadcast([P, 2, nh, RD]),
                     op=ADD,
                 )
+            xbs[(n, half)] = xb
+
+        def rope_out(n, half):
+            rc = rope_cols(n)
+            nc.scalar.copy(
+                out=xbs[(n, half)][:]
+                .rearrange("p t (h d) -> p t h d", d=HD)[:, :, :, 0:RD]
+                .rearrange("p t h (j f) -> p t h j f", f=2),
+                in_=ybanks[n][half][:, :, :, 0:rc].rearrange("p f t (h j) -> p t h j f", j=HJ),
+            )
+
+        def store(n, half):
+            col, w = TILES[n][0], TILES[n][1]
+            t0 = 2 * half
             if col < QCOLS:
                 dst = out_0.rearrange("(t p) h d -> p t (h d)", p=P)[:, t0 : t0 + 2, col : col + w]
             elif col < QCOLS + KCOLS:
                 dst = out_1.rearrange("(t p) h d -> p t (h d)", p=P)[:, t0 : t0 + 2, :]
             else:
                 dst = out_2.rearrange("(t p) h d -> p t (h d)", p=P)[:, t0 : t0 + 2, :]
-            nc.sync.dma_start(out=dst, in_=xb[:])
+            nc.sync.dma_start(out=dst, in_=xbs[(n, half)][:])
 
         wscale = const.tile([P, G, PACK], F32, name="wscale")
         nc.sync.dma_start(out=wscale[:], in_=W_qkv_scale.rearrange("(g p t) o -> p g (t o)", p=P, t=PACK))
@@ -230,6 +334,15 @@ def tile_selfattention_pa_kernel(
         cos_sb = const.tile([P, TT, RD], BF16, name="cos_sb")
         sin_sb = const.tile([P, TT, RD], BF16, name="sin_sb")
         bias_sb = const.tile([P, OUT], BF16, name="bias_sb")
+        n_rope = QCOLS // NT + 1
+        bias_r = const.tile([P, n_rope, 2], BF16, name="bias_r")
+        nc.vector.memset(bias_r[:], 0.0)
+        bq = b_qkv[0:QCOLS].rearrange("(n h r j e) -> h r j n e", h=4, r=2, j=HJ, e=2)
+        bk = b_qkv[QCOLS : QCOLS + KCOLS].rearrange("(n h r j e) -> h r j n e", h=2, r=2, j=HJ, e=2)
+        for h in range(4):
+            nc.scalar.dma_start(out=bias_r[h * HJ : (h + 1) * HJ, 0 : n_rope - 1, :], in_=bq[h, 0])
+        for h in range(2):
+            nc.scalar.dma_start(out=bias_r[h * HJ : (h + 1) * HJ, n_rope - 1 : n_rope, :], in_=bk[h, 0])
         for item in HEAD:
             if item[0] == "l":
                 load(item[1])
@@ -252,116 +365,118 @@ def tile_selfattention_pa_kernel(
         ident_b = const.tile([P, P], BF16, name="ident_b")
         make_identity(nc, ident_b[:])
 
-        xc = const.tile([P, TT, G * P], U32, name="xc", align_bytes=64)
-        xs = const.tile([P, TT, G * P], U8, name="xs", align_bytes=64)
-        cs_tab = const.tile([P, TT, 2, RD], F32, name="cs_tab")
+
+        xc = const.tile([P, G, T], U32, name="xc", align_bytes=64)
+        xs = const.tile([P, G, T], U8, name="xs", align_bytes=64)
+        tab_src = const.tile([P, TT, 4, 4, HJ], BF16, name="tab_src")
+        tabs = [const.tile([P, 2, T], BF16, name="tab_even"), const.tile([P, 2, T], BF16, name="tab_odd")]
         xgs = {}
 
-        def hidden_transpose(tt):
-            words = x_sb[:, tt, :].bitcast(F32)
-            pts = []
-            for gh in range(2):
+        def hidden_half(th):
+            for g in range(G):
+                if th == 0:
+                    xg = hid.tile([P, TT, P, PACK], BF16, name="xg", align_bytes=64)
+                    xgs[g] = xg
                 pt = accp.tile([P, NT], F32, name="acc")
-                for gl in range(2):
-                    g = 2 * gh + gl
+                for tl in range(2):
+                    words = x_sb[:, 2 * th + tl, :].bitcast(F32)
                     for u in range(2):
-                        q = 2 * gl + u
+                        q = 2 * tl + u
                         nc.tensor.transpose(
                             pt[:, q * P : (q + 1) * P], words[:, 256 * g + u : 256 * (g + 1) : 2], ident_f[:]
                         )
-                pts.append(pt)
-            return pts
+                nc.scalar.copy(
+                    out=xgs[g][:, 2 * th : 2 * th + 2, :, :].bitcast(F32),
+                    in_=pt[:].rearrange("p (t u r) -> p t r u", t=2, u=2),
+                )
 
-        def hidden_copy(tt, pts):
-            xg = hid.tile([P, G, P, PACK], BF16, name="xg", align_bytes=64)
-            for gh in range(2):
-                if HIDDEN_ON_SCALAR:
-                    nc.scalar.copy(
-                        out=xg[:, 2 * gh : 2 * gh + 2, :, :].bitcast(F32),
-                        in_=pts[gh][:].rearrange("p (g u r) -> p g r u", g=2, u=2),
-                    )
-                else:
-                    nc.vector.tensor_copy(
-                        out=xg[:, 2 * gh : 2 * gh + 2, :, :].bitcast(F32),
-                        in_=pts[gh][:].rearrange("p (g u r) -> p g r u", g=2, u=2),
-                    )
-            xgs[tt] = xg
-
-        def hidden_quantise(tt):
+        def hidden_quantise(g):
             nc.vector.quantize_mx(
-                out=xc[:, tt, :].bitcast(FP8X4),
-                scales=xs[:, tt, :],
-                in_=xgs[tt][:].rearrange("p g r j -> p (g r j)"),
+                out=xc[:, g, :].bitcast(FP8X4),
+                scales=xs[:, g, :],
+                in_=xgs[g][:].rearrange("p t r j -> p (t r j)"),
             )
 
-        def rope_tables():
-            nc.vector.tensor_copy(
-                out=cs_tab[:, :, 0, :].rearrange("p t (j e) -> p t j e", e=2),
-                in_=cos_sb[:].rearrange("p t (e j) -> p t j e", e=2),
-            )
-            sv = cs_tab[:, :, 1, :].rearrange("p t (j e) -> p t j e", e=2)
-            sn = sin_sb[:].rearrange("p t (e j) -> p t j e", e=2)
-            nc.vector.tensor_scalar(out=sv[:, :, :, 1:2], in0=sn[:, :, :, 0:1], scalar1=-1.0, scalar2=None, op0=MULT)
-            nc.vector.tensor_copy(out=sv[:, :, :, 0:1], in_=sn[:, :, :, 1:2])
+        def table_sources():
+            for k, (src, lo) in enumerate(((cos_sb, 0), (sin_sb, HJ), (sin_sb, 0), (cos_sb, HJ))):
+                nc.vector.tensor_scalar(
+                    out=tab_src[:, :, k, :, :],
+                    in0=src[:, :, lo : lo + HJ].unsqueeze(2).to_broadcast([P, TT, 4, HJ]),
+                    scalar1=(-1.0 if k == 2 else 1.0),
+                    scalar2=None,
+                    op0=MULT,
+                )
 
-        mm_queue = []
-        pending = []
-        summing = []
-        last_n = len(TILES) - 1
-        last_accs = []
-        s = 0
-        while s < n_units + 2 or pending or mm_queue or summing:
+        def table_transposes():
+            for e in range(2):
+                pt = accp.tile([P, 2, T], BF16, name="acc")
+                for f in range(2):
+                    for tt in range(TT):
+                        nc.tensor.transpose(
+                            pt[:, f, tt * P : (tt + 1) * P],
+                            tab_src[:, tt, 2 * e + f, :, :].rearrange("p h j -> p (h j)"),
+                            ident_b[:],
+                        )
+                nc.scalar.copy(out=tabs[e][:], in_=pt[:])
+
+        def tile_at(s, d):
+            k = s - 3 - d
+            return k // 2 if (k >= 0 and k % 2 == 0 and k // 2 < len(TILES)) else None
+
+        def has_rope(n):
+            return n is not None and TILES[n][2] != "v"
+
+        def is_v(n):
+            return n is not None and TILES[n][2] == "v"
+
+        for s in range(n_units + 4):
             if s >= 1:
                 for r in range(2):
                     if next_load < len(loads):
                         load(next_load)
                         next_load += 1
             if s < n_units:
-                widen(s, 0, 2 * PACK)
+                widen(s)
             if 0 <= s - 1 < n_units:
                 scalar_interleave(s - 1)
                 vector_interleave(s - 1)
-            if s < 2:
-                for tt in (2 * s, 2 * s + 1):
-                    hidden_copy(tt, hidden_transpose(tt))
-                for tt in (2 * s, 2 * s + 1):
-                    hidden_quantise(tt)
+            if s == 0:
+                table_sources()
+            if s in (1, 2):
+                hidden_half(s - 1)
+            if s == 3:
+                for g in range(G):
+                    hidden_quantise(g)
             if s == 2:
-                rope_tables()
-            if summing:
-                out_sum_store(*summing.pop(0))
-            job = None
-            if pending:
-                job = pending.pop(0)
-                xb = out_bias(*job)
+                table_transposes()
+            n0, n1, n2, n3 = tile_at(s, 0), tile_at(s, 1), tile_at(s, 2), tile_at(s, 3)
+            if has_rope(n3):
+                for half in range(2):
+                    rope_out(n3, half)
+                    store(n3, half)
+            if has_rope(n1):
+                products(n1, 0)
+            if has_rope(n2):
+                bias_plain(n2, 0)
+            if is_v(n1):
+                bias_plain(n1, 0)
+                store(n1, 0)
             if 0 <= s - 2 < n_units:
-                i = s - 2
-                quantise(i)
-                n, gp = units[i]
-                if n == last_n:
-                    for tt in range(TT):
-                        if gp == 0:
-                            acc = accp.tile([P, NT], F32, name="acc")
-                            last_accs.append(acc)
-                        mx_pass(last_accs[tt], n, tt, 2 * gp)
-                        mx_pass(last_accs[tt], n, tt, 2 * gp + 1)
-                    if gp == 1:
-                        pending.append((n, 0, last_accs[0:2]))
-                        pending.append((n, 1, last_accs[2:4]))
-                elif gp == 1:
-                    mm_queue.append((n, 0))
-                    mm_queue.append((n, 1))
-            if job is not None:
-                summing.append((job[0], job[1], xb, out_products(job[0], job[1], xb)))
-            if mm_queue:
-                n, half = mm_queue.pop(0)
-                accs = []
-                for k in range(2):
-                    acc = accp.tile([P, NT], F32, name="acc")
-                    for g in range(G):
-                        mx_pass(acc, n, 2 * half + k, g)
-                    accs.append(acc)
-                pending.append((n, half, accs))
+                quantise(s - 2)
+            if has_rope(n1):
+                products(n1, 1)
+            if has_rope(n2):
+                bias_plain(n2, 1)
+            if is_v(n1):
+                bias_plain(n1, 1)
+                store(n1, 1)
+            if has_rope(n2):
+                rope_transposes(n2)
+            if has_rope(n0):
+                mx_rope(n0)
+            if has_rope(n1):
+                mx_plain(n1)
+            if is_v(n0):
+                mx_plain(n0)
             if s < n_units:
                 pe_interleave(s)
-            s += 1

@@ -42,7 +42,7 @@ TILES = [
 ]
 LOAD_COLS = 512
 LOADS_AHEAD = 12
-HEAD = [("l", 0), ("l", 1), ("l", 2), ("l", 3), ("c", 0), ("x", 0), ("x", 1), ("l", 4), ("l", 5), ("x", 2), ("x", 3), ("l", 6), ("l", 7), ("b", 0), ("l", 8), ("l", 9), ("l", 10), ("l", 11)]
+HEAD = [("l", 0), ("l", 1), ("l", 2), ("l", 3), ("c", 0), ("r", 0), ("x", 0), ("x", 1), ("l", 4), ("l", 5), ("x", 2), ("x", 3), ("l", 6), ("l", 7), ("b", 0), ("l", 8), ("l", 9), ("l", 10), ("l", 11)]
 
 
 def tile_selfattention_pa_kernel(
@@ -171,9 +171,15 @@ def tile_selfattention_pa_kernel(
             for (bank, gl, k) in st[i][2]:
                 if kind == "q":
                     a = gl * w * PACK
-                    nc.scalar.copy(out=grouped[:, a : a + k * NT], in_=bank[:, 0:k, :].rearrange("p h c -> p (h c)"))
+                    nc.scalar.copy(
+                        out=grouped[:, a : a + k * NT].bitcast(F32),
+                        in_=bank[:, 0:k, :].rearrange("p h c -> p (h c)").bitcast(F32),
+                    )
                 else:
-                    nc.scalar.copy(out=grouped[:].rearrange("p (g c) -> p g c", g=2)[:, :, 0:NT], in_=bank[:])
+                    nc.scalar.copy(
+                        out=grouped[:].bitcast(F32).rearrange("p (g c) -> p g c", g=2)[:, :, 0 : NT // 2],
+                        in_=bank[:].rearrange("p g c -> p (g c)").bitcast(F32).rearrange("p (g c) -> p g c", g=2),
+                    )
             if nsc > 0:
                 for gl in range(2):
                     plain_interleave(nc.scalar.copy, i, gl, plain_blocks(n) - nsc, plain_blocks(n))
@@ -214,92 +220,85 @@ def tile_selfattention_pa_kernel(
         prods = {}
         ybanks = {}
         xbs = {}
+        HT = T // 2
 
-        def mx_rope(n):
+        def mx_rope(n, half):
             wcod, wsc = codes[n]
             rc = rope_cols(n)
-            rope_acc[n] = []
+            acc = accp.tile([P, 2, HT], F32, name="acc")
             for e in range(2):
-                acc = accp.tile([P, NT], F32, name="acc")
                 for g in range(G):
                     nc.tensor.matmul_mx(
-                        out=acc[:],
+                        out=acc[:, e, :],
                         lhsT=wcod[:, g, e * rc : e * rc + P].bitcast(FP8X4),
                         lhsT_scale=wsc[:, g, e * rc : e * rc + P],
-                        rhs=xc[:, g, :].bitcast(FP8X4),
-                        rhs_scale=xs[:, g, :],
+                        rhs=xc[:, g, half * HT : (half + 1) * HT].bitcast(FP8X4),
+                        rhs_scale=xs[:, g, half * HT : (half + 1) * HT],
                         start=(g == 0),
                         stop=(g == G - 1),
                     )
-                rope_acc[n].append(acc)
+            rope_acc[(n, half)] = acc
 
-        def mx_plain(n):
+        def mx_plain(n, half):
             wcod, wsc = codes[n]
             p0 = 2 * rope_cols(n)
             pw = TILES[n][1] - p0
-            per_bank = NT // pw
-            views = []
-            for b in range(TT // per_bank):
-                acc = accp.tile([P, per_bank, pw], F32, name="acc")
-                for k in range(per_bank):
-                    tt = b * per_bank + k
-                    for g in range(G):
-                        nc.tensor.matmul_mx(
-                            out=acc[:, k, :],
-                            lhsT=xc[:, g, tt * P : (tt + 1) * P].bitcast(FP8X4),
-                            lhsT_scale=xs[:, g, tt * P : (tt + 1) * P],
-                            rhs=wcod[:, g, p0 : p0 + pw].bitcast(FP8X4),
-                            rhs_scale=wsc[:, g, p0 : p0 + pw],
-                            start=(g == 0),
-                            stop=(g == G - 1),
+            acc = accp.tile([P, 2, pw], F32, name="acc")
+            for k in range(2):
+                tt = 2 * half + k
+                for g in range(G):
+                    nc.tensor.matmul_mx(
+                        out=acc[:, k, :],
+                        lhsT=xc[:, g, tt * P : (tt + 1) * P].bitcast(FP8X4),
+                        lhsT_scale=xs[:, g, tt * P : (tt + 1) * P],
+                        rhs=wcod[:, g, p0 : p0 + pw].bitcast(FP8X4),
+                        rhs_scale=wsc[:, g, p0 : p0 + pw],
+                        start=(g == 0),
+                        stop=(g == G - 1),
+                    )
+            plain_acc[(n, half)] = acc
+
+        def products(n, half):
+            m = mp.tile([P, 2, 2, HT], F32, name="m")
+            for e in range(2):
+                nc.vector.scalar_tensor_tensor(
+                    out=m[:, e, :, :],
+                    in0=rope_acc[(n, half)][:, e, :].unsqueeze(1).to_broadcast([P, 2, HT]),
+                    scalar=bias_r[:, n, e : e + 1],
+                    in1=tabs[e][:, :, half * HT : (half + 1) * HT],
+                    op0=ADD,
+                    op1=MULT,
+                )
+            prods[(n, half)] = m
+
+        def rope_transposes(n, half):
+            y = accp.tile([P, 2, 2, P], F32, name="acc")
+            for f in range(2):
+                for tl in range(2):
+                    for e in range(2):
+                        nc.tensor.matmul(
+                            out=y[:, f, tl, :],
+                            lhsT=prods[(n, half)][:, e, f, tl * P : (tl + 1) * P],
+                            rhs=ident_f[:],
+                            is_transpose=True,
+                            start=(e == 0),
+                            stop=(e == 1),
                         )
-                for k in range(0, per_bank, 2):
-                    views.append(acc[:, k : k + 2, :])
-            plain_acc[n] = views
-
-        def products(n, e):
-            m = mp.tile([P, 2, T], F32, name="m")
-            nc.vector.scalar_tensor_tensor(
-                out=m[:],
-                in0=rope_acc[n][e][:].unsqueeze(1).to_broadcast([P, 2, T]),
-                scalar=bias_r[:, n, e : e + 1],
-                in1=tabs[e][:],
-                op0=ADD,
-                op1=MULT,
-            )
-            prods[(n, e)] = m
-
-        def rope_transposes(n):
-            ybanks[n] = []
-            for half in range(2):
-                y = accp.tile([P, 2, 2, P], F32, name="acc")
-                for f in range(2):
-                    for tl in range(2):
-                        tt = 2 * half + tl
-                        for e in range(2):
-                            nc.tensor.matmul(
-                                out=y[:, f, tl, :],
-                                lhsT=prods[(n, e)][:, f, tt * P : (tt + 1) * P],
-                                rhs=ident_f[:],
-                                is_transpose=True,
-                                start=(e == 0),
-                                stop=(e == 1),
-                            )
-                ybanks[n].append(y)
+            ybanks[(n, half)] = y
 
         def bias_plain(n, half):
             col, w, kind = TILES[n][0], TILES[n][1], TILES[n][2]
             xb = obp.tile([P, 2, w], F32, name="xb")
-            acc = plain_acc[n][half]
+            acc = plain_acc[(n, half)]
             if kind == "v":
                 nc.vector.tensor_tensor(
-                    out=xb[:], in0=acc, in1=bias_sb[:, col : col + w].unsqueeze(1).to_broadcast([P, 2, w]), op=ADD
+                    out=xb[:], in0=acc[:], in1=bias_sb[:, col : col + w].unsqueeze(1).to_broadcast([P, 2, w]), op=ADD
                 )
             else:
                 nh = w // HD
                 nc.vector.tensor_tensor(
                     out=xb[:].rearrange("p t (h d) -> p t h d", d=HD)[:, :, :, RD:HD],
-                    in0=acc.rearrange("p t (h d) -> p t h d", d=RD),
+                    in0=acc[:].rearrange("p t (h d) -> p t h d", d=RD),
                     in1=bias_sb[:, col : col + w]
                     .rearrange("p (h d) -> p h d", d=HD)[:, :, RD:HD]
                     .unsqueeze(1)
@@ -314,7 +313,7 @@ def tile_selfattention_pa_kernel(
                 out=xbs[(n, half)][:]
                 .rearrange("p t (h d) -> p t h d", d=HD)[:, :, :, 0:RD]
                 .rearrange("p t h (j f) -> p t h j f", f=2),
-                in_=ybanks[n][half][:, :, :, 0:rc].rearrange("p f t (h j) -> p t h j f", j=HJ),
+                in_=ybanks[(n, half)][:, :, :, 0:rc].rearrange("p f t (h j) -> p t h j f", j=HJ),
             )
 
         def store(n, half):
@@ -335,14 +334,8 @@ def tile_selfattention_pa_kernel(
         sin_sb = const.tile([P, TT, RD], BF16, name="sin_sb")
         bias_sb = const.tile([P, OUT], BF16, name="bias_sb")
         n_rope = QCOLS // NT + 1
-        bias_r = const.tile([P, n_rope, 2], BF16, name="bias_r")
-        nc.vector.memset(bias_r[:], 0.0)
-        bq = b_qkv[0:QCOLS].rearrange("(n h r j e) -> h r j n e", h=4, r=2, j=HJ, e=2)
-        bk = b_qkv[QCOLS : QCOLS + KCOLS].rearrange("(n h r j e) -> h r j n e", h=2, r=2, j=HJ, e=2)
-        for h in range(4):
-            nc.scalar.dma_start(out=bias_r[h * HJ : (h + 1) * HJ, 0 : n_rope - 1, :], in_=bq[h, 0])
-        for h in range(2):
-            nc.scalar.dma_start(out=bias_r[h * HJ : (h + 1) * HJ, n_rope - 1 : n_rope, :], in_=bk[h, 0])
+        b_rows = const.tile([P, NT], BF16, name="b_rows")
+        nc.gpsimd.memset(b_rows[:], 0.0)
         for item in HEAD:
             if item[0] == "l":
                 load(item[1])
@@ -352,6 +345,12 @@ def tile_selfattention_pa_kernel(
             elif item[0] == "c":
                 nc.sync.dma_start(out=cos_sb[:], in_=cos.rearrange("(t p) d -> p t d", p=P))
                 nc.sync.dma_start(out=sin_sb[:], in_=sin.rearrange("(t p) d -> p t d", p=P))
+            elif item[0] == "r":
+                nc.sync.dma_start(out=b_rows[0 : n_rope - 1, :], in_=b_qkv[0:QCOLS].rearrange("(n c) -> n c", c=NT))
+                nc.sync.dma_start(
+                    out=b_rows[n_rope - 1 : n_rope, 0:KCOLS],
+                    in_=b_qkv[QCOLS : QCOLS + KCOLS].rearrange("(n c) -> n c", c=KCOLS),
+                )
             else:
                 nc.sync.dma_start(out=bias_sb[:], in_=b_qkv.partition_broadcast(P))
         next_load = LOADS_AHEAD
@@ -407,6 +406,21 @@ def tile_selfattention_pa_kernel(
                     op0=MULT,
                 )
 
+        b_cols = const.tile([P, 2, 4, HJ], BF16, name="b_cols")
+        bias_r = const.tile([P, n_rope, 2], BF16, name="bias_r")
+
+        def rope_bias_sources():
+            nc.vector.tensor_copy(
+                out=b_cols[:],
+                in_=b_rows[:].rearrange("p (h r j e) -> p r e h j", r=2, j=HJ, e=2)[:, 0],
+            )
+
+        def rope_bias_transposes():
+            pt = accp.tile([P, 2, P], BF16, name="acc")
+            for e in range(2):
+                nc.tensor.transpose(pt[:, e, :], b_cols[:, e, :, :].rearrange("p h j -> p (h j)"), ident_b[:])
+            nc.scalar.copy(out=bias_r[:].rearrange("p n e -> p e n"), in_=pt[:, :, 0:n_rope])
+
         def table_transposes():
             for e in range(2):
                 pt = accp.tile([P, 2, T], BF16, name="acc")
@@ -419,29 +433,44 @@ def tile_selfattention_pa_kernel(
                         )
                 nc.scalar.copy(out=tabs[e][:], in_=pt[:])
 
-        def tile_at(s, d):
-            k = s - 3 - d
-            return k // 2 if (k >= 0 and k % 2 == 0 and k // 2 < len(TILES)) else None
+        jobs = {}
+        for n in range(len(TILES)):
+            done = 2 * n + 3
+            if TILES[n][2] == "q":
+                jobs[done + 1] = [(n, 0)]
+                jobs[done + 2] = [(n, 1)]
+            elif TILES[n][2] == "k":
+                jobs[done + 1] = [(n, 0), (n, 1)]
+            else:
+                jobs[done] = [(n, 0), (n, 1)]
 
-        def has_rope(n):
-            return n is not None and TILES[n][2] != "v"
+        def rope_jobs(s):
+            return [j for j in jobs.get(s, []) if TILES[j[0]][2] != "v"]
 
-        def is_v(n):
-            return n is not None and TILES[n][2] == "v"
-
-        for s in range(n_units + 4):
+        last_step = max(jobs) + 3
+        for s in range(last_step + 1):
             if s >= 1:
                 for r in range(2):
                     if next_load < len(loads):
                         load(next_load)
                         next_load += 1
+            for (n, half) in rope_jobs(s - 3):
+                rope_out(n, half)
+                store(n, half)
+            for (n, half) in jobs.get(s - 1, []):
+                bias_plain(n, half)
+                if TILES[n][2] == "v":
+                    store(n, half)
+                else:
+                    products(n, half)
             if s < n_units:
                 widen(s)
             if 0 <= s - 1 < n_units:
                 scalar_interleave(s - 1)
                 vector_interleave(s - 1)
-            if s == 0:
+            if s == 1:
                 table_sources()
+                rope_bias_sources()
             if s in (1, 2):
                 hidden_half(s - 1)
             if s == 3:
@@ -449,34 +478,16 @@ def tile_selfattention_pa_kernel(
                     hidden_quantise(g)
             if s == 2:
                 table_transposes()
-            n0, n1, n2, n3 = tile_at(s, 0), tile_at(s, 1), tile_at(s, 2), tile_at(s, 3)
-            if has_rope(n3):
-                for half in range(2):
-                    rope_out(n3, half)
-                    store(n3, half)
-            if has_rope(n1):
-                products(n1, 0)
-            if has_rope(n2):
-                bias_plain(n2, 0)
-            if is_v(n1):
-                bias_plain(n1, 0)
-                store(n1, 0)
+                rope_bias_transposes()
             if 0 <= s - 2 < n_units:
                 quantise(s - 2)
-            if has_rope(n1):
-                products(n1, 1)
-            if has_rope(n2):
-                bias_plain(n2, 1)
-            if is_v(n1):
-                bias_plain(n1, 1)
-                store(n1, 1)
-            if has_rope(n2):
-                rope_transposes(n2)
-            if has_rope(n0):
-                mx_rope(n0)
-            if has_rope(n1):
-                mx_plain(n1)
-            if is_v(n0):
-                mx_plain(n0)
+            for (n, half) in rope_jobs(s):
+                mx_rope(n, half)
+                mx_plain(n, half)
+            for (n, half) in rope_jobs(s - 2):
+                rope_transposes(n, half)
+            for (n, half) in jobs.get(s, []):
+                if TILES[n][2] == "v":
+                    mx_plain(n, half)
             if s < n_units:
                 pe_interleave(s)

@@ -31,12 +31,12 @@ KCOLS = 256
 TILES = [
     (0, 512, "q", (2, 3), (0, 0), (4, 4)),
     (512, 512, "q", (3, 3), (0, 0), (3, 3)),
-    (1024, 512, "q", (4, 3), (0, 0), (2, 2)),
-    (1536, 512, "q", (4, 3), (0, 0), (2, 2)),
-    (2048, 512, "q", (4, 3), (0, 0), (2, 2)),
-    (2560, 512, "q", (4, 3), (0, 0), (2, 2)),
-    (3072, 512, "q", (4, 3), (0, 0), (2, 2)),
-    (3584, 512, "q", (4, 3), (0, 0), (2, 2)),
+    (1024, 512, "q", (4, 3), (0, 0), (1, 0)),
+    (1536, 512, "q", (4, 3), (0, 0), (1, 0)),
+    (2048, 512, "q", (4, 3), (0, 0), (1, 0)),
+    (2560, 512, "q", (4, 3), (0, 0), (1, 0)),
+    (3072, 512, "q", (4, 3), (0, 0), (1, 0)),
+    (3584, 512, "q", (4, 3), (0, 0), (1, 0)),
     (4096, 256, "k", (2, 2), (0, 0), (1, 1)),
     (4352, 256, "v", (0, 0), (2, 2), (0, 0)),
 ]

@@ -29,14 +29,14 @@ QCOLS = 4096
 KCOLS = 256
 
 TILES = [
-    (0, 512, "q", (2, 3), (0, 0), (4, 4)),
-    (512, 512, "q", (3, 3), (0, 0), (3, 3)),
-    (1024, 512, "q", (4, 3), (0, 0), (1, 0)),
-    (1536, 512, "q", (4, 3), (0, 0), (1, 0)),
-    (2048, 512, "q", (4, 3), (0, 0), (1, 0)),
-    (2560, 512, "q", (4, 3), (0, 0), (1, 0)),
-    (3072, 512, "q", (4, 3), (0, 0), (1, 0)),
-    (3584, 512, "q", (4, 3), (0, 0), (1, 0)),
+    (0, 512, "q", (2, 2), (0, 0), (4, 4)),
+    (512, 512, "q", (2, 2), (0, 0), (3, 3)),
+    (1024, 512, "q", (2, 2), (0, 0), (1, 0)),
+    (1536, 512, "q", (2, 2), (0, 0), (1, 0)),
+    (2048, 512, "q", (2, 2), (0, 0), (1, 0)),
+    (2560, 512, "q", (2, 2), (0, 0), (1, 0)),
+    (3072, 512, "q", (2, 2), (0, 0), (1, 0)),
+    (3584, 512, "q", (2, 2), (0, 0), (1, 0)),
     (4096, 256, "k", (2, 2), (0, 0), (1, 1)),
     (4352, 256, "v", (0, 0), (2, 2), (0, 0)),
 ]

@@ -29,16 +29,16 @@ QCOLS = 4096
 KCOLS = 256
 
 TILES = [
-    (0, 512, "q", (2, 2), (0, 0), (4, 4)),
-    (512, 512, "q", (2, 2), (0, 0), (3, 3)),
-    (1024, 512, "q", (2, 2), (0, 0), (1, 0)),
-    (1536, 512, "q", (2, 2), (0, 0), (1, 0)),
-    (2048, 512, "q", (2, 2), (0, 0), (1, 0)),
-    (2560, 512, "q", (2, 2), (0, 0), (1, 0)),
-    (3072, 512, "q", (2, 2), (0, 0), (1, 0)),
-    (3584, 512, "q", (2, 2), (0, 0), (1, 0)),
-    (4096, 256, "k", (2, 2), (0, 0), (1, 1)),
-    (4352, 256, "v", (0, 0), (2, 2), (0, 0)),
+    (0, 512, "q", (2, 2), (0, 0), (4, 4), (0, 0)),
+    (512, 512, "q", (2, 2), (0, 0), (3, 3), (0, 0)),
+    (1024, 512, "q", (2, 2), (0, 0), (1, 0), (0, 0)),
+    (1536, 512, "q", (2, 2), (0, 0), (1, 0), (0, 0)),
+    (2048, 512, "q", (2, 2), (0, 0), (1, 0), (0, 0)),
+    (2560, 512, "q", (2, 2), (0, 0), (1, 0), (0, 0)),
+    (3072, 512, "q", (2, 2), (0, 0), (1, 0), (0, 0)),
+    (3584, 512, "q", (2, 2), (0, 0), (1, 0), (0, 0)),
+    (4096, 256, "k", (0, 0), (2, 2), (0, 0), (0, 0)),
+    (4352, 256, "v", (0, 0), (2, 2), (0, 0), (0, 0)),
 ]
 LOAD_COLS = 512
 LOADS_AHEAD = 12
@@ -51,13 +51,15 @@ def tile_selfattention_pa_kernel(
     nc = tc.nc
     with ExitStack() as ctx:
         const = ctx.enter_context(tc.tile_pool(name="const", bufs=1))
-        wbp = ctx.enter_context(tc.tile_pool(name="wbp", bufs=16))
+        wbp = ctx.enter_context(tc.tile_pool(name="wbp", bufs=14))
         plp = ctx.enter_context(tc.tile_pool(name="plp", bufs=4))
         grp = ctx.enter_context(tc.tile_pool(name="grp", bufs=4))
         cdp = ctx.enter_context(tc.tile_pool(name="cdp", bufs=3))
         hid = ctx.enter_context(tc.tile_pool(name="hid", bufs=4))
         obp = ctx.enter_context(tc.tile_pool(name="obp", bufs=6))
         mp = ctx.enter_context(tc.tile_pool(name="mp", bufs=4))
+        trg = ctx.enter_context(tc.tile_pool(name="trg", bufs=4))
+        tmp = ctx.enter_context(tc.tile_pool(name="tmp", bufs=2))
         accp = ctx.enter_context(tc.psum_pool(name="accp", bufs=6))
         ilp = ctx.enter_context(tc.psum_pool(name="ilp", bufs=2))
         ctx.enter_context(tc.manual_schedule())
@@ -111,14 +113,14 @@ def tile_selfattention_pa_kernel(
             return v[:, :, :, 0, :, e].rearrange("p t h j -> p h j t")
 
         def plain_src(planes, gl, kind, h0, h1):
-            if kind == "v":
+            if kind != "q":
                 v = planes[:, gl, :, :].rearrange("p t (h d) -> p t h d", d=RD)
             else:
                 v = planes[:, gl, :, :].rearrange("p t (h r d) -> p t h r d", r=2, d=RD)[:, :, :, 1, :]
             return v[:, :, h0:h1, :].rearrange("p t h d -> p h d t")
 
         def rope_cols(n):
-            return 0 if TILES[n][2] == "v" else (TILES[n][1] // HD) * HJ
+            return (TILES[n][1] // HD) * HJ if TILES[n][2] == "q" else 0
 
         def pe_interleave(i):
             n, gp = units[i]
@@ -138,18 +140,6 @@ def tile_selfattention_pa_kernel(
                                 stop=True,
                             )
                         st[i][2].append((bank, gl, k))
-            elif kind == "k" and npe > 0:
-                bank = ilp.tile([P, 2, NT], BF16, name="bank")
-                for gl in range(2):
-                    for e in range(2):
-                        nc.tensor.matmul(
-                            out=bank[:, gl, e * 256 : (e + 1) * 256].rearrange("p (h j t) -> p h j t", j=HJ, t=PACK),
-                            lhsT=ident_b[:],
-                            rhs=rope_src(planes, gl, e),
-                            start=True,
-                            stop=True,
-                        )
-                st[i][2].append((bank, 0, 0))
 
         def plain_interleave(copy, i, gl, h0, h1):
             n, gp = units[i]
@@ -169,17 +159,11 @@ def tile_selfattention_pa_kernel(
             w, kind, nsc = TILES[n][1], TILES[n][2], TILES[n][4][gp]
             grouped = st[i][1]
             for (bank, gl, k) in st[i][2]:
-                if kind == "q":
-                    a = gl * w * PACK
-                    nc.scalar.copy(
-                        out=grouped[:, a : a + k * NT].bitcast(F32),
-                        in_=bank[:, 0:k, :].rearrange("p h c -> p (h c)").bitcast(F32),
-                    )
-                else:
-                    nc.scalar.copy(
-                        out=grouped[:].bitcast(F32).rearrange("p (g c) -> p g c", g=2)[:, :, 0 : NT // 2],
-                        in_=bank[:].rearrange("p g c -> p (g c)").bitcast(F32).rearrange("p (g c) -> p g c", g=2),
-                    )
+                a = gl * w * PACK
+                nc.scalar.copy(
+                    out=grouped[:, a : a + k * NT].bitcast(F32),
+                    in_=bank[:, 0:k, :].rearrange("p h c -> p (h c)").bitcast(F32),
+                )
             if nsc > 0:
                 for gl in range(2):
                     plain_interleave(nc.scalar.copy, i, gl, plain_blocks(n) - nsc, plain_blocks(n))
@@ -191,15 +175,27 @@ def tile_selfattention_pa_kernel(
             rc = rope_cols(n)
             for gl in range(2):
                 for e in range(2):
-                    on_pe = (2 * gl + e < npe) if kind == "q" else (npe > 0)
-                    if rc > 0 and not on_pe:
+                    if rc > 0 and 2 * gl + e >= npe:
                         a = gl * w * PACK + e * rc * PACK
                         nc.vector.tensor_copy(
                             out=grouped[:, a : a + rc * PACK].rearrange("p (h j t) -> p h j t", j=HJ, t=PACK),
                             in_=rope_src(planes, gl, e),
                         )
-                if plain_blocks(n) - nsc > 0:
-                    plain_interleave(nc.vector.tensor_copy, i, gl, 0, plain_blocks(n) - nsc)
+                nv = plain_blocks(n) - nsc - (TILES[n][6][gp] if gl == 1 else 0)
+                if nv > 0:
+                    plain_interleave(nc.vector.tensor_copy, i, gl, 0, nv)
+
+        def gpsimd_copy(out, in_):
+            one = trg.tile([P, 1], F32, name="one")
+            nc.vector.memset(one[:], 1.0)
+            nc.gpsimd.tensor_scalar(out=out, in0=in_, scalar1=one[:, 0:1], scalar2=0.0, op0=MULT, op1=ADD)
+
+        def gpsimd_interleave(i):
+            n, gp = units[i]
+            ng = TILES[n][6][gp]
+            if ng > 0:
+                hi = plain_blocks(n) - TILES[n][4][gp]
+                plain_interleave(gpsimd_copy, i, 1, hi - ng, hi)
 
         def quantise(i):
             n, gp = units[i]
@@ -290,7 +286,7 @@ def tile_selfattention_pa_kernel(
             col, w, kind = TILES[n][0], TILES[n][1], TILES[n][2]
             xb = obp.tile([P, 2, w], F32, name="xb")
             acc = plain_acc[(n, half)]
-            if kind == "v":
+            if kind != "q":
                 nc.vector.tensor_tensor(
                     out=xb[:], in0=acc[:], in1=bias_sb[:, col : col + w].unsqueeze(1).to_broadcast([P, 2, w]), op=ADD
                 )
@@ -306,6 +302,28 @@ def tile_selfattention_pa_kernel(
                     op=ADD,
                 )
             xbs[(n, half)] = xb
+
+        def k_products(n, half):
+            nh = TILES[n][1] // HD
+            m12 = tmp.tile([P, 2, nh, 2, RD], F32, name="m12")
+            xr = xbs[(n, half)][:].rearrange("p t (h d) -> p t h d", d=HD)[:, :, :, 0:RD]
+            nc.vector.tensor_tensor(
+                out=m12[:],
+                in0=xr.unsqueeze(3).to_broadcast([P, 2, nh, 2, RD]),
+                in1=cs_tab[:, 2 * half : 2 * half + 2, :, :].unsqueeze(2).to_broadcast([P, 2, nh, 2, RD]),
+                op=MULT,
+            )
+            prods[(n, half)] = m12
+
+        def k_sum(n, half):
+            m12 = prods[(n, half)]
+            xr = xbs[(n, half)][:].rearrange("p t (h d) -> p t h d", d=HD)[:, :, :, 0:RD]
+            nc.vector.tensor_tensor(
+                out=xr.rearrange("p t h (j e) -> p t h j e", e=2),
+                in0=m12[:, :, :, 0, :].rearrange("p t h (j e) -> p t h j e", e=2),
+                in1=m12[:, :, :, 1, :].rearrange("p t h (j e) -> p t h j e", e=2)[:, :, :, :, ::-1],
+                op=ADD,
+            )
 
         def rope_out(n, half):
             rc = rope_cols(n)
@@ -333,7 +351,7 @@ def tile_selfattention_pa_kernel(
         cos_sb = const.tile([P, TT, RD], BF16, name="cos_sb")
         sin_sb = const.tile([P, TT, RD], BF16, name="sin_sb")
         bias_sb = const.tile([P, OUT], BF16, name="bias_sb")
-        n_rope = QCOLS // NT + 1
+        n_rope = QCOLS // NT
         b_rows = const.tile([P, NT], BF16, name="b_rows")
         nc.gpsimd.memset(b_rows[:], 0.0)
         for item in HEAD:
@@ -346,11 +364,7 @@ def tile_selfattention_pa_kernel(
                 nc.sync.dma_start(out=cos_sb[:], in_=cos.rearrange("(t p) d -> p t d", p=P))
                 nc.sync.dma_start(out=sin_sb[:], in_=sin.rearrange("(t p) d -> p t d", p=P))
             elif item[0] == "r":
-                nc.sync.dma_start(out=b_rows[0 : n_rope - 1, :], in_=b_qkv[0:QCOLS].rearrange("(n c) -> n c", c=NT))
-                nc.sync.dma_start(
-                    out=b_rows[n_rope - 1 : n_rope, 0:KCOLS],
-                    in_=b_qkv[QCOLS : QCOLS + KCOLS].rearrange("(n c) -> n c", c=KCOLS),
-                )
+                nc.sync.dma_start(out=b_rows[0:n_rope, :], in_=b_qkv[0:QCOLS].rearrange("(n c) -> n c", c=NT))
             else:
                 nc.sync.dma_start(out=bias_sb[:], in_=b_qkv.partition_broadcast(P))
         next_load = LOADS_AHEAD
@@ -421,6 +435,18 @@ def tile_selfattention_pa_kernel(
                 nc.tensor.transpose(pt[:, e, :], b_cols[:, e, :, :].rearrange("p h j -> p (h j)"), ident_b[:])
             nc.scalar.copy(out=bias_r[:].rearrange("p n e -> p e n"), in_=pt[:, :, 0:n_rope])
 
+        cs_tab = const.tile([P, TT, 2, RD], F32, name="cs_tab")
+
+        def k_tables():
+            nc.vector.tensor_copy(
+                out=cs_tab[:, :, 0, :].rearrange("p t (j e) -> p t j e", e=2),
+                in_=cos_sb[:].rearrange("p t (e j) -> p t j e", e=2),
+            )
+            sv = cs_tab[:, :, 1, :].rearrange("p t (j e) -> p t j e", e=2)
+            sn = sin_sb[:].rearrange("p t (e j) -> p t j e", e=2)
+            nc.vector.tensor_scalar(out=sv[:, :, :, 1:2], in0=sn[:, :, :, 0:1], scalar1=-1.0, scalar2=None, op0=MULT)
+            nc.vector.tensor_copy(out=sv[:, :, :, 0:1], in_=sn[:, :, :, 1:2])
+
         def table_transposes():
             for e in range(2):
                 pt = accp.tile([P, 2, T], BF16, name="acc")
@@ -437,15 +463,13 @@ def tile_selfattention_pa_kernel(
         for n in range(len(TILES)):
             done = 2 * n + 3
             if TILES[n][2] == "q":
-                jobs[done + 1] = [(n, 0)]
-                jobs[done + 2] = [(n, 1)]
-            elif TILES[n][2] == "k":
-                jobs[done + 1] = [(n, 0), (n, 1)]
+                jobs[done + 1] = jobs.get(done + 1, []) + [(n, 0)]
+                jobs[done + 2] = jobs.get(done + 2, []) + [(n, 1)]
             else:
-                jobs[done] = [(n, 0), (n, 1)]
+                jobs[done] = jobs.get(done, []) + [(n, 0), (n, 1)]
 
-        def rope_jobs(s):
-            return [j for j in jobs.get(s, []) if TILES[j[0]][2] != "v"]
+        def jobs_of(s, kinds):
+            return [j for j in jobs.get(s, []) if TILES[j[0]][2] in kinds]
 
         last_step = max(jobs) + 3
         for s in range(last_step + 1):
@@ -454,20 +478,28 @@ def tile_selfattention_pa_kernel(
                     if next_load < len(loads):
                         load(next_load)
                         next_load += 1
-            for (n, half) in rope_jobs(s - 3):
+            for (n, half) in jobs_of(s - 3, "q"):
                 rope_out(n, half)
                 store(n, half)
-            for (n, half) in jobs.get(s - 1, []):
+            if 0 <= s - 1 < n_units:
+                gpsimd_interleave(s - 1)
+            for (n, half) in jobs_of(s - 1, "q"):
                 bias_plain(n, half)
-                if TILES[n][2] == "v":
-                    store(n, half)
-                else:
-                    products(n, half)
+                products(n, half)
+            for (n, half) in jobs_of(s - 1, "kv"):
+                bias_plain(n, half)
+            for (n, half) in jobs_of(s - 1, "v"):
+                store(n, half)
+            for (n, half) in jobs_of(s - 1, "k"):
+                k_products(n, half)
             if s < n_units:
                 widen(s)
             if 0 <= s - 1 < n_units:
                 scalar_interleave(s - 1)
                 vector_interleave(s - 1)
+            for (n, half) in jobs_of(s - 1, "k"):
+                k_sum(n, half)
+                store(n, half)
             if s == 1:
                 table_sources()
                 rope_bias_sources()
@@ -476,18 +508,18 @@ def tile_selfattention_pa_kernel(
             if s == 3:
                 for g in range(G):
                     hidden_quantise(g)
+                k_tables()
             if s == 2:
                 table_transposes()
                 rope_bias_transposes()
             if 0 <= s - 2 < n_units:
                 quantise(s - 2)
-            for (n, half) in rope_jobs(s):
+            for (n, half) in jobs_of(s, "q"):
                 mx_rope(n, half)
                 mx_plain(n, half)
-            for (n, half) in rope_jobs(s - 2):
+            for (n, half) in jobs_of(s - 2, "q"):
                 rope_transposes(n, half)
-            for (n, half) in jobs.get(s, []):
-                if TILES[n][2] == "v":
-                    mx_plain(n, half)
+            for (n, half) in jobs_of(s, "kv"):
+                mx_plain(n, half)
             if s < n_units:
                 pe_interleave(s)

@@ -31,12 +31,12 @@ KCOLS = 256
 TILES = [
     (0, 512, "q", (2, 2), (0, 0), (4, 4), (0, 0)),
     (512, 512, "q", (2, 2), (0, 0), (3, 3), (0, 0)),
-    (1024, 512, "q", (2, 2), (0, 0), (1, 0), (0, 0)),
-    (1536, 512, "q", (2, 2), (0, 0), (1, 0), (0, 0)),
-    (2048, 512, "q", (2, 2), (0, 0), (1, 0), (0, 0)),
-    (2560, 512, "q", (2, 2), (0, 0), (1, 0), (0, 0)),
-    (3072, 512, "q", (2, 2), (0, 0), (1, 0), (0, 0)),
-    (3584, 512, "q", (2, 2), (0, 0), (1, 0), (0, 0)),
+    (1024, 512, "q", (2, 2), (0, 0), (2, 1), (4, 4)),
+    (1536, 512, "q", (2, 2), (0, 0), (2, 1), (4, 4)),
+    (2048, 512, "q", (2, 2), (0, 0), (2, 1), (4, 4)),
+    (2560, 512, "q", (2, 2), (0, 0), (2, 1), (4, 4)),
+    (3072, 512, "q", (2, 2), (0, 0), (2, 1), (4, 4)),
+    (3584, 512, "q", (2, 2), (0, 0), (2, 1), (4, 4)),
     (4096, 256, "k", (0, 0), (2, 2), (0, 0), (0, 0)),
     (4352, 256, "v", (0, 0), (2, 2), (0, 0), (0, 0)),
 ]

@@ -31,12 +31,12 @@ KCOLS = 256
 TILES = [
     (0, 512, "q", (2, 2), (0, 0), (4, 4), (0, 0)),
     (512, 512, "q", (2, 2), (0, 0), (3, 3), (0, 0)),
-    (1024, 512, "q", (2, 2), (0, 0), (2, 1), (4, 4)),
-    (1536, 512, "q", (2, 2), (0, 0), (2, 1), (4, 4)),
-    (2048, 512, "q", (2, 2), (0, 0), (2, 1), (4, 4)),
-    (2560, 512, "q", (2, 2), (0, 0), (2, 1), (4, 4)),
-    (3072, 512, "q", (2, 2), (0, 0), (2, 1), (4, 4)),
-    (3584, 512, "q", (2, 2), (0, 0), (2, 1), (4, 4)),
+    (1024, 512, "q", (2, 2), (0, 0), (1, 1), (4, 4)),
+    (1536, 512, "q", (2, 2), (0, 0), (1, 1), (4, 4)),
+    (2048, 512, "q", (2, 2), (0, 0), (1, 1), (4, 4)),
+    (2560, 512, "q", (2, 2), (0, 0), (1, 1), (4, 4)),
+    (3072, 512, "q", (2, 2), (0, 0), (1, 1), (4, 4)),
+    (3584, 512, "q", (2, 2), (0, 0), (1, 1), (4, 4)),
     (4096, 256, "k", (0, 0), (2, 2), (0, 0), (0, 0)),
     (4352, 256, "v", (0, 0), (2, 2), (0, 0), (0, 0)),
 ]

@@ -518,7 +518,9 @@ def tile_selfattention_pa_kernel(
                 mx_rope(n, half)
                 mx_plain(n, half)
             for (n, half) in jobs_of(s - 2, "q"):
-                rope_transposes(n, half)
+                if half == 0:
+                    rope_transposes(n, 0)
+                    rope_transposes(n, 1)
             for (n, half) in jobs_of(s, "kv"):
                 mx_plain(n, half)
             if s < n_units:

@@ -29,16 +29,16 @@ QCOLS = 4096
 KCOLS = 256
 
 TILES = [
-    (0, 512, "q", (2, 2), (0, 0), (4, 4), (0, 0)),
-    (512, 512, "q", (2, 2), (0, 0), (3, 3), (0, 0)),
-    (1024, 512, "q", (2, 2), (0, 0), (1, 1), (4, 4)),
-    (1536, 512, "q", (2, 2), (0, 0), (1, 1), (4, 4)),
-    (2048, 512, "q", (2, 2), (0, 0), (1, 1), (4, 4)),
-    (2560, 512, "q", (2, 2), (0, 0), (1, 1), (4, 4)),
-    (3072, 512, "q", (2, 2), (0, 0), (1, 1), (4, 4)),
-    (3584, 512, "q", (2, 2), (0, 0), (1, 1), (4, 4)),
-    (4096, 256, "k", (0, 0), (2, 2), (0, 0), (0, 0)),
-    (4352, 256, "v", (0, 0), (2, 2), (0, 0), (0, 0)),
+    (0, 512, "q", (1, 1), (0, 0), (4, 4), (0, 0)),
+    (512, 512, "q", (1, 1), (0, 0), (3, 3), (0, 0)),
+    (1024, 512, "q", (1, 1), (0, 0), (1, 1), (1, 1)),
+    (1536, 512, "q", (1, 1), (0, 0), (1, 1), (1, 1)),
+    (2048, 512, "q", (1, 1), (0, 0), (1, 1), (1, 1)),
+    (2560, 512, "q", (1, 1), (0, 0), (1, 1), (1, 1)),
+    (3072, 512, "q", (1, 1), (0, 0), (1, 1), (1, 1)),
+    (3584, 512, "q", (1, 1), (0, 0), (1, 1), (1, 1)),
+    (4096, 256, "k", (0, 0), (1, 1), (0, 0), (0, 0)),
+    (4352, 256, "v", (0, 0), (1, 0), (0, 0), (0, 0)),
 ]
 LOAD_COLS = 512
 LOADS_AHEAD = 12
@@ -108,82 +108,60 @@ def tile_selfattention_pa_kernel(
                         scale=wscale[:, g, t : t + 1],
                     )
 
-        def rope_src(planes, gl, e):
-            v = planes[:, gl, :, :].rearrange("p t (h r j e) -> p t h r j e", r=2, j=HJ, e=2)
-            return v[:, :, :, 0, :, e].rearrange("p t h j -> p h j t")
-
-        def plain_src(planes, gl, kind, h0, h1):
-            if kind != "q":
-                v = planes[:, gl, :, :].rearrange("p t (h d) -> p t h d", d=RD)
+        def interleave(copy, i, h0, h1):
+            n = units[i][0]
+            w = TILES[n][1]
+            planes, grouped = st[i][0], st[i][1]
+            if TILES[n][2] != "q":
+                for gl in range(h0, h1):
+                    copy(
+                        out=grouped[:, gl * w * PACK : (gl + 1) * w * PACK].rearrange("p (c t) -> p c t", t=PACK),
+                        in_=planes[:, gl, :, :].rearrange("p t c -> p c t"),
+                    )
             else:
-                v = planes[:, gl, :, :].rearrange("p t (h r d) -> p t h r d", r=2, d=RD)[:, :, :, 1, :]
-            return v[:, :, h0:h1, :].rearrange("p t h d -> p h d t")
+                for gl in range(2):
+                    r0, r1 = max(h0 - 2 * gl, 0), min(h1 - 2 * gl, 2)
+                    if r0 < r1:
+                        hw = w // 2 * PACK
+                        copy(
+                            out=grouped[:, (2 * gl + r0) * hw : (2 * gl + r1) * hw].rearrange(
+                                "p (r h d t) -> p r h d t", r=r1 - r0, d=RD, t=PACK
+                            ),
+                            in_=planes[:, gl, :, :]
+                            .rearrange("p t (h r d) -> p t h r d", r=2, d=RD)[:, :, :, r0:r1, :]
+                            .rearrange("p t h r d -> p r h d t"),
+                        )
 
         def rope_cols(n):
-            return (TILES[n][1] // HD) * HJ if TILES[n][2] == "q" else 0
+            return TILES[n][1] // 2 if TILES[n][2] == "q" else 0
 
         def pe_interleave(i):
             n, gp = units[i]
-            kind, npe = TILES[n][2], TILES[n][3][gp]
-            planes = st[i][0]
-            if kind == "q":
-                for gl in range(2):
-                    k = min(2, npe - 2 * gl)
-                    if k > 0:
-                        bank = ilp.tile([P, 2, NT], BF16, name="bank")
-                        for e in range(k):
-                            nc.tensor.matmul(
-                                out=bank[:, e, :].rearrange("p (h j t) -> p h j t", j=HJ, t=PACK),
-                                lhsT=ident_b[:],
-                                rhs=rope_src(planes, gl, e),
-                                start=True,
-                                stop=True,
-                            )
-                        st[i][2].append((bank, gl, k))
+            if TILES[n][3][gp] > 0:
+                src = st[i][0][:, 0, :, :].rearrange("p t (b h r d) -> p t b h r d", b=2, r=2, d=RD)
+                bank = ilp.tile([P, 2, NT], BF16, name="bank")
+                for b in range(2):
+                    nc.tensor.matmul(
+                        out=bank[:, b, :].rearrange("p (h d t) -> p h d t", d=RD, t=PACK),
+                        lhsT=ident_b[:],
+                        rhs=src[:, :, b, :, 0, :].rearrange("p t h d -> p h d t"),
+                        start=True,
+                        stop=True,
+                    )
+                st[i][2].append(bank)
 
-        def plain_interleave(copy, i, gl, h0, h1):
-            n, gp = units[i]
-            w, kind = TILES[n][1], TILES[n][2]
-            planes, grouped = st[i][0], st[i][1]
-            a = gl * w * PACK + 2 * rope_cols(n) * PACK
-            copy(
-                out=grouped[:, a + h0 * RD * PACK : a + h1 * RD * PACK].rearrange("p (h d t) -> p h d t", d=RD, t=PACK),
-                in_=plain_src(planes, gl, kind, h0, h1),
-            )
-
-        def plain_blocks(n):
-            return (TILES[n][1] - 2 * rope_cols(n)) // RD
+        def halves_of(n):
+            return 4 if TILES[n][2] == "q" else 2
 
         def scalar_interleave(i):
             n, gp = units[i]
-            w, kind, nsc = TILES[n][1], TILES[n][2], TILES[n][4][gp]
             grouped = st[i][1]
-            for (bank, gl, k) in st[i][2]:
-                a = gl * w * PACK
+            for bank in st[i][2]:
                 nc.scalar.copy(
-                    out=grouped[:, a : a + k * NT].bitcast(F32),
-                    in_=bank[:, 0:k, :].rearrange("p h c -> p (h c)").bitcast(F32),
+                    out=grouped[:, 0 : 2 * NT].bitcast(F32),
+                    in_=bank[:].rearrange("p k c -> p (k c)").bitcast(F32),
                 )
-            if nsc > 0:
-                for gl in range(2):
-                    plain_interleave(nc.scalar.copy, i, gl, plain_blocks(n) - nsc, plain_blocks(n))
-
-        def vector_interleave(i):
-            n, gp = units[i]
-            w, kind, npe, nsc = TILES[n][1], TILES[n][2], TILES[n][3][gp], TILES[n][4][gp]
-            planes, grouped = st[i][0], st[i][1]
-            rc = rope_cols(n)
-            for gl in range(2):
-                for e in range(2):
-                    if rc > 0 and 2 * gl + e >= npe:
-                        a = gl * w * PACK + e * rc * PACK
-                        nc.vector.tensor_copy(
-                            out=grouped[:, a : a + rc * PACK].rearrange("p (h j t) -> p h j t", j=HJ, t=PACK),
-                            in_=rope_src(planes, gl, e),
-                        )
-                nv = plain_blocks(n) - nsc - (TILES[n][6][gp] if gl == 1 else 0)
-                if nv > 0:
-                    plain_interleave(nc.vector.tensor_copy, i, gl, 0, nv)
+            interleave(nc.scalar.copy, i, halves_of(n) - TILES[n][4][gp], halves_of(n))
 
         def gpsimd_copy(out, in_):
             one = trg.tile([P, 1], F32, name="one")
@@ -192,10 +170,11 @@ def tile_selfattention_pa_kernel(
 
         def gpsimd_interleave(i):
             n, gp = units[i]
-            ng = TILES[n][6][gp]
-            if ng > 0:
-                hi = plain_blocks(n) - TILES[n][4][gp]
-                plain_interleave(gpsimd_copy, i, 1, hi - ng, hi)
+            interleave(gpsimd_copy, i, TILES[n][3][gp], TILES[n][3][gp] + TILES[n][6][gp])
+
+        def vector_interleave(i):
+            n, gp = units[i]
+            interleave(nc.vector.tensor_copy, i, TILES[n][3][gp] + TILES[n][6][gp], halves_of(n) - TILES[n][4][gp])
 
         def quantise(i):
             n, gp = units[i]
@@ -220,14 +199,13 @@ def tile_selfattention_pa_kernel(
 
         def mx_rope(n, half):
             wcod, wsc = codes[n]
-            rc = rope_cols(n)
             acc = accp.tile([P, 2, HT], F32, name="acc")
-            for e in range(2):
+            for b in range(2):
                 for g in range(G):
                     nc.tensor.matmul_mx(
-                        out=acc[:, e, :],
-                        lhsT=wcod[:, g, e * rc : e * rc + P].bitcast(FP8X4),
-                        lhsT_scale=wsc[:, g, e * rc : e * rc + P],
+                        out=acc[:, b, :],
+                        lhsT=wcod[:, g, b * P : (b + 1) * P].bitcast(FP8X4),
+                        lhsT_scale=wsc[:, g, b * P : (b + 1) * P],
                         rhs=xc[:, g, half * HT : (half + 1) * HT].bitcast(FP8X4),
                         rhs_scale=xs[:, g, half * HT : (half + 1) * HT],
                         start=(g == 0),
@@ -237,7 +215,7 @@ def tile_selfattention_pa_kernel(
 
         def mx_plain(n, half):
             wcod, wsc = codes[n]
-            p0 = 2 * rope_cols(n)
+            p0 = rope_cols(n)
             pw = TILES[n][1] - p0
             acc = accp.tile([P, 2, pw], F32, name="acc")
             for k in range(2):
@@ -254,14 +232,40 @@ def tile_selfattention_pa_kernel(
                     )
             plain_acc[(n, half)] = acc
 
+        def mx_open(n, tt, pool, tag):
+            acc = pool.tile([P, TILES[n][1]], F32, name=tag)
+            plain_acc[(n, tt)] = acc
+            mx_passes(n, tt, 0, G // 2)
+
+        def mx_passes(n, tt, g0, g1):
+            wcod, wsc = codes[n]
+            for g in range(g0, g1):
+                nc.tensor.matmul_mx(
+                    out=plain_acc[(n, tt)][:],
+                    lhsT=xc[:, g, tt * P : (tt + 1) * P].bitcast(FP8X4),
+                    lhsT_scale=xs[:, g, tt * P : (tt + 1) * P],
+                    rhs=wcod[:, g, :].bitcast(FP8X4),
+                    rhs_scale=wsc[:, g, :],
+                    start=(g == 0),
+                    stop=(g == G - 1),
+                )
+
+        def bias_tile(n, tt):
+            col, w = TILES[n][0], TILES[n][1]
+            if tt % 2 == 0:
+                xbs[(n, tt // 2)] = obp.tile([P, 2, w], F32, name="xb")
+            nc.vector.tensor_tensor(
+                out=xbs[(n, tt // 2)][:, tt % 2, :], in0=plain_acc[(n, tt)][:], in1=bias_sb[:, col : col + w], op=ADD
+            )
+
         def products(n, half):
             m = mp.tile([P, 2, 2, HT], F32, name="m")
-            for e in range(2):
+            for b in range(2):
                 nc.vector.scalar_tensor_tensor(
-                    out=m[:, e, :, :],
-                    in0=rope_acc[(n, half)][:, e, :].unsqueeze(1).to_broadcast([P, 2, HT]),
-                    scalar=bias_r[:, n, e : e + 1],
-                    in1=tabs[e][:, :, half * HT : (half + 1) * HT],
+                    out=m[:, b, :, :],
+                    in0=rope_acc[(n, half)][:, b, :].unsqueeze(1).to_broadcast([P, 2, HT]),
+                    scalar=bias_r[:, n, b : b + 1],
+                    in1=tabs[:, :, half * HT : (half + 1) * HT],
                     op0=ADD,
                     op1=MULT,
                 )
@@ -269,16 +273,16 @@ def tile_selfattention_pa_kernel(
 
         def rope_transposes(n, half):
             y = accp.tile([P, 2, 2, P], F32, name="acc")
-            for f in range(2):
-                for tl in range(2):
-                    for e in range(2):
+            for tl in range(2):
+                for b in range(2):
+                    for f in range(2):
                         nc.tensor.matmul(
-                            out=y[:, f, tl, :],
-                            lhsT=prods[(n, half)][:, e, f, tl * P : (tl + 1) * P],
-                            rhs=ident_f[:],
+                            out=y[:, tl, b, :],
+                            lhsT=prods[(n, half)][:, b, f, tl * P : (tl + 1) * P],
+                            rhs=(ident_f[:] if f == 0 else swap_f[:]),
                             is_transpose=True,
-                            start=(e == 0),
-                            stop=(e == 1),
+                            start=(f == 0),
+                            stop=(f == 1),
                         )
             ybanks[(n, half)] = y
 
@@ -326,12 +330,9 @@ def tile_selfattention_pa_kernel(
             )
 
         def rope_out(n, half):
-            rc = rope_cols(n)
             nc.scalar.copy(
-                out=xbs[(n, half)][:]
-                .rearrange("p t (h d) -> p t h d", d=HD)[:, :, :, 0:RD]
-                .rearrange("p t h (j f) -> p t h j f", f=2),
-                in_=ybanks[(n, half)][:, :, :, 0:rc].rearrange("p f t (h j) -> p t h j f", j=HJ),
+                out=xbs[(n, half)][:].rearrange("p t (h d) -> p t h d", d=HD)[:, :, :, 0:RD],
+                in_=ybanks[(n, half)][:].rearrange("p t b (h d) -> p t (b h) d", d=RD),
             )
 
         def store(n, half):
@@ -377,12 +378,18 @@ def tile_selfattention_pa_kernel(
         make_identity(nc, ident_f[:])
         ident_b = const.tile([P, P], BF16, name="ident_b")
         make_identity(nc, ident_b[:])
+        swap_f = const.tile([P, P], F32, name="swap_f")
+        for e in range(2):
+            nc.vector.tensor_copy(
+                out=swap_f[:].rearrange("p (j e) -> p j e", e=2)[:, :, e : e + 1],
+                in_=ident_f[:].rearrange("p (j e) -> p j e", e=2)[:, :, 1 - e : 2 - e],
+            )
 
 
         xc = const.tile([P, G, T], U32, name="xc", align_bytes=64)
         xs = const.tile([P, G, T], U8, name="xs", align_bytes=64)
-        tab_src = const.tile([P, TT, 4, 4, HJ], BF16, name="tab_src")
-        tabs = [const.tile([P, 2, T], BF16, name="tab_even"), const.tile([P, 2, T], BF16, name="tab_odd")]
+        tab_src = const.tile([P, TT, 2, 2, RD], BF16, name="tab_src")
+        tabs = const.tile([P, 2, T], BF16, name="tabs")
         xgs = {}
 
         def hidden_half(th):
@@ -411,29 +418,29 @@ def tile_selfattention_pa_kernel(
             )
 
         def table_sources():
-            for k, (src, lo) in enumerate(((cos_sb, 0), (sin_sb, HJ), (sin_sb, 0), (cos_sb, HJ))):
+            for f, e, src, lo in ((0, 0, cos_sb, 0), (0, 1, cos_sb, HJ), (1, 0, sin_sb, HJ), (1, 1, sin_sb, 0)):
                 nc.vector.tensor_scalar(
-                    out=tab_src[:, :, k, :, :],
-                    in0=src[:, :, lo : lo + HJ].unsqueeze(2).to_broadcast([P, TT, 4, HJ]),
-                    scalar1=(-1.0 if k == 2 else 1.0),
+                    out=tab_src[:, :, f, :, :].rearrange("p t h (j e) -> p t h j e", e=2)[:, :, :, :, e],
+                    in0=src[:, :, lo : lo + HJ].unsqueeze(2).to_broadcast([P, TT, 2, HJ]),
+                    scalar1=(-1.0 if (f, e) == (1, 1) else 1.0),
                     scalar2=None,
                     op0=MULT,
                 )
 
-        b_cols = const.tile([P, 2, 4, HJ], BF16, name="b_cols")
+        b_cols = const.tile([P, 2, 2, RD], BF16, name="b_cols")
         bias_r = const.tile([P, n_rope, 2], BF16, name="bias_r")
 
         def rope_bias_sources():
             nc.vector.tensor_copy(
                 out=b_cols[:],
-                in_=b_rows[:].rearrange("p (h r j e) -> p r e h j", r=2, j=HJ, e=2)[:, 0],
+                in_=b_rows[:].rearrange("p (b h r d) -> p b h r d", b=2, h=2, r=2)[:, :, :, 0, :],
             )
 
         def rope_bias_transposes():
             pt = accp.tile([P, 2, P], BF16, name="acc")
-            for e in range(2):
-                nc.tensor.transpose(pt[:, e, :], b_cols[:, e, :, :].rearrange("p h j -> p (h j)"), ident_b[:])
-            nc.scalar.copy(out=bias_r[:].rearrange("p n e -> p e n"), in_=pt[:, :, 0:n_rope])
+            for b in range(2):
+                nc.tensor.transpose(pt[:, b, :], b_cols[:, b, :, :].rearrange("p h d -> p (h d)"), ident_b[:])
+            nc.scalar.copy(out=bias_r[:].rearrange("p n b -> p b n"), in_=pt[:, :, 0:n_rope])
 
         cs_tab = const.tile([P, TT, 2, RD], F32, name="cs_tab")
 
@@ -448,16 +455,15 @@ def tile_selfattention_pa_kernel(
             nc.vector.tensor_copy(out=sv[:, :, :, 0:1], in_=sn[:, :, :, 1:2])
 
         def table_transposes():
-            for e in range(2):
-                pt = accp.tile([P, 2, T], BF16, name="acc")
-                for f in range(2):
-                    for tt in range(TT):
-                        nc.tensor.transpose(
-                            pt[:, f, tt * P : (tt + 1) * P],
-                            tab_src[:, tt, 2 * e + f, :, :].rearrange("p h j -> p (h j)"),
-                            ident_b[:],
-                        )
-                nc.scalar.copy(out=tabs[e][:], in_=pt[:])
+            pt = accp.tile([P, 2, T], BF16, name="acc")
+            for f in range(2):
+                for tt in range(TT):
+                    nc.tensor.transpose(
+                        pt[:, f, tt * P : (tt + 1) * P],
+                        tab_src[:, tt, f, :, :].rearrange("p h d -> p (h d)"),
+                        ident_b[:],
+                    )
+            nc.scalar.copy(out=tabs[:], in_=pt[:])
 
         jobs = {}
         for n in range(len(TILES)):
@@ -471,8 +477,7 @@ def tile_selfattention_pa_kernel(
         def jobs_of(s, kinds):
             return [j for j in jobs.get(s, []) if TILES[j[0]][2] in kinds]
 
-        last_step = max(jobs) + 3
-        for s in range(last_step + 1):
+        for s in range(n_units - 1):
             if s >= 1:
                 for r in range(2):
                     if next_load < len(loads):
@@ -525,3 +530,46 @@ def tile_selfattention_pa_kernel(
                 mx_plain(n, half)
             if s < n_units:
                 pe_interleave(s)
+
+        q6, q7, kt, vt = 6, 7, 8, 9
+        u = n_units - 1
+        rope_out(q6, 0)
+        store(q6, 0)
+        bias_plain(q7, 0)
+        products(q7, 0)
+        widen(u)
+        scalar_interleave(u - 1)
+        vector_interleave(u - 1)
+        quantise(u - 2)
+        mx_rope(q7, 1)
+        mx_plain(q7, 1)
+        rope_transposes(q7, 0)
+        mx_plain(kt, 0)
+        mx_plain(kt, 1)
+        rope_out(q6, 1)
+        store(q6, 1)
+        bias_plain(q7, 1)
+        products(q7, 1)
+        vector_interleave(u)
+        quantise(u - 1)
+        rope_transposes(q7, 1)
+        for tt in range(TT):
+            mx_open(vt, tt, (ilp if tt < 2 else accp), ("bank" if tt < 2 else "acc"))
+        quantise(u)
+        for tt in range(TT):
+            mx_passes(vt, tt, G // 2, G)
+        for half in range(2):
+            bias_plain(kt, half)
+        rope_out(q7, 0)
+        store(q7, 0)
+        for half in range(2):
+            k_products(kt, half)
+        rope_out(q7, 1)
+        store(q7, 1)
+        for half in range(2):
+            k_sum(kt, half)
+            store(kt, half)
+        for tt in range(TT):
+            bias_tile(vt, tt)
+            if tt % 2 == 1:
+                store(vt, tt // 2)

@@ -25,6 +25,7 @@ NT = 512
 RD = 64
 HJ = RD // 2
 HD = 128
+NEAR = 4
 QCOLS = 4096
 KCOLS = 256
 
@@ -108,15 +109,24 @@ def tile_selfattention_pa_kernel(
                         scale=wscale[:, g, t : t + 1],
                     )
 
-        def interleave(copy, i, h0, h1):
+        def interleave(copy, i, h0, h1, near=False):
             n = units[i][0]
             w = TILES[n][1]
             planes, grouped = st[i][0], st[i][1]
             if TILES[n][2] != "q":
                 for gl in range(h0, h1):
                     copy(
-                        out=grouped[:, gl * w * PACK : (gl + 1) * w * PACK].rearrange("p (c t) -> p c t", t=PACK),
-                        in_=planes[:, gl, :, :].rearrange("p t c -> p c t"),
+                        out=grouped[:, gl * w * PACK : (gl + 1) * w * PACK].rearrange("p (c q t) -> p c t q", q=NEAR, t=PACK),
+                        in_=planes[:, gl, :, :].rearrange("p t (c q) -> p c t q", q=NEAR),
+                    )
+            elif near:
+                hw = w // 2 * PACK
+                for hf in range(h0, h1):
+                    copy(
+                        out=grouped[:, hf * hw : (hf + 1) * hw].rearrange("p (h c q t) -> p h c t q", h=w // HD, q=NEAR, t=PACK),
+                        in_=planes[:, hf // 2, :, :]
+                        .rearrange("p t (h r c q) -> p t h r c q", r=2, c=RD // NEAR, q=NEAR)[:, :, :, hf % 2, :, :]
+                        .rearrange("p t h c q -> p h c t q"),
                     )
             else:
                 for gl in range(2):
@@ -174,7 +184,7 @@ def tile_selfattention_pa_kernel(
 
         def vector_interleave(i):
             n, gp = units[i]
-            interleave(nc.vector.tensor_copy, i, TILES[n][3][gp] + TILES[n][6][gp], halves_of(n) - TILES[n][4][gp])
+            interleave(nc.vector.tensor_copy, i, TILES[n][3][gp] + TILES[n][6][gp], halves_of(n) - TILES[n][4][gp], near=True)
 
         def quantise(i):
             n, gp = units[i]

@@ -31,7 +31,7 @@ KCOLS = 256
 
 TILES = [
     (0, 512, "q", (1, 1), (0, 0), (4, 4), (0, 0)),
-    (512, 512, "q", (1, 1), (0, 0), (3, 3), (0, 0)),
+    (512, 512, "q", (1, 1), (0, 0), (4, 4), (0, 0)),
     (1024, 512, "q", (1, 1), (0, 0), (1, 1), (1, 1)),
     (1536, 512, "q", (1, 1), (0, 0), (1, 1), (1, 1)),
     (2048, 512, "q", (1, 1), (0, 0), (1, 1), (1, 1)),
@@ -93,7 +93,7 @@ def tile_selfattention_pa_kernel(
             for q in range(2 * PACK):
                 gl, t = q // PACK, q % PACK
                 g = 2 * gp + gl
-                if q >= 2 * PACK - vw:
+                if t >= PACK - (vw + gl) // 2:
                     nc.vector.tensor_scalar(
                         out=planes[:, gl, t, :],
                         in0=w_tiles[(base, g)][:, t, c0 - base : c0 - base + w].bitcast(FP8),

@@ -32,12 +32,12 @@ KCOLS = 256
 TILES = [
     (0, 512, "q", (1, 1), (0, 0), (4, 4), (0, 0)),
     (512, 512, "q", (1, 1), (0, 0), (4, 4), (0, 0)),
-    (1024, 512, "q", (1, 1), (0, 0), (1, 1), (1, 1)),
-    (1536, 512, "q", (1, 1), (0, 0), (1, 1), (1, 1)),
-    (2048, 512, "q", (1, 1), (0, 0), (1, 1), (1, 1)),
-    (2560, 512, "q", (1, 1), (0, 0), (1, 1), (1, 1)),
-    (3072, 512, "q", (1, 1), (0, 0), (1, 1), (1, 1)),
-    (3584, 512, "q", (1, 1), (0, 0), (1, 1), (1, 1)),
+    (1024, 512, "q", (1, 1), (0, 0), (1, 2), (1, 1)),
+    (1536, 512, "q", (1, 1), (0, 0), (1, 2), (1, 1)),
+    (2048, 512, "q", (1, 1), (0, 0), (1, 2), (1, 1)),
+    (2560, 512, "q", (1, 1), (0, 0), (1, 2), (1, 1)),
+    (3072, 512, "q", (1, 1), (0, 0), (1, 2), (1, 1)),
+    (3584, 512, "q", (1, 1), (0, 0), (1, 2), (1, 1)),
     (4096, 256, "k", (0, 0), (1, 1), (0, 0), (0, 0)),
     (4352, 256, "v", (0, 0), (1, 0), (0, 0), (0, 0)),
 ]

@@ -25,7 +25,7 @@ NT = 512
 RD = 64
 HJ = RD // 2
 HD = 128
-NEAR = 4
+NEAR = 8
 QCOLS = 4096
 KCOLS = 256
 
@@ -496,8 +496,6 @@ def tile_selfattention_pa_kernel(
             for (n, half) in jobs_of(s - 3, "q"):
                 rope_out(n, half)
                 store(n, half)
-            if 0 <= s - 1 < n_units:
-                gpsimd_interleave(s - 1)
             for (n, half) in jobs_of(s - 1, "q"):
                 bias_plain(n, half)
                 products(n, half)
@@ -527,6 +525,7 @@ def tile_selfattention_pa_kernel(
             if s == 2:
                 table_transposes()
                 rope_bias_transposes()
+            gpsimd_interleave(s)
             if 0 <= s - 2 < n_units:
                 quantise(s - 2)
             for (n, half) in jobs_of(s, "q"):

@@ -39,11 +39,11 @@ TILES = [
     (3072, 512, "q", (1, 1), (0, 0), (1, 2), (1, 1)),
     (3584, 512, "q", (1, 1), (0, 0), (1, 2), (1, 1)),
     (4096, 256, "k", (0, 0), (1, 1), (0, 0), (0, 0)),
-    (4352, 256, "v", (0, 0), (1, 0), (0, 0), (0, 0)),
+    (4352, 256, "v", (0, 0), (0, 0), (0, 0), (0, 0)),
 ]
 LOAD_COLS = 512
 LOADS_AHEAD = 12
-HEAD = [("l", 0), ("l", 1), ("l", 2), ("l", 3), ("c", 0), ("r", 0), ("x", 0), ("x", 1), ("l", 4), ("l", 5), ("x", 2), ("x", 3), ("l", 6), ("l", 7), ("b", 0), ("l", 8), ("l", 9), ("l", 10), ("l", 11)]
+HEAD = [("l", 0), ("l", 1), ("l", 2), ("l", 3), ("x", 0), ("x", 1), ("c", 0), ("r", 0), ("l", 4), ("l", 5), ("x", 2), ("x", 3), ("l", 6), ("l", 7), ("b", 0), ("l", 8), ("l", 9), ("l", 10), ("l", 11)]
 
 
 def tile_selfattention_pa_kernel(

@@ -38,8 +38,8 @@ TILES = [
     (2560, 512, "q", (1, 1), (0, 0), (1, 2), (1, 1)),
     (3072, 512, "q", (1, 1), (0, 0), (1, 2), (1, 1)),
     (3584, 512, "q", (1, 1), (0, 0), (1, 2), (1, 1)),
-    (4096, 256, "k", (0, 0), (1, 1), (0, 0), (0, 0)),
-    (4352, 256, "v", (0, 0), (0, 0), (0, 0), (0, 0)),
+    (4096, 256, "k", (0, 0), (1, 1), (0, 0), (1, 1)),
+    (4352, 256, "v", (0, 0), (0, 0), (0, 0), (1, 1)),
 ]
 LOAD_COLS = 512
 LOADS_AHEAD = 12
@@ -319,12 +319,12 @@ def tile_selfattention_pa_kernel(
 
         def k_products(n, half):
             nh = TILES[n][1] // HD
-            m12 = tmp.tile([P, 2, nh, 2, RD], F32, name="m12")
+            m12 = tmp.tile([P, 2, 2, nh, RD], F32, name="m12")
             xr = xbs[(n, half)][:].rearrange("p t (h d) -> p t h d", d=HD)[:, :, :, 0:RD]
             nc.vector.tensor_tensor(
                 out=m12[:],
-                in0=xr.unsqueeze(3).to_broadcast([P, 2, nh, 2, RD]),
-                in1=cs_tab[:, 2 * half : 2 * half + 2, :, :].unsqueeze(2).to_broadcast([P, 2, nh, 2, RD]),
+                in0=xr.unsqueeze(1).to_broadcast([P, 2, 2, nh, RD]),
+                in1=tab_src[:, 2 * half : 2 * half + 2, :, :, :].rearrange("p t f h d -> p f t h d"),
                 op=MULT,
             )
             prods[(n, half)] = m12
@@ -334,8 +334,8 @@ def tile_selfattention_pa_kernel(
             xr = xbs[(n, half)][:].rearrange("p t (h d) -> p t h d", d=HD)[:, :, :, 0:RD]
             nc.vector.tensor_tensor(
                 out=xr.rearrange("p t h (j e) -> p t h j e", e=2),
-                in0=m12[:, :, :, 0, :].rearrange("p t h (j e) -> p t h j e", e=2),
-                in1=m12[:, :, :, 1, :].rearrange("p t h (j e) -> p t h j e", e=2)[:, :, :, :, ::-1],
+                in0=m12[:, 0, :, :, :].rearrange("p t h (j e) -> p t h j e", e=2),
+                in1=m12[:, 1, :, :, :].rearrange("p t h (j e) -> p t h j e", e=2)[:, :, :, :, ::-1],
                 op=ADD,
             )
 
@@ -452,18 +452,6 @@ def tile_selfattention_pa_kernel(
                 nc.tensor.transpose(pt[:, b, :], b_cols[:, b, :, :].rearrange("p h d -> p (h d)"), ident_b[:])
             nc.scalar.copy(out=bias_r[:].rearrange("p n b -> p b n"), in_=pt[:, :, 0:n_rope])
 
-        cs_tab = const.tile([P, TT, 2, RD], F32, name="cs_tab")
-
-        def k_tables():
-            nc.vector.tensor_copy(
-                out=cs_tab[:, :, 0, :].rearrange("p t (j e) -> p t j e", e=2),
-                in_=cos_sb[:].rearrange("p t (e j) -> p t j e", e=2),
-            )
-            sv = cs_tab[:, :, 1, :].rearrange("p t (j e) -> p t j e", e=2)
-            sn = sin_sb[:].rearrange("p t (e j) -> p t j e", e=2)
-            nc.vector.tensor_scalar(out=sv[:, :, :, 1:2], in0=sn[:, :, :, 0:1], scalar1=-1.0, scalar2=None, op0=MULT)
-            nc.vector.tensor_copy(out=sv[:, :, :, 0:1], in_=sn[:, :, :, 1:2])
-
         def table_transposes():
             pt = accp.tile([P, 2, T], BF16, name="acc")
             for f in range(2):
@@ -521,7 +509,6 @@ def tile_selfattention_pa_kernel(
             if s == 3:
                 for g in range(G):
                     hidden_quantise(g)
-                k_tables()
             if s == 2:
                 table_transposes()
                 rope_bias_transposes()
@@ -549,6 +536,7 @@ def tile_selfattention_pa_kernel(
         widen(u)
         scalar_interleave(u - 1)
         vector_interleave(u - 1)
+        gpsimd_interleave(u)
         quantise(u - 2)
         mx_rope(q7, 1)
         mx_plain(q7, 1)

@@ -115,10 +115,16 @@ def tile_selfattention_pa_kernel(
             planes, grouped = st[i][0], st[i][1]
             if TILES[n][2] != "q":
                 for gl in range(h0, h1):
-                    copy(
-                        out=grouped[:, gl * w * PACK : (gl + 1) * w * PACK].rearrange("p (c q t) -> p c t q", q=NEAR, t=PACK),
-                        in_=planes[:, gl, :, :].rearrange("p t (c q) -> p c t q", q=NEAR),
-                    )
+                    if near:
+                        copy(
+                            out=grouped[:, gl * w * PACK : (gl + 1) * w * PACK].rearrange("p (c q t) -> p c t q", q=NEAR, t=PACK),
+                            in_=planes[:, gl, :, :].rearrange("p t (c q) -> p c t q", q=NEAR),
+                        )
+                    else:
+                        copy(
+                            out=grouped[:, gl * w * PACK : (gl + 1) * w * PACK].rearrange("p (c t) -> p c t", t=PACK),
+                            in_=planes[:, gl, :, :].rearrange("p t c -> p c t"),
+                        )
             elif near:
                 hw = w // 2 * PACK
                 for hf in range(h0, h1):
@@ -171,7 +177,7 @@ def tile_selfattention_pa_kernel(
                     out=grouped[:, 0 : 2 * NT].bitcast(F32),
                     in_=bank[:].rearrange("p k c -> p (k c)").bitcast(F32),
                 )
-            interleave(nc.scalar.copy, i, halves_of(n) - TILES[n][4][gp], halves_of(n))
+            interleave(nc.scalar.copy, i, halves_of(n) - TILES[n][4][gp], halves_of(n), near=(TILES[n][2] != "q"))
 
         def gpsimd_copy(out, in_):
             one = trg.tile([P, 1], F32, name="one")

@@ -43,6 +43,7 @@ TILES = [
 ]
 LOAD_COLS = 512
 LOADS_AHEAD = 12
+WARM_START = 6
 HEAD = [("l", 0), ("l", 1), ("l", 2), ("l", 3), ("x", 0), ("x", 1), ("c", 0), ("r", 0), ("l", 4), ("l", 5), ("x", 2), ("x", 3), ("l", 6), ("l", 7), ("b", 0), ("l", 8), ("l", 9), ("l", 10), ("l", 11)]
 
 
@@ -394,6 +395,15 @@ def tile_selfattention_pa_kernel(
         make_identity(nc, ident_f[:])
         ident_b = const.tile([P, P], BF16, name="ident_b")
         make_identity(nc, ident_b[:])
+        warm_src = const.tile([P, NT], BF16, name="warm_src")
+        nc.gpsimd.memset(warm_src[:], 0.0)
+
+        def pe_warm(k):
+            idle = accp.tile([P, NT], F32, name="acc")
+            for r in range(k):
+                nc.tensor.matmul(out=idle[:], lhsT=ident_b[:], rhs=warm_src[:], start=True, stop=True)
+
+        pe_warm(WARM_START)
         swap_f = const.tile([P, P], F32, name="swap_f")
         for e in range(2):
             nc.vector.tensor_copy(
@@ -425,6 +435,7 @@ def tile_selfattention_pa_kernel(
                     out=xgs[g][:, 2 * th : 2 * th + 2, :, :].bitcast(F32),
                     in_=pt[:].rearrange("p (t u r) -> p t r u", t=2, u=2),
                 )
+                pe_warm(1)
 
         def hidden_quantise(g):
             nc.vector.quantize_mx(
@@ -532,6 +543,8 @@ def tile_selfattention_pa_kernel(
                 mx_plain(n, half)
             if s < n_units:
                 pe_interleave(s)
+            if s < 4:
+                pe_warm(2)
 
         q6, q7, kt, vt = 6, 7, 8, 9
         u = n_units - 1

@@ -39,7 +39,7 @@ TILES = [
     (3072, 512, "q", (1, 1), (0, 0), (1, 2), (1, 1)),
     (3584, 512, "q", (1, 1), (0, 0), (1, 2), (1, 1)),
     (4096, 256, "k", (0, 0), (1, 1), (0, 0), (1, 1)),
-    (4352, 256, "v", (0, 0), (0, 0), (0, 0), (1, 1)),
+    (4352, 256, "v", (0, 0), (0, 0), (2, 6), (1, 1)),
 ]
 LOAD_COLS = 512
 LOADS_AHEAD = 12

@@ -39,7 +39,7 @@ TILES = [
     (3072, 512, "q", (1, 1), (0, 0), (1, 2), (1, 1)),
     (3584, 512, "q", (1, 1), (0, 0), (1, 2), (1, 1)),
     (4096, 256, "k", (0, 0), (1, 1), (0, 0), (1, 1)),
-    (4352, 256, "v", (0, 0), (0, 0), (2, 6), (1, 1)),
+    (4352, 256, "v", (0, 0), (1, 0), (2, 6), (1, 1)),
 ]
 LOAD_COLS = 512
 LOADS_AHEAD = 12

@@ -489,6 +489,14 @@ def tile_selfattention_pa_kernel(
             else:
                 jobs[done] = jobs.get(done, []) + [(n, 0), (n, 1)]
 
+        last_q = max([n for n in range(len(TILES)) if TILES[n][2] == "q"])
+        mx_jobs = {}
+        for step in sorted(jobs):
+            for (n, half) in jobs[step]:
+                if TILES[n][2] == "q":
+                    at = step - 1 if n == last_q else step
+                    mx_jobs[at] = mx_jobs.get(at, []) + [(n, half)]
+
         def jobs_of(s, kinds):
             return [j for j in jobs.get(s, []) if TILES[j[0]][2] in kinds]
 
@@ -532,7 +540,7 @@ def tile_selfattention_pa_kernel(
             gpsimd_interleave(s)
             if 0 <= s - 2 < n_units:
                 quantise(s - 2)
-            for (n, half) in jobs_of(s, "q"):
+            for (n, half) in mx_jobs.get(s, []):
                 mx_rope(n, half)
                 mx_plain(n, half)
             for (n, half) in jobs_of(s - 2, "q"):
@@ -557,15 +565,13 @@ def tile_selfattention_pa_kernel(
         vector_interleave(u - 1)
         gpsimd_interleave(u)
         quantise(u - 2)
-        mx_rope(q7, 1)
-        mx_plain(q7, 1)
         rope_transposes(q7, 0)
         mx_plain(kt, 0)
-        mx_plain(kt, 1)
         rope_out(q6, 1)
         store(q6, 1)
         bias_plain(q7, 1)
         products(q7, 1)
+        mx_plain(kt, 1)
         vector_interleave(u)
         quantise(u - 1)
         rope_transposes(q7, 1)

@@ -593,5 +593,6 @@ def tile_selfattention_pa_kernel(
             store(kt, half)
         for tt in range(TT):
             bias_tile(vt, tt)
-            if tt % 2 == 1:
-                store(vt, tt // 2)
+            nc.sync.dma_start(
+                out=out_2.rearrange("(t p) h d -> p t (h d)", p=P)[:, tt, :], in_=xbs[(vt, tt // 2)][:, tt % 2, :]
+            )

@@ -571,10 +571,10 @@ def tile_selfattention_pa_kernel(
         store(q6, 1)
         bias_plain(q7, 1)
         products(q7, 1)
+        rope_transposes(q7, 1)
         mx_plain(kt, 1)
         vector_interleave(u)
         quantise(u - 1)
-        rope_transposes(q7, 1)
         for tt in range(TT):
             mx_open(vt, tt, (ilp if tt < 2 else accp), ("bank" if tt < 2 else "acc"))
         quantise(u)
@@ -590,7 +590,10 @@ def tile_selfattention_pa_kernel(
         store(q7, 1)
         for half in range(2):
             k_sum(kt, half)
-            store(kt, half)
+            for k in range(2):
+                nc.sync.dma_start(
+                    out=out_1.rearrange("(t p) h d -> p t (h d)", p=P)[:, 2 * half + k, :], in_=xbs[(kt, half)][:, k, :]
+                )
         for tt in range(TT):
             bias_tile(vt, tt)
             nc.sync.dma_start(

@@ -230,6 +230,21 @@ def tile_selfattention_pa_kernel(
                     )
             rope_acc[(n, half)] = acc
 
+        def mx_rope_slice(n, b):
+            wcod, wsc = codes[n]
+            acc = accp.tile([P, T], F32, name="acc")
+            for g in range(G):
+                nc.tensor.matmul_mx(
+                    out=acc[:],
+                    lhsT=wcod[:, g, b * P : (b + 1) * P].bitcast(FP8X4),
+                    lhsT_scale=wsc[:, g, b * P : (b + 1) * P],
+                    rhs=xc[:, g, :].bitcast(FP8X4),
+                    rhs_scale=xs[:, g, :],
+                    start=(g == 0),
+                    stop=(g == G - 1),
+                )
+            rope_acc[(n, b)] = acc
+
         def mx_plain(n, half):
             wcod, wsc = codes[n]
             p0 = rope_cols(n)
@@ -287,6 +302,36 @@ def tile_selfattention_pa_kernel(
                     op1=MULT,
                 )
             prods[(n, half)] = m
+
+        def products_slice(n, b):
+            m = mp.tile([P, 2, T], F32, name="m")
+            nc.vector.scalar_tensor_tensor(
+                out=m[:],
+                in0=rope_acc[(n, b)][:].unsqueeze(1).to_broadcast([P, 2, T]),
+                scalar=bias_r[:, n, b : b + 1],
+                in1=tabs[:],
+                op0=ADD,
+                op1=MULT,
+            )
+            prods[(n, b)] = m
+
+        def rope_transposes_tile(n):
+            ys = []
+            for half in range(2):
+                y = accp.tile([P, 2, 2, P], F32, name="acc")
+                ys.append(y)
+                ybanks[(n, half)] = y
+            for b in range(2):
+                for tt in range(TT):
+                    for f in range(2):
+                        nc.tensor.matmul(
+                            out=ys[tt // 2][:, tt % 2, b, :],
+                            lhsT=prods[(n, b)][:, f, tt * P : (tt + 1) * P],
+                            rhs=(ident_f[:] if f == 0 else swap_f[:]),
+                            is_transpose=True,
+                            start=(f == 0),
+                            stop=(f == 1),
+                        )
 
         def rope_transposes(n, half):
             y = accp.tile([P, 2, 2, P], F32, name="acc")
@@ -511,7 +556,7 @@ def tile_selfattention_pa_kernel(
                 store(n, half)
             for (n, half) in jobs_of(s - 1, "q"):
                 bias_plain(n, half)
-                products(n, half)
+                products_slice(n, half)
             for (n, half) in jobs_of(s - 1, "kv"):
                 bias_plain(n, half)
             for (n, half) in jobs_of(s - 1, "v"):
@@ -541,12 +586,14 @@ def tile_selfattention_pa_kernel(
             if 0 <= s - 2 < n_units:
                 quantise(s - 2)
             for (n, half) in mx_jobs.get(s, []):
-                mx_rope(n, half)
+                if n == last_q:
+                    mx_rope(n, half)
+                else:
+                    mx_rope_slice(n, half)
                 mx_plain(n, half)
             for (n, half) in jobs_of(s - 2, "q"):
                 if half == 0:
-                    rope_transposes(n, 0)
-                    rope_transposes(n, 1)
+                    rope_transposes_tile(n)
             for (n, half) in jobs_of(s, "kv"):
                 mx_plain(n, half)
             if s < n_units:

@@ -44,6 +44,7 @@ TILES = [
 LOAD_COLS = 512
 LOADS_AHEAD = 12
 WARM_START = 6
+SIGNAL = (0, PACK - 1)
 HEAD = [("l", 0), ("l", 1), ("l", 2), ("l", 3), ("x", 0), ("x", 1), ("c", 0), ("r", 0), ("l", 4), ("l", 5), ("x", 2), ("x", 3), ("l", 6), ("l", 7), ("b", 0), ("l", 8), ("l", 9), ("l", 10), ("l", 11)]
 
 
@@ -83,6 +84,23 @@ def tile_selfattention_pa_kernel(
             )
             w_tiles[(c0, g)] = w_bytes
 
+        def has_signal_plane(i):
+            n, gp = units[i]
+            return TILES[n][5][gp] > 0 and TILES[n][6][gp] > 0
+
+        def vector_widen(i, gl, t):
+            n, gp = units[i]
+            c0, w = TILES[n][0], TILES[n][1]
+            base = (c0 // LOAD_COLS) * LOAD_COLS
+            g = 2 * gp + gl
+            nc.vector.tensor_scalar(
+                out=st[i][0][:, gl, t, :],
+                in0=w_tiles[(base, g)][:, t, c0 - base : c0 - base + w].bitcast(FP8),
+                scalar1=wscale[:, g, t : t + 1],
+                scalar2=None,
+                op0=MULT,
+            )
+
         def widen(i):
             n, gp = units[i]
             c0, w = TILES[n][0], TILES[n][1]
@@ -94,14 +112,9 @@ def tile_selfattention_pa_kernel(
             for q in range(2 * PACK):
                 gl, t = q // PACK, q % PACK
                 g = 2 * gp + gl
-                if t >= PACK - (vw + gl) // 2:
-                    nc.vector.tensor_scalar(
-                        out=planes[:, gl, t, :],
-                        in0=w_tiles[(base, g)][:, t, c0 - base : c0 - base + w].bitcast(FP8),
-                        scalar1=wscale[:, g, t : t + 1],
-                        scalar2=None,
-                        op0=MULT,
-                    )
+                if t >= PACK - (vw + 1 - gl) // 2:
+                    if not (has_signal_plane(i) and (gl, t) == SIGNAL):
+                        vector_widen(i, gl, t)
                 else:
                     nc.scalar.activation(
                         out=planes[:, gl, t, :],
@@ -185,9 +198,16 @@ def tile_selfattention_pa_kernel(
             nc.vector.memset(one[:], 1.0)
             nc.gpsimd.tensor_scalar(out=out, in0=in_, scalar1=one[:, 0:1], scalar2=0.0, op0=MULT, op1=ADD)
 
+        def gpsimd_copy_plain(out, in_):
+            nc.gpsimd.tensor_scalar(out=out, in0=in_, scalar1=1.0, scalar2=0.0, op0=MULT, op1=ADD)
+
         def gpsimd_interleave(i):
             n, gp = units[i]
-            interleave(gpsimd_copy, i, TILES[n][3][gp], TILES[n][3][gp] + TILES[n][6][gp])
+            if has_signal_plane(i):
+                vector_widen(i, SIGNAL[0], SIGNAL[1])
+                interleave(gpsimd_copy_plain, i, TILES[n][3][gp], TILES[n][3][gp] + TILES[n][6][gp])
+            else:
+                interleave(gpsimd_copy, i, TILES[n][3][gp], TILES[n][3][gp] + TILES[n][6][gp])
 
         def vector_interleave(i):
             n, gp = units[i]

@@ -33,10 +33,10 @@ TILES = [
     (0, 512, "q", (1, 1), (0, 0), (4, 4), (0, 0)),
     (512, 512, "q", (1, 1), (0, 0), (4, 4), (0, 0)),
     (1024, 512, "q", (1, 1), (0, 0), (1, 2), (1, 1)),
-    (1536, 512, "q", (1, 1), (0, 0), (1, 2), (1, 1)),
+    (1536, 512, "q", (1, 1), (0, 0), (2, 2), (1, 1)),
     (2048, 512, "q", (1, 1), (0, 0), (1, 2), (1, 1)),
     (2560, 512, "q", (1, 1), (0, 0), (1, 2), (1, 1)),
-    (3072, 512, "q", (1, 1), (0, 0), (1, 2), (1, 1)),
+    (3072, 512, "q", (1, 1), (0, 0), (2, 2), (1, 1)),
     (3584, 512, "q", (1, 1), (0, 0), (1, 2), (1, 1)),
     (4096, 256, "k", (0, 0), (1, 1), (0, 0), (1, 1)),
     (4352, 256, "v", (0, 0), (1, 0), (2, 6), (1, 1)),

@@ -38,7 +38,7 @@ TILES = [
     (2560, 512, "q", (1, 1), (0, 0), (1, 2), (1, 1)),
     (3072, 512, "q", (1, 1), (0, 0), (2, 2), (1, 1)),
     (3584, 512, "q", (1, 1), (0, 0), (1, 2), (1, 1)),
-    (4096, 256, "k", (0, 0), (1, 1), (0, 0), (1, 1)),
+    (4096, 256, "k", (0, 0), (2, 2), (0, 0), (2, 2)),
     (4352, 256, "v", (0, 0), (1, 0), (2, 6), (1, 1)),
 ]
 LOAD_COLS = 512
@@ -123,11 +123,14 @@ def tile_selfattention_pa_kernel(
                         scale=wscale[:, g, t : t + 1],
                     )
 
+        def split(n):
+            return TILES[n][2] in ("q", "k")
+
         def interleave(copy, i, h0, h1, near=False):
             n = units[i][0]
             w = TILES[n][1]
             planes, grouped = st[i][0], st[i][1]
-            if TILES[n][2] != "q":
+            if not split(n):
                 for gl in range(h0, h1):
                     if near:
                         copy(
@@ -163,7 +166,7 @@ def tile_selfattention_pa_kernel(
                         )
 
         def rope_cols(n):
-            return TILES[n][1] // 2 if TILES[n][2] == "q" else 0
+            return TILES[n][1] // 2 if split(n) else 0
 
         def pe_interleave(i):
             n, gp = units[i]
@@ -181,7 +184,7 @@ def tile_selfattention_pa_kernel(
                 st[i][2].append(bank)
 
         def halves_of(n):
-            return 4 if TILES[n][2] == "q" else 2
+            return 4 if split(n) else 2
 
         def scalar_interleave(i):
             n, gp = units[i]
@@ -207,7 +210,8 @@ def tile_selfattention_pa_kernel(
                 vector_widen(i, SIGNAL[0], SIGNAL[1])
                 interleave(gpsimd_copy_plain, i, TILES[n][3][gp], TILES[n][3][gp] + TILES[n][6][gp])
             else:
-                interleave(gpsimd_copy, i, TILES[n][3][gp], TILES[n][3][gp] + TILES[n][6][gp])
+                for hf in range(TILES[n][3][gp], TILES[n][3][gp] + TILES[n][6][gp]):
+                    interleave((gpsimd_copy if hf == TILES[n][3][gp] else gpsimd_copy_plain), i, hf, hf + 1)
 
         def vector_interleave(i):
             n, gp = units[i]
@@ -353,6 +357,58 @@ def tile_selfattention_pa_kernel(
                             stop=(f == 1),
                         )
 
+        def k_plain(n):
+            wcod, wsc = codes[n]
+            p0 = rope_cols(n)
+            pw = TILES[n][1] - p0
+            acc = accp.tile([P, TT, pw], F32, name="acc")
+            for tt in range(TT):
+                for g in range(G):
+                    nc.tensor.matmul_mx(
+                        out=acc[:, tt, :],
+                        lhsT=xc[:, g, tt * P : (tt + 1) * P].bitcast(FP8X4),
+                        lhsT_scale=xs[:, g, tt * P : (tt + 1) * P],
+                        rhs=wcod[:, g, p0 : p0 + pw].bitcast(FP8X4),
+                        rhs_scale=wsc[:, g, p0 : p0 + pw],
+                        start=(g == 0),
+                        stop=(g == G - 1),
+                    )
+            plain_acc[n] = acc
+
+        def k_bias(n):
+            col, w = TILES[n][0], TILES[n][1]
+            xb = obp.tile([P, TT, w], F32, name="xb")
+            nc.vector.tensor_tensor(
+                out=xb[:].rearrange("p t (h d) -> p t h d", d=HD)[:, :, :, RD:HD],
+                in0=plain_acc[n][:].rearrange("p t (h d) -> p t h d", d=RD),
+                in1=bias_sb[:, col : col + w]
+                .rearrange("p (h d) -> p h d", d=HD)[:, :, RD:HD]
+                .unsqueeze(1)
+                .to_broadcast([P, TT, w // HD, RD]),
+                op=ADD,
+            )
+            xbs[n] = xb
+
+        def k_transposes(n):
+            y = accp.tile([P, TT, P], F32, name="acc")
+            for tt in range(TT):
+                for f in range(2):
+                    nc.tensor.matmul(
+                        out=y[:, tt, :],
+                        lhsT=prods[(n, 0)][:, f, tt * P : (tt + 1) * P],
+                        rhs=(ident_f[:] if f == 0 else swap_f[:]),
+                        is_transpose=True,
+                        start=(f == 0),
+                        stop=(f == 1),
+                    )
+            ybanks[n] = y
+
+        def k_rope_out(n):
+            nc.scalar.copy(
+                out=xbs[n][:].rearrange("p t (h d) -> p t h d", d=HD)[:, :, :, 0:RD],
+                in_=ybanks[n][:].rearrange("p t (h d) -> p t h d", d=RD),
+            )
+
         def rope_transposes(n, half):
             y = accp.tile([P, 2, 2, P], F32, name="acc")
             for tl in range(2):
@@ -372,7 +428,7 @@ def tile_selfattention_pa_kernel(
             col, w, kind = TILES[n][0], TILES[n][1], TILES[n][2]
             xb = obp.tile([P, 2, w], F32, name="xb")
             acc = plain_acc[(n, half)]
-            if kind != "q":
+            if not split(n):
                 nc.vector.tensor_tensor(
                     out=xb[:], in0=acc[:], in1=bias_sb[:, col : col + w].unsqueeze(1).to_broadcast([P, 2, w]), op=ADD
                 )
@@ -434,7 +490,7 @@ def tile_selfattention_pa_kernel(
         cos_sb = const.tile([P, TT, RD], BF16, name="cos_sb")
         sin_sb = const.tile([P, TT, RD], BF16, name="sin_sb")
         bias_sb = const.tile([P, OUT], BF16, name="bias_sb")
-        n_rope = QCOLS // NT
+        n_rope = OUT // NT
         b_rows = const.tile([P, NT], BF16, name="b_rows")
         nc.gpsimd.memset(b_rows[:], 0.0)
         for item in HEAD:
@@ -447,7 +503,7 @@ def tile_selfattention_pa_kernel(
                 nc.sync.dma_start(out=cos_sb[:], in_=cos.rearrange("(t p) d -> p t d", p=P))
                 nc.sync.dma_start(out=sin_sb[:], in_=sin.rearrange("(t p) d -> p t d", p=P))
             elif item[0] == "r":
-                nc.sync.dma_start(out=b_rows[0:n_rope, :], in_=b_qkv[0:QCOLS].rearrange("(n c) -> n c", c=NT))
+                nc.sync.dma_start(out=b_rows[0:n_rope, :], in_=b_qkv.rearrange("(n c) -> n c", c=NT))
             else:
                 nc.sync.dma_start(out=bias_sb[:], in_=b_qkv.partition_broadcast(P))
         next_load = LOADS_AHEAD
@@ -633,34 +689,30 @@ def tile_selfattention_pa_kernel(
         gpsimd_interleave(u)
         quantise(u - 2)
         rope_transposes(q7, 0)
-        mx_plain(kt, 0)
+        mx_rope_slice(kt, 0)
         rope_out(q6, 1)
         store(q6, 1)
         bias_plain(q7, 1)
         products(q7, 1)
         rope_transposes(q7, 1)
-        mx_plain(kt, 1)
+        k_plain(kt)
+        products_slice(kt, 0)
         vector_interleave(u)
         quantise(u - 1)
+        k_transposes(kt)
+        rope_out(q7, 0)
+        store(q7, 0)
         for tt in range(TT):
             mx_open(vt, tt, (ilp if tt < 2 else accp), ("bank" if tt < 2 else "acc"))
         quantise(u)
         for tt in range(TT):
             mx_passes(vt, tt, G // 2, G)
-        for half in range(2):
-            bias_plain(kt, half)
-        rope_out(q7, 0)
-        store(q7, 0)
-        for half in range(2):
-            k_products(kt, half)
+        k_bias(kt)
         rope_out(q7, 1)
         store(q7, 1)
-        for half in range(2):
-            k_sum(kt, half)
-            for k in range(2):
-                nc.sync.dma_start(
-                    out=out_1.rearrange("(t p) h d -> p t (h d)", p=P)[:, 2 * half + k, :], in_=xbs[(kt, half)][:, k, :]
-                )
+        k_rope_out(kt)
+        for tt in range(TT):
+            nc.sync.dma_start(out=out_1.rearrange("(t p) h d -> p t (h d)", p=P)[:, tt, :], in_=xbs[kt][:, tt, :])
         for tt in range(TT):
             bias_tile(vt, tt)
             nc.sync.dma_start(

@@ -78,10 +78,12 @@ def tile_selfattention_pa_kernel(
         def load(j):
             c0, g = loads[j]
             w_bytes = wbp.tile([P, PACK, LOAD_COLS], U8, name="w_bytes")
-            nc.sync.dma_start(
-                out=w_bytes[:],
-                in_=W_qkv_bytes[g * KP : (g + 1) * KP, c0 : c0 + LOAD_COLS].rearrange("(p t) n -> p t n", t=PACK),
-            )
+            rows = W_qkv_bytes[g * KP : (g + 1) * KP, c0 : c0 + LOAD_COLS].rearrange("(p t) n -> p t n", t=PACK)
+            if j == 0:
+                for t in (0, 2, 1, 3):
+                    nc.sync.dma_start(out=w_bytes[:, t, :], in_=rows[:, t, :])
+            else:
+                nc.sync.dma_start(out=w_bytes[:], in_=rows)
             w_tiles[(c0, g)] = w_bytes
 
         def has_signal_plane(i):

@@ -58,7 +58,7 @@ def tile_selfattention_pa_kernel(
         plp = ctx.enter_context(tc.tile_pool(name="plp", bufs=4))
         grp = ctx.enter_context(tc.tile_pool(name="grp", bufs=4))
         cdp = ctx.enter_context(tc.tile_pool(name="cdp", bufs=3))
-        hid = ctx.enter_context(tc.tile_pool(name="hid", bufs=4))
+        hid = ctx.enter_context(tc.tile_pool(name="hid", bufs=2))
         obp = ctx.enter_context(tc.tile_pool(name="obp", bufs=6))
         mp = ctx.enter_context(tc.tile_pool(name="mp", bufs=4))
         trg = ctx.enter_context(tc.tile_pool(name="trg", bufs=4))
@@ -249,8 +249,8 @@ def tile_selfattention_pa_kernel(
                         out=acc[:, b, :],
                         lhsT=wcod[:, g, b * P : (b + 1) * P].bitcast(FP8X4),
                         lhsT_scale=wsc[:, g, b * P : (b + 1) * P],
-                        rhs=xc[:, g, half * HT : (half + 1) * HT].bitcast(FP8X4),
-                        rhs_scale=xs[:, g, half * HT : (half + 1) * HT],
+                        rhs=xc[half][:, g, :].bitcast(FP8X4),
+                        rhs_scale=xs[half][:, g, :],
                         start=(g == 0),
                         stop=(g == G - 1),
                     )
@@ -259,16 +259,17 @@ def tile_selfattention_pa_kernel(
         def mx_rope_slice(n, b):
             wcod, wsc = codes[n]
             acc = accp.tile([P, T], F32, name="acc")
-            for g in range(G):
-                nc.tensor.matmul_mx(
-                    out=acc[:],
-                    lhsT=wcod[:, g, b * P : (b + 1) * P].bitcast(FP8X4),
-                    lhsT_scale=wsc[:, g, b * P : (b + 1) * P],
-                    rhs=xc[:, g, :].bitcast(FP8X4),
-                    rhs_scale=xs[:, g, :],
-                    start=(g == 0),
-                    stop=(g == G - 1),
-                )
+            for th in range(2):
+                for g in range(G):
+                    nc.tensor.matmul_mx(
+                        out=acc[:, th * HT : (th + 1) * HT],
+                        lhsT=wcod[:, g, b * P : (b + 1) * P].bitcast(FP8X4),
+                        lhsT_scale=wsc[:, g, b * P : (b + 1) * P],
+                        rhs=xc[th][:, g, :].bitcast(FP8X4),
+                        rhs_scale=xs[th][:, g, :],
+                        start=(g == 0),
+                        stop=(g == G - 1),
+                    )
             rope_acc[(n, b)] = acc
 
         def mx_plain(n, half):
@@ -281,8 +282,8 @@ def tile_selfattention_pa_kernel(
                 for g in range(G):
                     nc.tensor.matmul_mx(
                         out=acc[:, k, :],
-                        lhsT=xc[:, g, tt * P : (tt + 1) * P].bitcast(FP8X4),
-                        lhsT_scale=xs[:, g, tt * P : (tt + 1) * P],
+                        lhsT=xc[half][:, g, k * P : (k + 1) * P].bitcast(FP8X4),
+                        lhsT_scale=xs[half][:, g, k * P : (k + 1) * P],
                         rhs=wcod[:, g, p0 : p0 + pw].bitcast(FP8X4),
                         rhs_scale=wsc[:, g, p0 : p0 + pw],
                         start=(g == 0),
@@ -300,8 +301,8 @@ def tile_selfattention_pa_kernel(
             for g in range(g0, g1):
                 nc.tensor.matmul_mx(
                     out=plain_acc[(n, tt)][:],
-                    lhsT=xc[:, g, tt * P : (tt + 1) * P].bitcast(FP8X4),
-                    lhsT_scale=xs[:, g, tt * P : (tt + 1) * P],
+                    lhsT=xc[tt // 2][:, g, (tt % 2) * P : (tt % 2 + 1) * P].bitcast(FP8X4),
+                    lhsT_scale=xs[tt // 2][:, g, (tt % 2) * P : (tt % 2 + 1) * P],
                     rhs=wcod[:, g, :].bitcast(FP8X4),
                     rhs_scale=wsc[:, g, :],
                     start=(g == 0),
@@ -368,8 +369,8 @@ def tile_selfattention_pa_kernel(
                 for g in range(G):
                     nc.tensor.matmul_mx(
                         out=acc[:, tt, :],
-                        lhsT=xc[:, g, tt * P : (tt + 1) * P].bitcast(FP8X4),
-                        lhsT_scale=xs[:, g, tt * P : (tt + 1) * P],
+                        lhsT=xc[tt // 2][:, g, (tt % 2) * P : (tt % 2 + 1) * P].bitcast(FP8X4),
+                        lhsT_scale=xs[tt // 2][:, g, (tt % 2) * P : (tt % 2 + 1) * P],
                         rhs=wcod[:, g, p0 : p0 + pw].bitcast(FP8X4),
                         rhs_scale=wsc[:, g, p0 : p0 + pw],
                         start=(g == 0),
@@ -535,36 +536,38 @@ def tile_selfattention_pa_kernel(
             )
 
 
-        xc = const.tile([P, G, T], U32, name="xc", align_bytes=64)
-        xs = const.tile([P, G, T], U8, name="xs", align_bytes=64)
+        xc = [const.tile([P, G, HT], U32, name="xc%d" % th, align_bytes=64) for th in range(2)]
+        xs = [const.tile([P, G, HT], U8, name="xs%d" % th, align_bytes=64) for th in range(2)]
         tab_src = const.tile([P, TT, 2, 2, RD], BF16, name="tab_src")
         tabs = const.tile([P, 2, T], BF16, name="tabs")
         xgs = {}
 
-        def hidden_half(th):
-            for g in range(G):
-                if th == 0:
-                    xg = hid.tile([P, TT, P, PACK], BF16, name="xg", align_bytes=64)
-                    xgs[g] = xg
+        def hidden_tile(tt):
+            th, tl = tt // 2, tt % 2
+            if tl == 0:
+                xg = hid.tile([P, G, 2, P, PACK], BF16, name="xg", align_bytes=64)
+                xgs[th] = xg
+            words = x_sb[:, tt, :].bitcast(F32)
+            for gp in range(2):
                 pt = accp.tile([P, NT], F32, name="acc")
-                for tl in range(2):
-                    words = x_sb[:, 2 * th + tl, :].bitcast(F32)
+                for gl in range(2):
+                    g = 2 * gp + gl
                     for u in range(2):
-                        q = 2 * tl + u
+                        q = 2 * gl + u
                         nc.tensor.transpose(
                             pt[:, q * P : (q + 1) * P], words[:, 256 * g + u : 256 * (g + 1) : 2], ident_f[:]
                         )
                 nc.scalar.copy(
-                    out=xgs[g][:, 2 * th : 2 * th + 2, :, :].bitcast(F32),
-                    in_=pt[:].rearrange("p (t u r) -> p t r u", t=2, u=2),
+                    out=xgs[th][:, 2 * gp : 2 * gp + 2, tl, :, :].bitcast(F32),
+                    in_=pt[:].rearrange("p (g u r) -> p g r u", g=2, u=2),
                 )
                 pe_warm(1)
 
-        def hidden_quantise(g):
+        def hidden_quantise(th):
             nc.vector.quantize_mx(
-                out=xc[:, g, :].bitcast(FP8X4),
-                scales=xs[:, g, :],
-                in_=xgs[g][:].rearrange("p t r j -> p (t r j)"),
+                out=xc[th][:].rearrange("p g c -> p (g c)").bitcast(FP8X4),
+                scales=xs[th][:].rearrange("p g c -> p (g c)"),
+                in_=xgs[th][:].rearrange("p g t r j -> p (g t r j)"),
             )
 
         def table_sources():
@@ -653,10 +656,10 @@ def tile_selfattention_pa_kernel(
                 table_sources()
                 rope_bias_sources()
             if s in (1, 2):
-                hidden_half(s - 1)
-            if s == 3:
-                for g in range(G):
-                    hidden_quantise(g)
+                hidden_tile(2 * s - 2)
+                hidden_tile(2 * s - 1)
+            if s in (2, 3):
+                hidden_quantise(s - 2)
             if s == 2:
                 table_transposes()
                 rope_bias_transposes()

@@ -30,8 +30,8 @@ QCOLS = 4096
 KCOLS = 256
 
 TILES = [
-    (0, 512, "q", (1, 1), (0, 0), (4, 4), (0, 0)),
-    (512, 512, "q", (1, 1), (0, 0), (4, 4), (0, 0)),
+    (0, 512, "q", (2, 2), (0, 0), (5, 6), (0, 0)),
+    (512, 512, "q", (2, 2), (0, 0), (5, 6), (0, 0)),
     (1024, 512, "q", (1, 1), (0, 0), (1, 2), (1, 1)),
     (1536, 512, "q", (1, 1), (0, 0), (2, 2), (1, 1)),
     (2048, 512, "q", (1, 1), (0, 0), (1, 2), (1, 1)),
@@ -172,14 +172,17 @@ def tile_selfattention_pa_kernel(
 
         def pe_interleave(i):
             n, gp = units[i]
-            if TILES[n][3][gp] > 0:
+            for hf in range(TILES[n][3][gp]):
                 src = st[i][0][:, 0, :, :].rearrange("p t (b h r d) -> p t b h r d", b=2, r=2, d=RD)
-                bank = ilp.tile([P, 2, NT], BF16, name="bank")
+                if hf == 0:
+                    bank = ilp.tile([P, 2, NT], BF16, name="bank")
+                else:
+                    bank = accp.tile([P, 2, NT], BF16, name="acc")
                 for b in range(2):
                     nc.tensor.matmul(
                         out=bank[:, b, :].rearrange("p (h d t) -> p h d t", d=RD, t=PACK),
                         lhsT=ident_b[:],
-                        rhs=src[:, :, b, :, 0, :].rearrange("p t h d -> p h d t"),
+                        rhs=src[:, :, b, :, hf, :].rearrange("p t h d -> p h d t"),
                         start=True,
                         stop=True,
                     )
@@ -191,9 +194,9 @@ def tile_selfattention_pa_kernel(
         def scalar_interleave(i):
             n, gp = units[i]
             grouped = st[i][1]
-            for bank in st[i][2]:
+            for k, bank in enumerate(st[i][2]):
                 nc.scalar.copy(
-                    out=grouped[:, 0 : 2 * NT].bitcast(F32),
+                    out=grouped[:, 2 * k * NT : 2 * (k + 1) * NT].bitcast(F32),
                     in_=bank[:].rearrange("p k c -> p (k c)").bitcast(F32),
                 )
             interleave(nc.scalar.copy, i, halves_of(n) - TILES[n][4][gp], halves_of(n), near=(TILES[n][2] != "q"))
@@ -679,8 +682,6 @@ def tile_selfattention_pa_kernel(
                 mx_plain(n, half)
             if s < n_units:
                 pe_interleave(s)
-            if s < 4:
-                pe_warm(2)
 
         q6, q7, kt, vt = 6, 7, 8, 9
         u = n_units - 1

@@ -65,7 +65,11 @@ def tile_selfattention_pa_kernel(
         tmp = ctx.enter_context(tc.tile_pool(name="tmp", bufs=2))
         accp = ctx.enter_context(tc.psum_pool(name="accp", bufs=6))
         ilp = ctx.enter_context(tc.psum_pool(name="ilp", bufs=2))
-        ctx.enter_context(tc.manual_schedule())
+        ctx.enter_context(
+            tc.manual_schedule(
+                engines={mybir.EngineType.Pool, mybir.EngineType.Activation, mybir.EngineType.PE, mybir.EngineType.DVE}
+            )
+        )
 
         units = [(n, gp) for n in range(len(TILES)) for gp in range(2)]
         n_units = len(units)

@@ -67,7 +67,7 @@ def tile_selfattention_pa_kernel(
         ilp = ctx.enter_context(tc.psum_pool(name="ilp", bufs=2))
         ctx.enter_context(
             tc.manual_schedule(
-                engines={mybir.EngineType.Pool, mybir.EngineType.Activation, mybir.EngineType.PE, mybir.EngineType.DVE}
+                engines={mybir.EngineType.Pool, mybir.EngineType.Activation, mybir.EngineType.DVE}
             )
         )
 

from contextlib import ExitStack

import concourse.mybir as mybir
from concourse.masks import make_identity

T, H, OUT = 512, 2048, 4608
FLOPS = 2 * T * H * OUT

F32 = mybir.dt.float32
BF16 = mybir.dt.bfloat16
U32 = mybir.dt.uint32
U8 = mybir.dt.uint8
FP8 = mybir.dt.float8_e4m3fn
FP8X4 = mybir.dt.float8_e4m3fn_x4
ADD = mybir.AluOpType.add
MULT = mybir.AluOpType.mult
COPY = mybir.ActivationFunctionType.Copy

P = 128
PACK = 4
KP = P * PACK
G = H // KP
TT = T // P
NT = 512
RD = 64
HJ = RD // 2
HD = 128
NEAR = 8
QCOLS = 4096
KCOLS = 256

TILES = [
    (0, 512, "q", (2, 2), (0, 0), (5, 6), (0, 0)),
    (512, 512, "q", (2, 2), (0, 0), (5, 6), (0, 0)),
    (1024, 512, "q", (1, 1), (0, 0), (1, 2), (1, 1)),
    (1536, 512, "q", (1, 1), (0, 0), (2, 2), (1, 1)),
    (2048, 512, "q", (1, 1), (0, 0), (1, 2), (1, 1)),
    (2560, 512, "q", (1, 1), (0, 0), (1, 2), (1, 1)),
    (3072, 512, "q", (1, 1), (0, 0), (2, 2), (1, 1)),
    (3584, 512, "q", (1, 1), (0, 0), (1, 2), (1, 1)),
    (4096, 256, "k", (0, 0), (2, 2), (0, 0), (2, 2)),
    (4352, 256, "v", (0, 0), (1, 0), (2, 6), (1, 1)),
]
LOAD_COLS = 512
LOADS_AHEAD = 12
WARM_START = 6
SIGNAL = (0, PACK - 1)
HEAD = [("l", 0), ("l", 1), ("l", 2), ("l", 3), ("x", 0), ("x", 1), ("c", 0), ("r", 0), ("l", 4), ("l", 5), ("x", 2), ("x", 3), ("l", 6), ("l", 7), ("b", 0), ("l", 8), ("l", 9), ("l", 10), ("l", 11)]


def tile_selfattention_pa_kernel(
    tc, hidden_states, cos, sin, W_qkv_bytes, W_qkv_scale, b_qkv, out_0, out_1, out_2
):
    nc = tc.nc
    with ExitStack() as ctx:
        const = ctx.enter_context(tc.tile_pool(name="const", bufs=1))
        wbp = ctx.enter_context(tc.tile_pool(name="wbp", bufs=14))
        plp = ctx.enter_context(tc.tile_pool(name="plp", bufs=4))
        grp = ctx.enter_context(tc.tile_pool(name="grp", bufs=4))
        cdp = ctx.enter_context(tc.tile_pool(name="cdp", bufs=3))
        hid = ctx.enter_context(tc.tile_pool(name="hid", bufs=2))
        obp = ctx.enter_context(tc.tile_pool(name="obp", bufs=6))
        mp = ctx.enter_context(tc.tile_pool(name="mp", bufs=4))
        trg = ctx.enter_context(tc.tile_pool(name="trg", bufs=4))
        tmp = ctx.enter_context(tc.tile_pool(name="tmp", bufs=2))
        accp = ctx.enter_context(tc.psum_pool(name="accp", bufs=6))
        ilp = ctx.enter_context(tc.psum_pool(name="ilp", bufs=2))
        ctx.enter_context(
            tc.manual_schedule(
                engines={mybir.EngineType.Pool, mybir.EngineType.Activation, mybir.EngineType.DVE}
            )
        )

        units = [(n, gp) for n in range(len(TILES)) for gp in range(2)]
        n_units = len(units)
        w_tiles = {}
        st = {}
        codes = {}

        loads = [(c0, g) for c0 in range(0, OUT, LOAD_COLS) for g in range(G)]

        def load(j):
            c0, g = loads[j]
            w_bytes = wbp.tile([P, PACK, LOAD_COLS], U8, name="w_bytes")
            rows = W_qkv_bytes[g * KP : (g + 1) * KP, c0 : c0 + LOAD_COLS].rearrange("(p t) n -> p t n", t=PACK)
            if j == 0:
                for t in (0, 2, 1, 3):
                    nc.sync.dma_start(out=w_bytes[:, t, :], in_=rows[:, t, :])
            else:
                nc.sync.dma_start(out=w_bytes[:], in_=rows)
            w_tiles[(c0, g)] = w_bytes

        def has_signal_plane(i):
            n, gp = units[i]
            return TILES[n][5][gp] > 0 and TILES[n][6][gp] > 0

        def vector_widen(i, gl, t):
            n, gp = units[i]
            c0, w = TILES[n][0], TILES[n][1]
            base = (c0 // LOAD_COLS) * LOAD_COLS
            g = 2 * gp + gl
            nc.vector.tensor_scalar(
                out=st[i][0][:, gl, t, :],
                in0=w_tiles[(base, g)][:, t, c0 - base : c0 - base + w].bitcast(FP8),
                scalar1=wscale[:, g, t : t + 1],
                scalar2=None,
                op0=MULT,
            )

        def widen(i):
            n, gp = units[i]
            c0, w = TILES[n][0], TILES[n][1]
            planes = plp.tile([P, 2, PACK, w], BF16, name="planes")
            grouped = grp.tile([P, 2 * w * PACK], BF16, name="grouped", align_bytes=64)
            st[i] = [planes, grouped, []]
            base = (c0 // LOAD_COLS) * LOAD_COLS
            vw = TILES[n][5][gp]
            for q in range(2 * PACK):
                gl, t = q // PACK, q % PACK
                g = 2 * gp + gl
                if t >= PACK - (vw + 1 - gl) // 2:
                    if not (has_signal_plane(i) and (gl, t) == SIGNAL):
                        vector_widen(i, gl, t)
                else:
                    nc.scalar.activation(
                        out=planes[:, gl, t, :],
                        in_=w_tiles[(base, g)][:, t, c0 - base : c0 - base + w].bitcast(FP8),
                        func=COPY,
                        scale=wscale[:, g, t : t + 1],
                    )

        def split(n):
            return TILES[n][2] in ("q", "k")

        def interleave(copy, i, h0, h1, near=False):
            n = units[i][0]
            w = TILES[n][1]
            planes, grouped = st[i][0], st[i][1]
            if not split(n):
                for gl in range(h0, h1):
                    if near:
                        copy(
                            out=grouped[:, gl * w * PACK : (gl + 1) * w * PACK].rearrange("p (c q t) -> p c t q", q=NEAR, t=PACK),
                            in_=planes[:, gl, :, :].rearrange("p t (c q) -> p c t q", q=NEAR),
                        )
                    else:
                        copy(
                            out=grouped[:, gl * w * PACK : (gl + 1) * w * PACK].rearrange("p (c t) -> p c t", t=PACK),
                            in_=planes[:, gl, :, :].rearrange("p t c -> p c t"),
                        )
            elif near:
                hw = w // 2 * PACK
                for hf in range(h0, h1):
                    copy(
                        out=grouped[:, hf * hw : (hf + 1) * hw].rearrange("p (h c q t) -> p h c t q", h=w // HD, q=NEAR, t=PACK),
                        in_=planes[:, hf // 2, :, :]
                        .rearrange("p t (h r c q) -> p t h r c q", r=2, c=RD // NEAR, q=NEAR)[:, :, :, hf % 2, :, :]
                        .rearrange("p t h c q -> p h c t q"),
                    )
            else:
                for gl in range(2):
                    r0, r1 = max(h0 - 2 * gl, 0), min(h1 - 2 * gl, 2)
                    if r0 < r1:
                        hw = w // 2 * PACK
                        copy(
                            out=grouped[:, (2 * gl + r0) * hw : (2 * gl + r1) * hw].rearrange(
                                "p (r h d t) -> p r h d t", r=r1 - r0, d=RD, t=PACK
                            ),
                            in_=planes[:, gl, :, :]
                            .rearrange("p t (h r d) -> p t h r d", r=2, d=RD)[:, :, :, r0:r1, :]
                            .rearrange("p t h r d -> p r h d t"),
                        )

        def rope_cols(n):
            return TILES[n][1] // 2 if split(n) else 0

        def pe_interleave(i):
            n, gp = units[i]
            for hf in range(TILES[n][3][gp]):
                src = st[i][0][:, 0, :, :].rearrange("p t (b h r d) -> p t b h r d", b=2, r=2, d=RD)
                if hf == 0:
                    bank = ilp.tile([P, 2, NT], BF16, name="bank")
                else:
                    bank = accp.tile([P, 2, NT], BF16, name="acc")
                for b in range(2):
                    nc.tensor.matmul(
                        out=bank[:, b, :].rearrange("p (h d t) -> p h d t", d=RD, t=PACK),
                        lhsT=ident_b[:],
                        rhs=src[:, :, b, :, hf, :].rearrange("p t h d -> p h d t"),
                        start=True,
                        stop=True,
                    )
                st[i][2].append(bank)

        def halves_of(n):
            return 4 if split(n) else 2

        def scalar_interleave(i):
            n, gp = units[i]
            grouped = st[i][1]
            for k, bank in enumerate(st[i][2]):
                nc.scalar.copy(
                    out=grouped[:, 2 * k * NT : 2 * (k + 1) * NT].bitcast(F32),
                    in_=bank[:].rearrange("p k c -> p (k c)").bitcast(F32),
                )
            interleave(nc.scalar.copy, i, halves_of(n) - TILES[n][4][gp], halves_of(n), near=(TILES[n][2] != "q"))

        def gpsimd_copy(out, in_):
            one = trg.tile([P, 1], F32, name="one")
            nc.vector.memset(one[:], 1.0)
            nc.gpsimd.tensor_scalar(out=out, in0=in_, scalar1=one[:, 0:1], scalar2=0.0, op0=MULT, op1=ADD)

        def gpsimd_copy_plain(out, in_):
            nc.gpsimd.tensor_scalar(out=out, in0=in_, scalar1=1.0, scalar2=0.0, op0=MULT, op1=ADD)

        def gpsimd_interleave(i):
            n, gp = units[i]
            if has_signal_plane(i):
                vector_widen(i, SIGNAL[0], SIGNAL[1])
                interleave(gpsimd_copy_plain, i, TILES[n][3][gp], TILES[n][3][gp] + TILES[n][6][gp])
            else:
                for hf in range(TILES[n][3][gp], TILES[n][3][gp] + TILES[n][6][gp]):
                    interleave((gpsimd_copy if hf == TILES[n][3][gp] else gpsimd_copy_plain), i, hf, hf + 1)

        def vector_interleave(i):
            n, gp = units[i]
            interleave(nc.vector.tensor_copy, i, TILES[n][3][gp] + TILES[n][6][gp], halves_of(n) - TILES[n][4][gp], near=True)

        def quantise(i):
            n, gp = units[i]
            w = TILES[n][1]
            if gp == 0:
                wcod = cdp.tile([P, G, w], U32, name="wcod", align_bytes=64)
                wsc = cdp.tile([P, G, w], U8, name="wsc", align_bytes=64)
                codes[n] = (wcod, wsc)
            wcod, wsc = codes[n]
            nc.vector.quantize_mx(
                out=wcod[:, 2 * gp : 2 * gp + 2, :].rearrange("p g c -> p (g c)").bitcast(FP8X4),
                scales=wsc[:, 2 * gp : 2 * gp + 2, :].rearrange("p g c -> p (g c)"),
                in_=st[i][1][:],
            )

        rope_acc = {}
        plain_acc = {}
        prods = {}
        ybanks = {}
        xbs = {}
        HT = T // 2

        def mx_rope(n, half):
            wcod, wsc = codes[n]
            acc = accp.tile([P, 2, HT], F32, name="acc")
            for b in range(2):
                for g in range(G):
                    nc.tensor.matmul_mx(
                        out=acc[:, b, :],
                        lhsT=wcod[:, g, b * P : (b + 1) * P].bitcast(FP8X4),
                        lhsT_scale=wsc[:, g, b * P : (b + 1) * P],
                        rhs=xc[half][:, g, :].bitcast(FP8X4),
                        rhs_scale=xs[half][:, g, :],
                        start=(g == 0),
                        stop=(g == G - 1),
                    )
            rope_acc[(n, half)] = acc

        def mx_rope_slice(n, b):
            wcod, wsc = codes[n]
            acc = accp.tile([P, T], F32, name="acc")
            for th in range(2):
                for g in range(G):
                    nc.tensor.matmul_mx(
                        out=acc[:, th * HT : (th + 1) * HT],
                        lhsT=wcod[:, g, b * P : (b + 1) * P].bitcast(FP8X4),
                        lhsT_scale=wsc[:, g, b * P : (b + 1) * P],
                        rhs=xc[th][:, g, :].bitcast(FP8X4),
                        rhs_scale=xs[th][:, g, :],
                        start=(g == 0),
                        stop=(g == G - 1),
                    )
            rope_acc[(n, b)] = acc

        def mx_plain(n, half):
            wcod, wsc = codes[n]
            p0 = rope_cols(n)
            pw = TILES[n][1] - p0
            acc = accp.tile([P, 2, pw], F32, name="acc")
            for k in range(2):
                tt = 2 * half + k
                for g in range(G):
                    nc.tensor.matmul_mx(
                        out=acc[:, k, :],
                        lhsT=xc[half][:, g, k * P : (k + 1) * P].bitcast(FP8X4),
                        lhsT_scale=xs[half][:, g, k * P : (k + 1) * P],
                        rhs=wcod[:, g, p0 : p0 + pw].bitcast(FP8X4),
                        rhs_scale=wsc[:, g, p0 : p0 + pw],
                        start=(g == 0),
                        stop=(g == G - 1),
                    )
            plain_acc[(n, half)] = acc

        def mx_open(n, tt, pool, tag):
            acc = pool.tile([P, TILES[n][1]], F32, name=tag)
            plain_acc[(n, tt)] = acc
            mx_passes(n, tt, 0, G // 2)

        def mx_passes(n, tt, g0, g1):
            wcod, wsc = codes[n]
            for g in range(g0, g1):
                nc.tensor.matmul_mx(
                    out=plain_acc[(n, tt)][:],
                    lhsT=xc[tt // 2][:, g, (tt % 2) * P : (tt % 2 + 1) * P].bitcast(FP8X4),
                    lhsT_scale=xs[tt // 2][:, g, (tt % 2) * P : (tt % 2 + 1) * P],
                    rhs=wcod[:, g, :].bitcast(FP8X4),
                    rhs_scale=wsc[:, g, :],
                    start=(g == 0),
                    stop=(g == G - 1),
                )

        def bias_tile(n, tt):
            col, w = TILES[n][0], TILES[n][1]
            if tt % 2 == 0:
                xbs[(n, tt // 2)] = obp.tile([P, 2, w], F32, name="xb")
            nc.vector.tensor_tensor(
                out=xbs[(n, tt // 2)][:, tt % 2, :], in0=plain_acc[(n, tt)][:], in1=bias_sb[:, col : col + w], op=ADD
            )

        def products(n, half):
            m = mp.tile([P, 2, 2, HT], F32, name="m")
            for b in range(2):
                nc.vector.scalar_tensor_tensor(
                    out=m[:, b, :, :],
                    in0=rope_acc[(n, half)][:, b, :].unsqueeze(1).to_broadcast([P, 2, HT]),
                    scalar=bias_r[:, n, b : b + 1],
                    in1=tabs[:, :, half * HT : (half + 1) * HT],
                    op0=ADD,
                    op1=MULT,
                )
            prods[(n, half)] = m

        def products_slice(n, b):
            m = mp.tile([P, 2, T], F32, name="m")
            nc.vector.scalar_tensor_tensor(
                out=m[:],
                in0=rope_acc[(n, b)][:].unsqueeze(1).to_broadcast([P, 2, T]),
                scalar=bias_r[:, n, b : b + 1],
                in1=tabs[:],
                op0=ADD,
                op1=MULT,
            )
            prods[(n, b)] = m

        def rope_transposes_tile(n):
            ys = []
            for half in range(2):
                y = accp.tile([P, 2, 2, P], F32, name="acc")
                ys.append(y)
                ybanks[(n, half)] = y
            for b in range(2):
                for tt in range(TT):
                    for f in range(2):
                        nc.tensor.matmul(
                            out=ys[tt // 2][:, tt % 2, b, :],
                            lhsT=prods[(n, b)][:, f, tt * P : (tt + 1) * P],
                            rhs=(ident_f[:] if f == 0 else swap_f[:]),
                            is_transpose=True,
                            start=(f == 0),
                            stop=(f == 1),
                        )

        def k_plain(n):
            wcod, wsc = codes[n]
            p0 = rope_cols(n)
            pw = TILES[n][1] - p0
            acc = accp.tile([P, TT, pw], F32, name="acc")
            for tt in range(TT):
                for g in range(G):
                    nc.tensor.matmul_mx(
                        out=acc[:, tt, :],
                        lhsT=xc[tt // 2][:, g, (tt % 2) * P : (tt % 2 + 1) * P].bitcast(FP8X4),
                        lhsT_scale=xs[tt // 2][:, g, (tt % 2) * P : (tt % 2 + 1) * P],
                        rhs=wcod[:, g, p0 : p0 + pw].bitcast(FP8X4),
                        rhs_scale=wsc[:, g, p0 : p0 + pw],
                        start=(g == 0),
                        stop=(g == G - 1),
                    )
            plain_acc[n] = acc

        def k_bias(n):
            col, w = TILES[n][0], TILES[n][1]
            xb = obp.tile([P, TT, w], F32, name="xb")
            nc.vector.tensor_tensor(
                out=xb[:].rearrange("p t (h d) -> p t h d", d=HD)[:, :, :, RD:HD],
                in0=plain_acc[n][:].rearrange("p t (h d) -> p t h d", d=RD),
                in1=bias_sb[:, col : col + w]
                .rearrange("p (h d) -> p h d", d=HD)[:, :, RD:HD]
                .unsqueeze(1)
                .to_broadcast([P, TT, w // HD, RD]),
                op=ADD,
            )
            xbs[n] = xb

        def k_transposes(n):
            y = accp.tile([P, TT, P], F32, name="acc")
            for tt in range(TT):
                for f in range(2):
                    nc.tensor.matmul(
                        out=y[:, tt, :],
                        lhsT=prods[(n, 0)][:, f, tt * P : (tt + 1) * P],
                        rhs=(ident_f[:] if f == 0 else swap_f[:]),
                        is_transpose=True,
                        start=(f == 0),
                        stop=(f == 1),
                    )
            ybanks[n] = y

        def k_rope_out(n):
            nc.scalar.copy(
                out=xbs[n][:].rearrange("p t (h d) -> p t h d", d=HD)[:, :, :, 0:RD],
                in_=ybanks[n][:].rearrange("p t (h d) -> p t h d", d=RD),
            )

        def rope_transposes(n, half):
            y = accp.tile([P, 2, 2, P], F32, name="acc")
            for tl in range(2):
                for b in range(2):
                    for f in range(2):
                        nc.tensor.matmul(
                            out=y[:, tl, b, :],
                            lhsT=prods[(n, half)][:, b, f, tl * P : (tl + 1) * P],
                            rhs=(ident_f[:] if f == 0 else swap_f[:]),
                            is_transpose=True,
                            start=(f == 0),
                            stop=(f == 1),
                        )
            ybanks[(n, half)] = y

        def bias_plain(n, half):
            col, w, kind = TILES[n][0], TILES[n][1], TILES[n][2]
            xb = obp.tile([P, 2, w], F32, name="xb")
            acc = plain_acc[(n, half)]
            if not split(n):
                nc.vector.tensor_tensor(
                    out=xb[:], in0=acc[:], in1=bias_sb[:, col : col + w].unsqueeze(1).to_broadcast([P, 2, w]), op=ADD
                )
            else:
                nh = w // HD
                nc.vector.tensor_tensor(
                    out=xb[:].rearrange("p t (h d) -> p t h d", d=HD)[:, :, :, RD:HD],
                    in0=acc[:].rearrange("p t (h d) -> p t h d", d=RD),
                    in1=bias_sb[:, col : col + w]
                    .rearrange("p (h d) -> p h d", d=HD)[:, :, RD:HD]
                    .unsqueeze(1)
                    .to_broadcast([P, 2, nh, RD]),
                    op=ADD,
                )
            xbs[(n, half)] = xb

        def k_products(n, half):
            nh = TILES[n][1] // HD
            m12 = tmp.tile([P, 2, 2, nh, RD], F32, name="m12")
            xr = xbs[(n, half)][:].rearrange("p t (h d) -> p t h d", d=HD)[:, :, :, 0:RD]
            nc.vector.tensor_tensor(
                out=m12[:],
                in0=xr.unsqueeze(1).to_broadcast([P, 2, 2, nh, RD]),
                in1=tab_src[:, 2 * half : 2 * half + 2, :, :, :].rearrange("p t f h d -> p f t h d"),
                op=MULT,
            )
            prods[(n, half)] = m12

        def k_sum(n, half):
            m12 = prods[(n, half)]
            xr = xbs[(n, half)][:].rearrange("p t (h d) -> p t h d", d=HD)[:, :, :, 0:RD]
            nc.vector.tensor_tensor(
                out=xr.rearrange("p t h (j e) -> p t h j e", e=2),
                in0=m12[:, 0, :, :, :].rearrange("p t h (j e) -> p t h j e", e=2),
                in1=m12[:, 1, :, :, :].rearrange("p t h (j e) -> p t h j e", e=2)[:, :, :, :, ::-1],
                op=ADD,
            )

        def rope_out(n, half):
            nc.scalar.copy(
                out=xbs[(n, half)][:].rearrange("p t (h d) -> p t h d", d=HD)[:, :, :, 0:RD],
                in_=ybanks[(n, half)][:].rearrange("p t b (h d) -> p t (b h) d", d=RD),
            )

        def store(n, half):
            col, w = TILES[n][0], TILES[n][1]
            t0 = 2 * half
            if col < QCOLS:
                dst = out_0.rearrange("(t p) h d -> p t (h d)", p=P)[:, t0 : t0 + 2, col : col + w]
            elif col < QCOLS + KCOLS:
                dst = out_1.rearrange("(t p) h d -> p t (h d)", p=P)[:, t0 : t0 + 2, :]
            else:
                dst = out_2.rearrange("(t p) h d -> p t (h d)", p=P)[:, t0 : t0 + 2, :]
            nc.sync.dma_start(out=dst, in_=xbs[(n, half)][:])

        wscale = const.tile([P, G, PACK], F32, name="wscale")
        nc.sync.dma_start(out=wscale[:], in_=W_qkv_scale.rearrange("(g p t) o -> p g (t o)", p=P, t=PACK))
        x_sb = const.tile([P, TT, H], BF16, name="x_sb")
        cos_sb = const.tile([P, TT, RD], BF16, name="cos_sb")
        sin_sb = const.tile([P, TT, RD], BF16, name="sin_sb")
        bias_sb = const.tile([P, OUT], BF16, name="bias_sb")
        n_rope = OUT // NT
        b_rows = const.tile([P, NT], BF16, name="b_rows")
        nc.gpsimd.memset(b_rows[:], 0.0)
        for item in HEAD:
            if item[0] == "l":
                load(item[1])
            elif item[0] == "x":
                tt = item[1]
                nc.sync.dma_start(out=x_sb[:, tt, :], in_=hidden_states[tt * P : (tt + 1) * P, :])
            elif item[0] == "c":
                nc.sync.dma_start(out=cos_sb[:], in_=cos.rearrange("(t p) d -> p t d", p=P))
                nc.sync.dma_start(out=sin_sb[:], in_=sin.rearrange("(t p) d -> p t d", p=P))
            elif item[0] == "r":
                nc.sync.dma_start(out=b_rows[0:n_rope, :], in_=b_qkv.rearrange("(n c) -> n c", c=NT))
            else:
                nc.sync.dma_start(out=bias_sb[:], in_=b_qkv.partition_broadcast(P))
        next_load = LOADS_AHEAD

        warm = const.tile([P, 2], F32, name="warm")
        nc.vector.memset(warm[:, 0:1], 0.0)
        nc.scalar.activation(out=warm[:, 1:2], in_=warm[:, 0:1], func=COPY)

        ident_f = const.tile([P, P], F32, name="ident_f")
        make_identity(nc, ident_f[:])
        ident_b = const.tile([P, P], BF16, name="ident_b")
        make_identity(nc, ident_b[:])
        warm_src = const.tile([P, NT], BF16, name="warm_src")
        nc.gpsimd.memset(warm_src[:], 0.0)

        def pe_warm(k):
            idle = accp.tile([P, NT], F32, name="acc")
            for r in range(k):
                nc.tensor.matmul(out=idle[:], lhsT=ident_b[:], rhs=warm_src[:], start=True, stop=True)

        pe_warm(WARM_START)
        swap_f = const.tile([P, P], F32, name="swap_f")
        for e in range(2):
            nc.vector.tensor_copy(
                out=swap_f[:].rearrange("p (j e) -> p j e", e=2)[:, :, e : e + 1],
                in_=ident_f[:].rearrange("p (j e) -> p j e", e=2)[:, :, 1 - e : 2 - e],
            )


        xc = [const.tile([P, G, HT], U32, name="xc%d" % th, align_bytes=64) for th in range(2)]
        xs = [const.tile([P, G, HT], U8, name="xs%d" % th, align_bytes=64) for th in range(2)]
        tab_src = const.tile([P, TT, 2, 2, RD], BF16, name="tab_src")
        tabs = const.tile([P, 2, T], BF16, name="tabs")
        xgs = {}

        def hidden_tile(tt):
            th, tl = tt // 2, tt % 2
            if tl == 0:
                xg = hid.tile([P, G, 2, P, PACK], BF16, name="xg", align_bytes=64)
                xgs[th] = xg
            words = x_sb[:, tt, :].bitcast(F32)
            for gp in range(2):
                pt = accp.tile([P, NT], F32, name="acc")
                for gl in range(2):
                    g = 2 * gp + gl
                    for u in range(2):
                        q = 2 * gl + u
                        nc.tensor.transpose(
                            pt[:, q * P : (q + 1) * P], words[:, 256 * g + u : 256 * (g + 1) : 2], ident_f[:]
                        )
                nc.scalar.copy(
                    out=xgs[th][:, 2 * gp : 2 * gp + 2, tl, :, :].bitcast(F32),
                    in_=pt[:].rearrange("p (g u r) -> p g r u", g=2, u=2),
                )
                pe_warm(1)

        def hidden_quantise(th):
            nc.vector.quantize_mx(
                out=xc[th][:].rearrange("p g c -> p (g c)").bitcast(FP8X4),
                scales=xs[th][:].rearrange("p g c -> p (g c)"),
                in_=xgs[th][:].rearrange("p g t r j -> p (g t r j)"),
            )

        def table_sources():
            for f, e, src, lo in ((0, 0, cos_sb, 0), (0, 1, cos_sb, HJ), (1, 0, sin_sb, HJ), (1, 1, sin_sb, 0)):
                nc.vector.tensor_scalar(
                    out=tab_src[:, :, f, :, :].rearrange("p t h (j e) -> p t h j e", e=2)[:, :, :, :, e],
                    in0=src[:, :, lo : lo + HJ].unsqueeze(2).to_broadcast([P, TT, 2, HJ]),
                    scalar1=(-1.0 if (f, e) == (1, 1) else 1.0),
                    scalar2=None,
                    op0=MULT,
                )

        b_cols = const.tile([P, 2, 2, RD], BF16, name="b_cols")
        bias_r = const.tile([P, n_rope, 2], BF16, name="bias_r")

        def rope_bias_sources():
            nc.vector.tensor_copy(
                out=b_cols[:],
                in_=b_rows[:].rearrange("p (b h r d) -> p b h r d", b=2, h=2, r=2)[:, :, :, 0, :],
            )

        def rope_bias_transposes():
            pt = accp.tile([P, 2, P], BF16, name="acc")
            for b in range(2):
                nc.tensor.transpose(pt[:, b, :], b_cols[:, b, :, :].rearrange("p h d -> p (h d)"), ident_b[:])
            nc.scalar.copy(out=bias_r[:].rearrange("p n b -> p b n"), in_=pt[:, :, 0:n_rope])

        def table_transposes():
            pt = accp.tile([P, 2, T], BF16, name="acc")
            for f in range(2):
                for tt in range(TT):
                    nc.tensor.transpose(
                        pt[:, f, tt * P : (tt + 1) * P],
                        tab_src[:, tt, f, :, :].rearrange("p h d -> p (h d)"),
                        ident_b[:],
                    )
            nc.scalar.copy(out=tabs[:], in_=pt[:])

        jobs = {}
        for n in range(len(TILES)):
            done = 2 * n + 3
            if TILES[n][2] == "q":
                jobs[done + 1] = jobs.get(done + 1, []) + [(n, 0)]
                jobs[done + 2] = jobs.get(done + 2, []) + [(n, 1)]
            else:
                jobs[done] = jobs.get(done, []) + [(n, 0), (n, 1)]

        last_q = max([n for n in range(len(TILES)) if TILES[n][2] == "q"])
        mx_jobs = {}
        for step in sorted(jobs):
            for (n, half) in jobs[step]:
                if TILES[n][2] == "q":
                    at = step - 1 if n == last_q else step
                    mx_jobs[at] = mx_jobs.get(at, []) + [(n, half)]

        def jobs_of(s, kinds):
            return [j for j in jobs.get(s, []) if TILES[j[0]][2] in kinds]

        for s in range(n_units - 1):
            if s >= 1:
                for r in range(2):
                    if next_load < len(loads):
                        load(next_load)
                        next_load += 1
            for (n, half) in jobs_of(s - 3, "q"):
                rope_out(n, half)
                store(n, half)
            for (n, half) in jobs_of(s - 1, "q"):
                bias_plain(n, half)
                products_slice(n, half)
            for (n, half) in jobs_of(s - 1, "kv"):
                bias_plain(n, half)
            for (n, half) in jobs_of(s - 1, "v"):
                store(n, half)
            for (n, half) in jobs_of(s - 1, "k"):
                k_products(n, half)
            if s < n_units:
                widen(s)
            if 0 <= s - 1 < n_units:
                scalar_interleave(s - 1)
                vector_interleave(s - 1)
            for (n, half) in jobs_of(s - 1, "k"):
                k_sum(n, half)
                store(n, half)
            if s == 1:
                table_sources()
                rope_bias_sources()
            if s in (1, 2):
                hidden_tile(2 * s - 2)
                hidden_tile(2 * s - 1)
            if s in (2, 3):
                hidden_quantise(s - 2)
            if s == 2:
                table_transposes()
                rope_bias_transposes()
            gpsimd_interleave(s)
            if 0 <= s - 2 < n_units:
                quantise(s - 2)
            for (n, half) in mx_jobs.get(s, []):
                if n == last_q:
                    mx_rope(n, half)
                else:
                    mx_rope_slice(n, half)
                mx_plain(n, half)
            for (n, half) in jobs_of(s - 2, "q"):
                if half == 0:
                    rope_transposes_tile(n)
            for (n, half) in jobs_of(s, "kv"):
                mx_plain(n, half)
            if s < n_units:
                pe_interleave(s)

        q6, q7, kt, vt = 6, 7, 8, 9
        u = n_units - 1
        rope_out(q6, 0)
        store(q6, 0)
        bias_plain(q7, 0)
        products(q7, 0)
        widen(u)
        scalar_interleave(u - 1)
        vector_interleave(u - 1)
        gpsimd_interleave(u)
        quantise(u - 2)
        rope_transposes(q7, 0)
        mx_rope_slice(kt, 0)
        rope_out(q6, 1)
        store(q6, 1)
        bias_plain(q7, 1)
        products(q7, 1)
        rope_transposes(q7, 1)
        k_plain(kt)
        products_slice(kt, 0)
        vector_interleave(u)
        quantise(u - 1)
        k_transposes(kt)
        rope_out(q7, 0)
        store(q7, 0)
        for tt in range(TT):
            mx_open(vt, tt, (ilp if tt < 2 else accp), ("bank" if tt < 2 else "acc"))
        quantise(u)
        for tt in range(TT):
            mx_passes(vt, tt, G // 2, G)
        k_bias(kt)
        rope_out(q7, 1)
        store(q7, 1)
        k_rope_out(kt)
        for tt in range(TT):
            nc.sync.dma_start(out=out_1.rearrange("(t p) h d -> p t (h d)", p=P)[:, tt, :], in_=xbs[kt][:, tt, :])
        for tt in range(TT):
            bias_tile(vt, tt)
            nc.sync.dma_start(
                out=out_2.rearrange("(t p) h d -> p t (h d)", p=P)[:, tt, :], in_=xbs[(vt, tt // 2)][:, tt % 2, :]
            )
